import numpy as np
import ml_dtypes


def mxq(x, axis, fmt="e4m3"):
    dtype, down = {"e4m3": (ml_dtypes.float8_e4m3fn, 7), "e5m2": (ml_dtypes.float8_e5m2, 14)}[fmt]
    v = np.moveaxis(np.asarray(x, np.float32).astype(ml_dtypes.bfloat16).astype(np.float64), axis, -1)
    blocks = v.reshape(v.shape[:-1] + (-1, 32))
    amax = np.abs(blocks).max(-1, keepdims=True)
    byte = np.maximum(np.where(amax > 0, np.frexp(amax)[1] - 1 + 127, 0) - down, 1)
    scale = np.exp2(byte - 127.0)
    codes = (blocks / scale).astype(np.float32).astype(dtype).astype(np.float64)
    return np.moveaxis((codes * scale).reshape(v.shape), -1, axis)


WIDE = False


def mx_kscale(k):
    if not WIDE:
        return np.ones(k)
    levels = np.array([10, -10, 5, -5, 0])
    if k % 512:
        return np.exp2(np.random.permutation(np.resize(levels, k // 32))).repeat(32)
    a = np.empty((k // 512, 16))
    for p in range(k // 512):
        a[p, :8] = np.random.permutation(np.resize(levels, 8))
        for g in range(8):
            far = levels[np.abs(levels - a[p, g]) >= 10]
            a[p, g + 8] = far[np.random.randint(len(far))]
    return np.exp2(a.ravel()).repeat(32)


BF16 = ml_dtypes.bfloat16


def bf(x):
    return np.asarray(x, np.float32).astype(BF16)


def f64(x):
    return np.asarray(x).astype(np.float64)


E2M1 = np.array([0.0, 0.5, 1.0, 1.5, 2.0, 3.0, 4.0, 6.0, -0.0, -0.5, -1.0, -1.5, -2.0, -3.0, -4.0, -6.0])


def pack_weight(w, fmt):
    k, n = w.shape
    w = f64(bf(w)).reshape(k // 32, 32, n)
    amax = np.abs(w).max(1)
    if fmt == "e4m3":
        byte = np.frexp(amax)[1] - 1 + 127 - 7
    else:
        mant, ex = np.frexp(amax / 6.0)
        byte = np.where(mant > 0.5, ex, ex - 1) + 127
    byte = np.clip(np.where(amax > 0, byte, 1), 1, 254)
    scaled = (w * np.exp2(127.0 - byte)[:, None, :]).reshape(k, n).astype(np.float32)
    by_word = np.ascontiguousarray(scaled.reshape(k // 512, 128, 4, n).transpose(0, 1, 3, 2))
    if fmt == "e4m3":
        words = by_word.astype(ml_dtypes.float8_e4m3fn).view(np.uint8)
    else:
        c = by_word.astype(ml_dtypes.float4_e2m1fn).view(np.uint8) & 0xF
        words = c[..., 0::2] | (c[..., 1::2] << 4)
    return np.ascontiguousarray(words), np.ascontiguousarray(byte.astype(np.uint8).reshape(k // 512, 16, n))


def unpack_weight(words, scales, fmt):
    g, p, n, _ = words.shape
    if fmt == "e4m3":
        vals = np.ascontiguousarray(words).view(ml_dtypes.float8_e4m3fn).astype(np.float64)
    else:
        nib = np.empty((g, p, n, 4), np.uint8)
        nib[..., 0::2] = words & 0xF
        nib[..., 1::2] = words >> 4
        vals = E2M1[nib]
    vals = vals * np.repeat(np.exp2(scales.astype(np.float64) - 127.0), 8, axis=1)[..., None]
    return vals.transpose(0, 1, 3, 2).reshape(g * 512, n)


N, T, B, C, H = 256, 4, 8, 512, 128
N3 = T * N
O = H + H


def sigmoid(v):
    return 1.0 / (1.0 + np.exp(-v))


def draw0():
    s, t = mx_kscale(N3), mx_kscale(C)
    x = bf(np.random.standard_normal((N3, B, C)) * s[:, None, None] * t[None, None, :])
    A = bf(np.random.standard_normal((N3, N3)) / np.sqrt(N3) / s[None, :])
    W0 = np.random.standard_normal((O, C)) / np.sqrt(C) / t[None, :]
    words, scales = pack_weight(W0.T, "e4m3")
    return {"x": x,
            "A": A,
            "W0_words": words,
            "W0_scales": scales,
            "b0": bf(np.random.standard_normal(O) * 0.3)}


def core(x, A, W0_words, W0_scales, b0):
    h = f64(x).transpose(1, 2, 0)
    g = mxq(h, 2, "e4m3") @ mxq(f64(A), 1, "e4m3").T
    y = (unpack_weight(W0_words, W0_scales, "e4m3").T @ mxq(g, 1, "e4m3")) + f64(b0)[None, :, None]
    h1 = y[:, :H] * sigmoid(y[:, H:])
    return h1.transpose(2, 0, 1)


def e4m3fn_bytes(y):
    return np.clip(np.asarray(y, np.float64), -448.0, 448.0).astype(np.float32).astype(ml_dtypes.float8_e4m3fn).view(np.uint8)


def e4m3fn_values(b):
    return np.asarray(b, np.uint8).view(ml_dtypes.float8_e4m3fn).astype(np.float64)


def setup_inputs():
    d = draw0()
    x0 = np.asarray(d['A']).astype(np.float64)
    s = (np.max(np.abs(x0), axis=(0,), keepdims=True) / 448.0).astype(np.float32)
    out = {}
    for k, v in d.items():
        if k == 'A':
            out['A_bytes'] = e4m3fn_bytes(x0 / s.astype(np.float64))
            out['A_scale'] = s
        else:
            out[k] = v
    return out


def reference(x, A_bytes, A_scale, W0_words, W0_scales, b0):
    return core(x, e4m3fn_values(A_bytes) * A_scale.astype(np.float64), W0_words, W0_scales, b0)

@@ -1,0 +1,266 @@
+from contextlib import ExitStack
+
+import concourse.mybir as mybir
+from concourse.masks import make_identity
+
+F32 = mybir.dt.float32
+BF16 = mybir.dt.bfloat16
+I32 = mybir.dt.int32
+U32 = mybir.dt.uint32
+U8 = mybir.dt.uint8
+FP8 = mybir.dt.float8_e4m3fn
+FP8X4 = mybir.dt.float8_e4m3fn_x4
+MULT = mybir.AluOpType.mult
+ADD = mybir.AluOpType.add
+ACT = mybir.ActivationFunctionType
+
+NODES, BATCH, CHAN, HID = 1024, 8, 512, 128
+P = 128
+VT = NODES // P
+FLOPS = 2 * NODES * NODES * BATCH * CHAN + 2 * NODES * BATCH * CHAN * 2 * HID
+
+
+SPLIT = True
+IL_SCALAR = {(0, 1, 1), (1, 0, 0), (1, 0, 1), (2, 0, 0), (2, 0, 1)}
+HEAD = (
+    "cast 0, il 0 0 2, tra 0, cast 1, il 0 1 1, cast 2, il 0 1 0, eva 0, qx 0, cast 3, "
+    "tra 1, eva 1, tra 2, tra 3, eva 2, il 1 0 0, qa 0, qa 1, il 1 0 1, cast 4, "
+    "qa 2, eva 3, mm1 0 2, tra 4, cast 5, il 1 1 2, qa 3, tra 5, eva 4, evg 0 2, "
+    "mm1 0 0, mm1 0 1, cast 6, mm1 0 3, cast 7, evg 0 0, qx 1, tra 6, evg 0 1, eva 5, "
+    "mm1 1 3, evg 0 3, evg 1 3, tra 7, il 2 0 1, qa 4, eva 6, il 2 0 0, mm1 1 2, qg 0 0, "
+    "mm1 1 0, mm1 1 1, evg 1 2 V, evg 1 0, mm1 0 4, qa 5, qa 6, mm1 1 6, mm2 0 0, eva 7, "
+    "evg 1 1, il 2 1 2, mm1 1 4, evg 0 4, sig 0 0, evg 1 6, qa 7, mm1 0 6, qg 1 0, evg 1 4, "
+    "mm1 0 5, mm1 1 7, glu 0 0, mm1 0 7, evg 0 6, evg 0 5, qx 2, mm2 1 0, tro 0 0, evg 1 7, "
+    "evg 0 7, il 3 1 2, qg 0 4, sig 1 0, mm1 2 0, evo 0 0, mm1 2 1, mm1 1 5, mm1 2 2, evg 2 0, "
+    "glu 1 0, mm2 0 4, il 4 0 2, mm1 2 3, evg 1 5, evg 2 1, sig 0 4, qg 1 4, glu 0 4, mm1 2 4, "
+    "evg 2 2, evg 2 3, mm1 2 5, il 3 0 2, mm2 1 4, qg 2 0, evg 2 4, sig 1 4, tro 0 4, glu 1 4, "
+    "mm1 2 6, mm1 2 7, evo 0 4, evg 2 6, qx 3, tro 1 0, evg 2 7, tro 1 4, mm2 2 0, evo 1 0, "
+    "sig 2 0, evg 2 5 V, evo 1 4, "
+)
+STEADY = (
+    "qg -1 4, mm1 0 0, mm1 0 1, glu -1 0, evg 0 0 V, evg 0 1, mm1 0 2, mm1 0 3, il 1 1 2, mm2 -1 4, "
+    "mm1 0 4, evg 0 2, mm1 0 5, evg 0 3, sig -1 4, evg 0 4, qg 0 0, evg 0 5, mm1 0 6, mm1 0 7, "
+    "glu -1 4, evg 0 6, mm2 0 0, tro -1 0, tro -1 4, qx 1, evg 0 7, sig 0 0, il 2 0 2, evo -1 0, "
+    "evo -1 4, "
+)
+TAIL = (
+    "mm1 7 0, mm1 7 1, qg 6 4, mm1 7 2, glu 6 0, evg 7 0 V, mm2 6 4, evg 7 1, mm1 7 3, sig 6 4, "
+    "evg 7 2 V, glu 6 4, evg 7 3, qg 7 0, mm1 7 4, mm1 7 5, evg 7 5 V, mm1 7 6, evg 7 4, evg 7 6 V, "
+    "mm2 7 0, qg 7 4, tro 6 0, sig 7 0, tro 6 4, mm1 7 7, evo 6 0, evg 7 7, glu 7 0, mm2 7 4, "
+    "sig 7 4, qg 7 6, evo 6 4, glu 7 4, mm2 7 6, tro 7 4, sig 7 6, glu 7 6, tro 7 0, evo 7 0 V, "
+    "evo 7 4, tro 7 6, evo 7 6 V, "
+)
+
+
+def program(do):
+    for text, entries in ((HEAD, (0,)), (STEADY, range(3, 7)), (TAIL, (0,))):
+        for b in entries:
+            for item in text.split(", "):
+                if item:
+                    words = item.split(" ")
+                    engine = words.pop() if words[-1] == "V" else None
+                    args = [int(w) for w in words[1:]]
+                    args[0] += b
+                    if words[0] in ("il", "qx") and args[0] > 7:
+                        continue
+                    do(words[0], *(args + [engine] if engine else args))
+
+
+def tile_stsgcm_pa_t_w8_kernel(tc, x, A_bytes, A_scale, W0_words, W0_scales, b0, out):
+    nc = tc.nc
+    with ExitStack() as ctx:
+        const = ctx.enter_context(tc.tile_pool(name="const", bufs=1))
+        raws = ctx.enter_context(tc.tile_pool(name="raws", bufs=1))
+        work = ctx.enter_context(tc.tile_pool(name="work", bufs=3))
+        psg = ctx.enter_context(tc.psum_pool(name="psg", bufs=4))
+        pst = ctx.enter_context(tc.psum_pool(name="pst", bufs=2))
+        psy = ctx.enter_context(tc.psum_pool(name="psy", bufs=1))
+
+        x_view = x.rearrange("(g p j) b c -> g b p j c", p=P, j=4)
+        a_view = A_bytes.rearrange("(k p) w -> p k w", p=P)
+        out_view = out.rearrange("(k p) b j -> b p k j", p=P)
+
+        warm = const.tile([P, 1], F32, name="warm")
+        nc.vector.memset(warm[:], 0.0)
+        nc.scalar.activation(out=warm[:], in_=warm[:], func=ACT.Sigmoid)
+        w_scales = const.tile([P, 2 * HID], U8, name="w_scales", align_bytes=64)
+        nc.vector.memset(w_scales[:].bitcast(I32), 0)
+
+        ident = const.tile([P, P], F32, name="ident")
+        make_identity(nc, ident[:])
+
+        scale = const.tile([P, 2, 4], F32, name="scale")
+        bias = const.tile([P, 2], BF16, name="bias")
+        with nc.allow_non_contiguous_dma(reason="short rows: four scales, one bias value"):
+            nc.scalar.dma_start(out=scale[:], in_=A_scale.rearrange("o (g p t) -> (o p) g t", p=P, t=4))
+            nc.scalar.dma_start(out=bias[:], in_=b0.rearrange("(o p) -> p o", p=P))
+
+        raw = {}
+        a_raw = {}
+
+        def load_x(b, g):
+            t = raws.tile([P, 4, CHAN], BF16, name="raw%d_%d" % (b, g))
+            nc.sync.dma_start(out=t[:], in_=x_view[g][b])
+            raw[b, g] = t
+
+        def load_a(lo, hi):
+            t = raws.tile([P, hi - lo, NODES], U8, name="abytes%d" % lo)
+            nc.sync.dma_start(out=t[:], in_=a_view[:, lo:hi, :])
+            for k in range(lo, hi):
+                a_raw[k] = t[:, k - lo, :]
+
+        load_a(0, 2)
+        load_x(0, 0)
+        load_x(0, 1)
+        load_a(2, 4)
+        load_x(1, 0)
+        load_x(1, 1)
+        load_a(4, 8)
+        w_words = const.tile([P, 2 * HID], U32, name="w_words", align_bytes=64)
+        nc.sync.dma_start(out=w_words[:].bitcast(I32), in_=W0_words.rearrange("o p n t -> (o p) (n t)").bitcast(I32))
+        ws_view = W0_scales.rearrange("o q n -> (o q) n").bitcast(I32)
+        for q in range(4):
+            nc.sync.dma_start(out=w_scales[32 * q : 32 * q + 4, :].bitcast(I32), in_=ws_view[4 * q : 4 * q + 4, :])
+        for b in range(2, 8):
+            for g in range(2):
+                load_x(b, g)
+
+        xq, aw, at, aq, xg, acc, gg, gq, yv, yg, sig, hh, tro, ob = ({} for _ in range(14))
+
+        def il(b, g, hf):
+            if b not in xg:
+                xg[b] = work.tile([P, 2, 2048], BF16, name="xg", bufs=3, align_bytes=64)
+            lo, hi = (0, 512) if hf == 2 else (256 * hf, 256 * hf + 256)
+            dst = xg[b][:, g, :].rearrange("p (t c) -> p t c", t=4)[:, :, lo:hi]
+            src = raw[b, g][:, :, lo:hi]
+            eng = nc.scalar.copy if (b, g, hf) in IL_SCALAR else nc.vector.tensor_copy
+            eng(
+                out=dst.rearrange("p t (m i j) -> p m j i t", i=2, j=4),
+                in_=src.rearrange("p j (m i t) -> p m j i t", i=2, t=4),
+            )
+
+        def qx(b):
+            codes = work.tile([P, 2, CHAN], U32, name="xcodes", bufs=4, align_bytes=64)
+            scales = work.tile([P, 2, CHAN], U8, name="xscales", bufs=4, align_bytes=64)
+            nc.vector.quantize_mx(
+                out=codes[:].rearrange("p g c -> p (g c)").bitcast(FP8X4),
+                scales=scales[:].rearrange("p g c -> p (g c)"),
+                in_=xg[b][:].rearrange("p g c -> p (g c)"),
+            )
+            xq[b] = (codes, scales)
+
+        def cast(k):
+            aw[k] = work.tile([P, NODES], BF16, name="aw", bufs=4)
+            nc.scalar.copy(out=aw[k][:], in_=a_raw[k].bitcast(FP8))
+
+        def tra(k):
+            at[k] = pst.tile([P, 4, P], F32, name="pst_t")
+            words = aw[k][:].bitcast(F32)
+            for g in range(2):
+                for u in range(2):
+                    nc.tensor.transpose(at[k][:, 2 * g + u, :], words[:, 256 * g + u : 256 * (g + 1) : 2], ident[:])
+
+        def eva(k):
+            ag = work.tile([P, NODES], BF16, name="ag", bufs=4, align_bytes=64)
+            for g in range(2):
+                nc.vector.tensor_tensor(
+                    out=ag[:, 512 * g : 512 * (g + 1)].rearrange("p (v u e) -> p v u e", u=2, e=2),
+                    in0=at[k][:, 2 * g : 2 * g + 2, :].rearrange("p u v -> p (u v)").bitcast(BF16).rearrange("p (u v e) -> p v u e", u=2, e=2),
+                    in1=scale[:, g, :].rearrange("p (u e) -> p u e", u=2).unsqueeze(1).to_broadcast([P, P, 2, 2]),
+                    op=MULT,
+                )
+            aq[k] = ag
+
+        def qa(k):
+            codes = const.tile([P, 2, P], U32, name="acodes%d" % k, align_bytes=64)
+            scales = const.tile([P, 2, P], U8, name="ascales%d" % k, align_bytes=64)
+            nc.vector.quantize_mx(
+                out=codes[:].rearrange("p g v -> p (g v)").bitcast(FP8X4),
+                scales=scales[:].rearrange("p g v -> p (g v)"),
+                in_=aq[k][:],
+            )
+            aq[k] = (codes, scales)
+
+        def mm1(b, k):
+            acc[b, k] = psg.tile([P, 4, P], F32, name="psg_t")
+            for t in range(4):
+                for g in range(2):
+                    nc.tensor.matmul_mx(
+                        out=acc[b, k][:, t, :],
+                        lhsT=xq[b][0][:, g, P * t : P * (t + 1)].bitcast(FP8X4),
+                        lhsT_scale=xq[b][1][:, g, P * t : P * (t + 1)],
+                        rhs=aq[k][0][:, g, :].bitcast(FP8X4),
+                        rhs_scale=aq[k][1][:, g, :],
+                        start=(g == 0),
+                        stop=(g == 1),
+                    )
+
+        def evg(b, k, engine="S"):
+            h = (b, 4 * (k // 4))
+            if h not in gg:
+                gg[h] = work.tile([P, 4, P, 4], BF16, name="gg", bufs=4, align_bytes=64)
+            eng = nc.scalar.copy if engine == "S" else nc.vector.tensor_copy
+            eng(out=gg[h][:, k % 4, :, :], in_=acc[b, k][:].rearrange("p t v -> p v t"))
+
+        def width(b, v0):
+            return 2 if (b, v0) in ((7, 4), (7, 6)) and SPLIT else 4
+
+        def qg(b, v0):
+            n = width(b, v0)
+            codes = work.tile([P, 512], U32, name="gcodes", bufs=4, align_bytes=64)
+            scales = work.tile([P, 512], U8, name="gscales", bufs=4, align_bytes=64)
+            src = gg[b, 4 * (v0 // 4)][:, v0 % 4 : v0 % 4 + n, :, :]
+            nc.vector.quantize_mx(
+                out=codes[:, : P * n].bitcast(FP8X4), scales=scales[:, : P * n], in_=src.rearrange("p k v t -> p (k v t)")
+            )
+            gq[b, v0] = (codes, scales)
+
+        def mm2(b, v0):
+            n = width(b, v0) * P
+            yv[b, v0] = psy.tile([P, 512], F32, name="yv")
+            yg[b, v0] = psy.tile([P, 512], F32, name="yg")
+            for dst, o in ((yg, 1), (yv, 0)):
+                nc.tensor.matmul_mx(
+                    out=dst[b, v0][:, :n],
+                    lhsT=w_words[:, HID * o : HID * (o + 1)].bitcast(FP8X4),
+                    lhsT_scale=w_scales[:, HID * o : HID * (o + 1)],
+                    rhs=gq[b, v0][0][:, :n].bitcast(FP8X4),
+                    rhs_scale=gq[b, v0][1][:, :n],
+                    start=True,
+                    stop=True,
+                )
+
+        def sigm(b, v0):
+            n = width(b, v0) * P
+            sig[b, v0] = work.tile([P, 512], F32, name="sig")
+            nc.scalar.activation(out=sig[b, v0][:, :n], in_=yg[b, v0][:, :n], func=ACT.Sigmoid, bias=bias[:, 1:2])
+
+        def glu(b, v0):
+            n = width(b, v0) * P
+            hh[b, v0] = work.tile([P, 512], F32, name="hh", bufs=6)
+            nc.vector.scalar_tensor_tensor(
+                out=hh[b, v0][:, :n], in0=yv[b, v0][:, :n], scalar=bias[:, 0:1], in1=sig[b, v0][:, :n], op0=ADD, op1=MULT
+            )
+
+        def trout(b, v0):
+            tro[b, v0] = pst.tile([P, 4, P], F32, name="pst_t")
+            for k in range(width(b, v0)):
+                nc.tensor.transpose(tro[b, v0][:, k, :], hh[b, v0][:, P * k : P * (k + 1)], ident[:])
+
+        def evo(b, v0, engine="S"):
+            n = width(b, v0)
+            ob[b, v0] = work.tile([P, 4, P], F32, name="ob", bufs=4)
+            eng = nc.scalar.copy if engine == "S" else nc.vector.tensor_copy
+            eng(out=ob[b, v0][:, :n, :], in_=tro[b, v0][:, :n, :])
+            nc.sync.dma_start(out=out_view[b][:, v0 : v0 + n, :], in_=ob[b, v0][:, :n, :])
+
+        stages = {
+            "il": il, "qx": qx, "cast": cast, "tra": tra, "eva": eva, "qa": qa, "mm1": mm1, "evg": evg,
+            "qg": qg, "mm2": mm2, "sig": sigm, "glu": glu, "tro": trout, "evo": evo,
+        }
+
+        def do(name, *args):
+            stages[name](*args)
+
+        with tc.manual_schedule():
+            program(do)

@@ -16,251 +16,275 @@ ACT = mybir.ActivationFunctionType
 
 NODES, BATCH, CHAN, HID = 1024, 8, 512, 128
 P = 128
-VT = NODES // P
+PAIR = 2 * P
+PAIRS = NODES // PAIR
 FLOPS = 2 * NODES * NODES * BATCH * CHAN + 2 * NODES * BATCH * CHAN * 2 * HID
-
-
-SPLIT = True
-IL_SCALAR = {(0, 1, 1), (1, 0, 0), (1, 0, 1), (2, 0, 0), (2, 0, 1)}
-HEAD = (
-    "cast 0, il 0 0 2, tra 0, cast 1, il 0 1 1, cast 2, il 0 1 0, eva 0, qx 0, cast 3, "
-    "tra 1, eva 1, tra 2, tra 3, eva 2, il 1 0 0, qa 0, qa 1, il 1 0 1, cast 4, "
-    "qa 2, eva 3, mm1 0 2, tra 4, cast 5, il 1 1 2, qa 3, tra 5, eva 4, evg 0 2, "
-    "mm1 0 0, mm1 0 1, cast 6, mm1 0 3, cast 7, evg 0 0, qx 1, tra 6, evg 0 1, eva 5, "
-    "mm1 1 3, evg 0 3, evg 1 3, tra 7, il 2 0 1, qa 4, eva 6, il 2 0 0, mm1 1 2, qg 0 0, "
-    "mm1 1 0, mm1 1 1, evg 1 2 V, evg 1 0, mm1 0 4, qa 5, qa 6, mm1 1 6, mm2 0 0, eva 7, "
-    "evg 1 1, il 2 1 2, mm1 1 4, evg 0 4, sig 0 0, evg 1 6, qa 7, mm1 0 6, qg 1 0, evg 1 4, "
-    "mm1 0 5, mm1 1 7, glu 0 0, mm1 0 7, evg 0 6, evg 0 5, qx 2, mm2 1 0, tro 0 0, evg 1 7, "
-    "evg 0 7, il 3 1 2, qg 0 4, sig 1 0, mm1 2 0, evo 0 0, mm1 2 1, mm1 1 5, mm1 2 2, evg 2 0, "
-    "glu 1 0, mm2 0 4, il 4 0 2, mm1 2 3, evg 1 5, evg 2 1, sig 0 4, qg 1 4, glu 0 4, mm1 2 4, "
-    "evg 2 2, evg 2 3, mm1 2 5, il 3 0 2, mm2 1 4, qg 2 0, evg 2 4, sig 1 4, tro 0 4, glu 1 4, "
-    "mm1 2 6, mm1 2 7, evo 0 4, evg 2 6, qx 3, tro 1 0, evg 2 7, tro 1 4, mm2 2 0, evo 1 0, "
-    "sig 2 0, evg 2 5 V, evo 1 4, "
-)
-STEADY = (
-    "qg -1 4, mm1 0 0, mm1 0 1, glu -1 0, evg 0 0 V, evg 0 1, mm1 0 2, mm1 0 3, il 1 1 2, mm2 -1 4, "
-    "mm1 0 4, evg 0 2, mm1 0 5, evg 0 3, sig -1 4, evg 0 4, qg 0 0, evg 0 5, mm1 0 6, mm1 0 7, "
-    "glu -1 4, evg 0 6, mm2 0 0, tro -1 0, tro -1 4, qx 1, evg 0 7, sig 0 0, il 2 0 2, evo -1 0, "
-    "evo -1 4, "
-)
-TAIL = (
-    "mm1 7 0, mm1 7 1, qg 6 4, mm1 7 2, glu 6 0, evg 7 0 V, mm2 6 4, evg 7 1, mm1 7 3, sig 6 4, "
-    "evg 7 2 V, glu 6 4, evg 7 3, qg 7 0, mm1 7 4, mm1 7 5, evg 7 5 V, mm1 7 6, evg 7 4, evg 7 6 V, "
-    "mm2 7 0, qg 7 4, tro 6 0, sig 7 0, tro 6 4, mm1 7 7, evo 6 0, evg 7 7, glu 7 0, mm2 7 4, "
-    "sig 7 4, qg 7 6, evo 6 4, glu 7 4, mm2 7 6, tro 7 4, sig 7 6, glu 7 6, tro 7 0, evo 7 0 V, "
-    "evo 7 4, tro 7 6, evo 7 6 V, "
-)
-
-
-def program(do):
-    for text, entries in ((HEAD, (0,)), (STEADY, range(3, 7)), (TAIL, (0,))):
-        for b in entries:
-            for item in text.split(", "):
-                if item:
-                    words = item.split(" ")
-                    engine = words.pop() if words[-1] == "V" else None
-                    args = [int(w) for w in words[1:]]
-                    args[0] += b
-                    if words[0] in ("il", "qx") and args[0] > 7:
-                        continue
-                    do(words[0], *(args + [engine] if engine else args))
 
 
 def tile_stsgcm_pa_t_w8_kernel(tc, x, A_bytes, A_scale, W0_words, W0_scales, b0, out):
     nc = tc.nc
     with ExitStack() as ctx:
         const = ctx.enter_context(tc.tile_pool(name="const", bufs=1))
-        raws = ctx.enter_context(tc.tile_pool(name="raws", bufs=1))
         work = ctx.enter_context(tc.tile_pool(name="work", bufs=3))
-        psg = ctx.enter_context(tc.psum_pool(name="psg", bufs=4))
-        pst = ctx.enter_context(tc.psum_pool(name="pst", bufs=2))
-        psy = ctx.enter_context(tc.psum_pool(name="psy", bufs=1))
+        psum = ctx.enter_context(tc.psum_pool(name="psum", bufs=8))
+        ctx.enter_context(tc.manual_schedule())
 
         x_view = x.rearrange("(g p j) b c -> g b p j c", p=P, j=4)
         a_view = A_bytes.rearrange("(k p) w -> p k w", p=P)
         out_view = out.rearrange("(k p) b j -> b p k j", p=P)
+
+        x_raw, a_raw = {}, {}
+
+        def load_x(b, g):
+            x_raw[b, g] = const.tile([P, 4, CHAN], BF16, name="x_raw%d_%d" % (b, g))
+            nc.sync.dma_start(out=x_raw[b, g][:], in_=x_view[g][b])
+
+        def load_a(q):
+            a_raw[q] = const.tile([P, 2, NODES], U8, name="a_raw%d" % q)
+            nc.sync.dma_start(out=a_raw[q][:], in_=a_view[:, 2 * q : 2 * q + 2, :])
 
         warm = const.tile([P, 1], F32, name="warm")
         nc.vector.memset(warm[:], 0.0)
         nc.scalar.activation(out=warm[:], in_=warm[:], func=ACT.Sigmoid)
         w_scales = const.tile([P, 2 * HID], U8, name="w_scales", align_bytes=64)
         nc.vector.memset(w_scales[:].bitcast(I32), 0)
-
         ident = const.tile([P, P], F32, name="ident")
         make_identity(nc, ident[:])
 
-        scale = const.tile([P, 2, 4], F32, name="scale")
-        bias = const.tile([P, 2], BF16, name="bias")
-        with nc.allow_non_contiguous_dma(reason="short rows: four scales, one bias value"):
-            nc.scalar.dma_start(out=scale[:], in_=A_scale.rearrange("o (g p t) -> (o p) g t", p=P, t=4))
-            nc.scalar.dma_start(out=bias[:], in_=b0.rearrange("(o p) -> p o", p=P))
-
-        raw = {}
-        a_raw = {}
-
-        def load_x(b, g):
-            t = raws.tile([P, 4, CHAN], BF16, name="raw%d_%d" % (b, g))
-            nc.sync.dma_start(out=t[:], in_=x_view[g][b])
-            raw[b, g] = t
-
-        def load_a(lo, hi):
-            t = raws.tile([P, hi - lo, NODES], U8, name="abytes%d" % lo)
-            nc.sync.dma_start(out=t[:], in_=a_view[:, lo:hi, :])
-            for k in range(lo, hi):
-                a_raw[k] = t[:, k - lo, :]
-
-        load_a(0, 2)
+        load_a(0)
         load_x(0, 0)
+        a_scale = const.tile([P, 2, 4], F32, name="a_scale")
+        with nc.allow_non_contiguous_dma(reason="four scales a partition and pass"):
+            nc.sync.dma_start(out=a_scale[:], in_=A_scale.rearrange("o (g p t) -> (o p) g t", p=P, t=4))
+        load_a(1)
         load_x(0, 1)
-        load_a(2, 4)
         load_x(1, 0)
+        load_a(2)
         load_x(1, 1)
-        load_a(4, 8)
+        load_a(3)
         w_words = const.tile([P, 2 * HID], U32, name="w_words", align_bytes=64)
         nc.sync.dma_start(out=w_words[:].bitcast(I32), in_=W0_words.rearrange("o p n t -> (o p) (n t)").bitcast(I32))
         ws_view = W0_scales.rearrange("o q n -> (o q) n").bitcast(I32)
-        for q in range(4):
-            nc.sync.dma_start(out=w_scales[32 * q : 32 * q + 4, :].bitcast(I32), in_=ws_view[4 * q : 4 * q + 4, :])
-        for b in range(2, 8):
+        for r in range(4):
+            nc.sync.dma_start(out=w_scales[32 * r : 32 * r + 4, :].bitcast(I32), in_=ws_view[4 * r : 4 * r + 4, :])
+        bias_col = const.tile([P, 2], BF16, name="bias_col")
+        with nc.allow_non_contiguous_dma(reason="one bias value a partition"):
+            nc.sync.dma_start(out=bias_col[:], in_=b0.rearrange("(o p) -> p o", p=P))
+        for b in range(2, BATCH):
             for g in range(2):
                 load_x(b, g)
 
-        xq, aw, at, aq, xg, acc, gg, gq, yv, yg, sig, hh, tro, ob = ({} for _ in range(14))
+        x_il, x_q, a_wide, a_bank, a_il, a_q, g_bank, g_il, g_q, y_bank, gate, gated, o_bank = ({} for i in range(13))
 
-        def il(b, g, hf):
-            if b not in xg:
-                xg[b] = work.tile([P, 2, 2048], BF16, name="xg", bufs=3, align_bytes=64)
-            lo, hi = (0, 512) if hf == 2 else (256 * hf, 256 * hf + 256)
-            dst = xg[b][:, g, :].rearrange("p (t c) -> p t c", t=4)[:, :, lo:hi]
-            src = raw[b, g][:, :, lo:hi]
-            eng = nc.scalar.copy if (b, g, hf) in IL_SCALAR else nc.vector.tensor_copy
-            eng(
-                out=dst.rearrange("p t (m i j) -> p m j i t", i=2, j=4),
-                in_=src.rearrange("p j (m i t) -> p m j i t", i=2, t=4),
+        def quantize(name, bufs, pool, src, cols):
+            codes = pool.tile([P, cols], U32, name=name + "_codes", bufs=bufs, align_bytes=64)
+            scales = pool.tile([P, cols], U8, name=name + "_scales", bufs=bufs, align_bytes=64)
+            nc.vector.quantize_mx(out=codes[:].bitcast(FP8X4), scales=scales[:], in_=src)
+            return codes, scales
+
+        def interleave_x(b, g, copy):
+            x_il[b, g] = work.tile([P, 4 * CHAN], BF16, name="x_il", bufs=4, align_bytes=64)
+            copy(
+                out=x_il[b, g][:].rearrange("p (t m i j) -> p m j i t", t=4, i=2, j=4),
+                in_=x_raw[b, g][:].rearrange("p j (m i t) -> p m j i t", i=2, t=4),
             )
 
-        def qx(b):
-            codes = work.tile([P, 2, CHAN], U32, name="xcodes", bufs=4, align_bytes=64)
-            scales = work.tile([P, 2, CHAN], U8, name="xscales", bufs=4, align_bytes=64)
-            nc.vector.quantize_mx(
-                out=codes[:].rearrange("p g c -> p (g c)").bitcast(FP8X4),
-                scales=scales[:].rearrange("p g c -> p (g c)"),
-                in_=xg[b][:].rearrange("p g c -> p (g c)"),
-            )
-            xq[b] = (codes, scales)
+        def quantize_x(b, g):
+            x_q[b, g] = quantize("x", 8, work, x_il[b, g][:], CHAN)
 
-        def cast(k):
-            aw[k] = work.tile([P, NODES], BF16, name="aw", bufs=4)
-            nc.scalar.copy(out=aw[k][:], in_=a_raw[k].bitcast(FP8))
+        def widen_a(q, k, copy):
+            a_wide[q, k] = work.tile([P, NODES], BF16, name="a_wide", bufs=4)
+            copy(out=a_wide[q, k][:], in_=a_raw[q][:, k, :].bitcast(FP8))
 
-        def tra(k):
-            at[k] = pst.tile([P, 4, P], F32, name="pst_t")
-            words = aw[k][:].bitcast(F32)
+        def turn_a(q):
             for g in range(2):
-                for u in range(2):
-                    nc.tensor.transpose(at[k][:, 2 * g + u, :], words[:, 256 * g + u : 256 * (g + 1) : 2], ident[:])
+                a_bank[q, g] = psum.tile([P, 2, PAIR], F32, name="bank")
+                for k in range(2):
+                    words = a_wide[q, k][:].bitcast(F32)
+                    for u in range(2):
+                        nc.tensor.transpose(a_bank[q, g][:, u, P * k : P * (k + 1)], words[:, 256 * g + u : 256 * (g + 1) : 2], ident[:])
 
-        def eva(k):
-            ag = work.tile([P, NODES], BF16, name="ag", bufs=4, align_bytes=64)
-            for g in range(2):
-                nc.vector.tensor_tensor(
-                    out=ag[:, 512 * g : 512 * (g + 1)].rearrange("p (v u e) -> p v u e", u=2, e=2),
-                    in0=at[k][:, 2 * g : 2 * g + 2, :].rearrange("p u v -> p (u v)").bitcast(BF16).rearrange("p (u v e) -> p v u e", u=2, e=2),
-                    in1=scale[:, g, :].rearrange("p (u e) -> p u e", u=2).unsqueeze(1).to_broadcast([P, P, 2, 2]),
-                    op=MULT,
-                )
-            aq[k] = ag
-
-        def qa(k):
-            codes = const.tile([P, 2, P], U32, name="acodes%d" % k, align_bytes=64)
-            scales = const.tile([P, 2, P], U8, name="ascales%d" % k, align_bytes=64)
-            nc.vector.quantize_mx(
-                out=codes[:].rearrange("p g v -> p (g v)").bitcast(FP8X4),
-                scales=scales[:].rearrange("p g v -> p (g v)"),
-                in_=aq[k][:],
+        def scale_a(q, g):
+            a_il[q, g] = work.tile([P, PAIR, 2, 2], BF16, name="a_il", bufs=3, align_bytes=64)
+            nc.vector.tensor_tensor(
+                out=a_il[q, g][:],
+                in0=a_bank[q, g][:].rearrange("p u v -> p (u v)").bitcast(BF16).rearrange("p (u v e) -> p v u e", u=2, e=2),
+                in1=a_scale[:, g, :].rearrange("p (u e) -> p u e", u=2).unsqueeze(1).to_broadcast([P, PAIR, 2, 2]),
+                op=MULT,
             )
-            aq[k] = (codes, scales)
 
-        def mm1(b, k):
-            acc[b, k] = psg.tile([P, 4, P], F32, name="psg_t")
+        def quantize_a(q, g):
+            a_q[q, g] = quantize("a%d_%d" % (q, g), 1, const, a_il[q, g][:].rearrange("p v u e -> p (v u e)"), PAIR)
+
+        def aggregate(b, k0, n):
+            for k in range(k0, k0 + n):
+                g_bank[b, k] = psum.tile([P, 4, P], F32, name="bank")
             for t in range(4):
                 for g in range(2):
-                    nc.tensor.matmul_mx(
-                        out=acc[b, k][:, t, :],
-                        lhsT=xq[b][0][:, g, P * t : P * (t + 1)].bitcast(FP8X4),
-                        lhsT_scale=xq[b][1][:, g, P * t : P * (t + 1)],
-                        rhs=aq[k][0][:, g, :].bitcast(FP8X4),
-                        rhs_scale=aq[k][1][:, g, :],
-                        start=(g == 0),
-                        stop=(g == 1),
-                    )
+                    for k in range(k0, k0 + n):
+                        cols = slice(P * (k % 2), P * (k % 2 + 1))
+                        nc.tensor.matmul_mx(
+                            out=g_bank[b, k][:, t, :],
+                            lhsT=x_q[b, g][0][:, P * t : P * (t + 1)].bitcast(FP8X4),
+                            lhsT_scale=x_q[b, g][1][:, P * t : P * (t + 1)],
+                            rhs=a_q[k // 2, g][0][:, cols].bitcast(FP8X4),
+                            rhs_scale=a_q[k // 2, g][1][:, cols],
+                            start=(g == 0),
+                            stop=(g == 1),
+                        )
 
-        def evg(b, k, engine="S"):
-            h = (b, 4 * (k // 4))
-            if h not in gg:
-                gg[h] = work.tile([P, 4, P, 4], BF16, name="gg", bufs=4, align_bytes=64)
-            eng = nc.scalar.copy if engine == "S" else nc.vector.tensor_copy
-            eng(out=gg[h][:, k % 4, :, :], in_=acc[b, k][:].rearrange("p t v -> p v t"))
+        def empty_g(b, k, copy):
+            if (b, k // 4) not in g_il:
+                g_il[b, k // 4] = work.tile([P, 4, P, 4], BF16, name="g_il", bufs=4, align_bytes=64)
+            copy(out=g_il[b, k // 4][:, k % 4, :, :], in_=g_bank[b, k][:].rearrange("p t v -> p v t"))
 
-        def width(b, v0):
-            return 2 if (b, v0) in ((7, 4), (7, 6)) and SPLIT else 4
+        def quantize_g(b, k0, n):
+            src = g_il[b, k0 // 4][:, k0 % 4 : k0 % 4 + n, :, :]
+            g_q[b, k0] = quantize("g%d" % n, 3, work, src.rearrange("p k v t -> p (k v t)"), n * P)
 
-        def qg(b, v0):
-            n = width(b, v0)
-            codes = work.tile([P, 512], U32, name="gcodes", bufs=4, align_bytes=64)
-            scales = work.tile([P, 512], U8, name="gscales", bufs=4, align_bytes=64)
-            src = gg[b, 4 * (v0 // 4)][:, v0 % 4 : v0 % 4 + n, :, :]
-            nc.vector.quantize_mx(
-                out=codes[:, : P * n].bitcast(FP8X4), scales=scales[:, : P * n], in_=src.rearrange("p k v t -> p (k v t)")
-            )
-            gq[b, v0] = (codes, scales)
-
-        def mm2(b, v0):
-            n = width(b, v0) * P
-            yv[b, v0] = psy.tile([P, 512], F32, name="yv")
-            yg[b, v0] = psy.tile([P, 512], F32, name="yg")
-            for dst, o in ((yg, 1), (yv, 0)):
+        def project(b, k0, n):
+            for half in (1, 0):
+                y_bank[b, k0, half] = psum.tile([P, n * P], F32, name="bank")
                 nc.tensor.matmul_mx(
-                    out=dst[b, v0][:, :n],
-                    lhsT=w_words[:, HID * o : HID * (o + 1)].bitcast(FP8X4),
-                    lhsT_scale=w_scales[:, HID * o : HID * (o + 1)],
-                    rhs=gq[b, v0][0][:, :n].bitcast(FP8X4),
-                    rhs_scale=gq[b, v0][1][:, :n],
+                    out=y_bank[b, k0, half][:],
+                    lhsT=w_words[:, HID * half : HID * (half + 1)].bitcast(FP8X4),
+                    lhsT_scale=w_scales[:, HID * half : HID * (half + 1)],
+                    rhs=g_q[b, k0][0][:].bitcast(FP8X4),
+                    rhs_scale=g_q[b, k0][1][:],
                     start=True,
                     stop=True,
                 )
 
-        def sigm(b, v0):
-            n = width(b, v0) * P
-            sig[b, v0] = work.tile([P, 512], F32, name="sig")
-            nc.scalar.activation(out=sig[b, v0][:, :n], in_=yg[b, v0][:, :n], func=ACT.Sigmoid, bias=bias[:, 1:2])
+        def sigmoid(b, k0, n):
+            gate[b, k0] = work.tile([P, n * P], F32, name="gate", bufs=6)
+            nc.scalar.activation(out=gate[b, k0][:], in_=y_bank[b, k0, 1][:], func=ACT.Sigmoid, bias=bias_col[:, 1:2])
 
-        def glu(b, v0):
-            n = width(b, v0) * P
-            hh[b, v0] = work.tile([P, 512], F32, name="hh", bufs=6)
+        def multiply(b, k0, n):
+            gated[b, k0] = work.tile([P, n * P], F32, name="gated", bufs=4)
             nc.vector.scalar_tensor_tensor(
-                out=hh[b, v0][:, :n], in0=yv[b, v0][:, :n], scalar=bias[:, 0:1], in1=sig[b, v0][:, :n], op0=ADD, op1=MULT
+                out=gated[b, k0][:], in0=y_bank[b, k0, 0][:], scalar=bias_col[:, 0:1], in1=gate[b, k0][:], op0=ADD, op1=MULT
             )
 
-        def trout(b, v0):
-            tro[b, v0] = pst.tile([P, 4, P], F32, name="pst_t")
-            for k in range(width(b, v0)):
-                nc.tensor.transpose(tro[b, v0][:, k, :], hh[b, v0][:, P * k : P * (k + 1)], ident[:])
+        def turn_out(b, k0, n):
+            o_bank[b, k0] = psum.tile([P, n, P], F32, name="bank")
+            for k in range(n):
+                nc.tensor.transpose(o_bank[b, k0][:, k, :], gated[b, k0][:, P * k : P * (k + 1)], ident[:])
 
-        def evo(b, v0, engine="S"):
-            n = width(b, v0)
-            ob[b, v0] = work.tile([P, 4, P], F32, name="ob", bufs=4)
-            eng = nc.scalar.copy if engine == "S" else nc.vector.tensor_copy
-            eng(out=ob[b, v0][:, :n, :], in_=tro[b, v0][:, :n, :])
-            nc.sync.dma_start(out=out_view[b][:, v0 : v0 + n, :], in_=ob[b, v0][:, :n, :])
+        def store(b, k0, n, copy):
+            rows = work.tile([P, n, HID], F32, name="rows", bufs=6)
+            copy(out=rows[:], in_=o_bank[b, k0][:])
+            nc.sync.dma_start(out=out_view[b][:, k0 : k0 + n, :], in_=rows[:])
 
-        stages = {
-            "il": il, "qx": qx, "cast": cast, "tra": tra, "eva": eva, "qa": qa, "mm1": mm1, "evg": evg,
-            "qg": qg, "mm2": mm2, "sig": sigm, "glu": glu, "tro": trout, "evo": evo,
-        }
+        groups = [(b, k0, 4) for k0 in (0, 4) for b in range(2)] + [(b, k0, 4) for b in range(2, BATCH) for k0 in (0, 4)]
+        last = len(groups) - 1
+        vector, scalar = nc.vector.tensor_copy, nc.scalar.copy
+        x_parts = [(b, g) for b in range(BATCH) for g in range(2)]
 
-        def do(name, *args):
-            stages[name](*args)
+        def widen_pair(q):
+            for k in range(2):
+                widen_a(q, k, scalar)
 
-        with tc.manual_schedule():
-            program(do)
+        widen_a(0, 0, scalar)
+        widen_a(0, 1, vector)
+        interleave_x(0, 0, vector)
+        turn_a(0)
+        widen_pair(1)
+        turn_a(1)
+        interleave_x(0, 1, scalar)
+        scale_a(0, 0)
+        quantize_x(0, 0)
+        scale_a(0, 1)
+        quantize_a(0, 0)
+        scale_a(1, 0)
+        quantize_a(0, 1)
+        quantize_x(0, 1)
+        widen_pair(2)
+        widen_pair(3)
+        for h in range(last):
+            b, k0, n = groups[h]
+            helper = vector if h + 3 >= len(x_parts) else scalar
+            aggregate(b, k0, 2)
+            if h == 0:
+                turn_a(2)
+            if h == 0:
+                scale_a(1, 1)
+                quantize_a(1, 0)
+                interleave_x(1, 1, scalar)
+                quantize_a(1, 1)
+                interleave_x(1, 0, vector)
+                scale_a(2, 0)
+                quantize_x(1, 0)
+                scale_a(2, 1)
+                quantize_x(1, 1)
+                quantize_a(2, 0)
+            if h == 1:
+                quantize_a(2, 1)
+                scale_a(3, 0)
+            if h > 0:
+                quantize_g(*groups[h - 1])
+            if h == 1:
+                scale_a(3, 1)
+            if 1 < h and h + 2 < len(x_parts):
+                quantize_x(*x_parts[h + 2])
+            if h >= 2:
+                sigmoid(*groups[h - 2])
+            if h % 2 == 0 and h >= 4:
+                store(*groups[h - 4], scalar)
+                store(*groups[h - 3], helper)
+            if h >= 2:
+                multiply(*groups[h - 2])
+            empty_g(b, k0, scalar)
+            empty_g(b, k0 + 1, helper)
+            aggregate(b, k0 + 2, 2)
+            if h == 1:
+                quantize_a(3, 0)
+                quantize_a(3, 1)
+            if 0 < h and h + 3 < len(x_parts):
+                interleave_x(*x_parts[h + 3], vector)
+            empty_g(b, k0 + 2, scalar)
+            empty_g(b, k0 + 3, helper)
+            if h == 0:
+                turn_a(3)
+            if h > 0:
+                project(*groups[h - 1])
+            if h % 2 == 1 and h >= 3:
+                turn_out(*groups[h - 3])
+                turn_out(*groups[h - 2])
+        b = BATCH - 1
+        aggregate(b, 4, 2)
+        quantize_g(b, 0, 4)
+        sigmoid(b - 1, 4, 4)
+        empty_g(b, 4, scalar)
+        empty_g(b, 5, vector)
+        aggregate(b, 6, 1)
+        project(b, 0, 4)
+        aggregate(b, 7, 1)
+        multiply(b - 1, 4, 4)
+        quantize_g(b, 4, 2)
+        empty_g(b, 6, scalar)
+        sigmoid(b, 0, 4)
+        empty_g(b, 7, scalar)
+        quantize_g(b, 6, 1)
+        project(b, 4, 2)
+        project(b, 6, 1)
+        turn_out(b - 1, 0, 4)
+        turn_out(b - 1, 4, 4)
+        multiply(b, 0, 4)
+        quantize_g(b, 7, 1)
+        project(b, 7, 1)
+        sigmoid(b, 4, 2)
+        sigmoid(b, 6, 1)
+        store(b - 1, 0, 4, scalar)
+        sigmoid(b, 7, 1)
+        turn_out(b, 0, 4)
+        multiply(b, 4, 2)
+        multiply(b, 6, 1)
+        store(b - 1, 4, 4, vector)
+        multiply(b, 7, 1)
+        turn_out(b, 4, 2)
+        turn_out(b, 6, 1)
+        turn_out(b, 7, 1)
+        store(b, 0, 4, scalar)
+        store(b, 4, 2, vector)
+        store(b, 6, 1, vector)
+        store(b, 7, 1, scalar)

@@ -105,7 +105,7 @@ def tile_stsgcm_pa_t_w8_kernel(tc, x, A_bytes, A_scale, W0_words, W0_scales, b0,
                         nc.tensor.transpose(a_bank[q, g][:, u, P * k : P * (k + 1)], words[:, 256 * g + u : 256 * (g + 1) : 2], ident[:])
 
         def scale_a(q, g):
-            a_il[q, g] = work.tile([P, PAIR, 2, 2], BF16, name="a_il", bufs=3, align_bytes=64)
+            a_il[q, g] = work.tile([P, PAIR, 2, 2], BF16, name="a_il", bufs=4, align_bytes=64)
             nc.vector.tensor_tensor(
                 out=a_il[q, g][:],
                 in0=a_bank[q, g][:].rearrange("p u v -> p (u v)").bitcast(BF16).rearrange("p (u v e) -> p v u e", u=2, e=2),
@@ -175,6 +175,28 @@ def tile_stsgcm_pa_t_w8_kernel(tc, x, A_bytes, A_scale, W0_words, W0_scales, b0,
             copy(out=rows[:], in_=o_bank[b, k0][:])
             nc.sync.dma_start(out=out_view[b][:, k0 : k0 + n, :], in_=rows[:])
 
+        pool = "pool"
+
+        def interleave_part(b, g, lo, hi, engine):
+            dst = x_il[b, g][:].rearrange("p (t m j) -> p t m j", t=4, j=4)[:, :, lo:hi, :]
+            src = x_raw[b, g][:, :, 4 * lo : 4 * hi]
+            if engine is pool:
+                nc.gpsimd.tensor_scalar(
+                    out=dst.rearrange("p t m j -> p m t j"),
+                    in0=src.rearrange("p j (m t) -> p m t j", t=4),
+                    scalar1=1.0,
+                    scalar2=0.0,
+                    op0=MULT,
+                    op1=ADD,
+                )
+            else:
+                engine(out=dst.rearrange("p t (m i) j -> p m j i t", i=2), in_=src.rearrange("p j (m i t) -> p m j i t", i=2, t=4))
+
+        def interleave_shared(b, g, *shares):
+            x_il[b, g] = work.tile([P, 4 * CHAN], BF16, name="x_il_shared", bufs=1, align_bytes=64)
+            for engine, lo, hi in shares:
+                interleave_part(b, g, lo, hi, engine)
+
         groups = [(b, k0, 4) for k0 in (0, 4) for b in range(2)] + [(b, k0, 4) for b in range(2, BATCH) for k0 in (0, 4)]
         last = len(groups) - 1
         vector, scalar = nc.vector.tensor_copy, nc.scalar.copy
@@ -184,70 +206,101 @@ def tile_stsgcm_pa_t_w8_kernel(tc, x, A_bytes, A_scale, W0_words, W0_scales, b0,
             for k in range(2):
                 widen_a(q, k, scalar)
 
+        def prepare_a(q):
+            for g in range(2):
+                scale_a(q, g)
+            for g in range(2):
+                quantize_a(q, g)
+
+        def empty_pair(b, k0, second):
+            empty_g(b, k0, scalar)
+            empty_g(b, k0 + 1, second)
+
         widen_a(0, 0, scalar)
         widen_a(0, 1, vector)
-        interleave_x(0, 0, vector)
+        interleave_shared(0, 0, (vector, 0, P))
         turn_a(0)
         widen_pair(1)
         turn_a(1)
-        interleave_x(0, 1, scalar)
-        scale_a(0, 0)
         quantize_x(0, 0)
+        interleave_shared(0, 1, (pool, 0, P))
+        scale_a(0, 0)
         scale_a(0, 1)
-        quantize_a(0, 0)
         scale_a(1, 0)
+        widen_pair(2)
+        turn_a(2)
+        quantize_a(0, 0)
         quantize_a(0, 1)
         quantize_x(0, 1)
-        widen_pair(2)
+        interleave_shared(1, 1, (pool, 0, P))
+        aggregate(0, 0, 2)
         widen_pair(3)
-        for h in range(last):
+        interleave_x(1, 0, scalar)
+        scale_a(1, 1)
+        scale_a(2, 0)
+        scale_a(2, 1)
+        turn_a(3)
+        for q in (1, 2):
+            for g in range(2):
+                quantize_a(q, g)
+        quantize_x(1, 0)
+        quantize_x(1, 1)
+        interleave_shared(2, 0, (pool, 0, P // 2))
+        aggregate(0, 2, 2)
+        empty_pair(0, 0, scalar)
+        aggregate(0, 4, 2)
+        scale_a(3, 0)
+        scale_a(3, 1)
+        aggregate(1, 0, 2)
+        empty_pair(0, 2, scalar)
+        empty_pair(0, 4, scalar)
+        quantize_g(0, 0, 4)
+        quantize_a(3, 0)
+        quantize_a(3, 1)
+        interleave_part(2, 0, P // 2, P, vector)
+        aggregate(1, 2, 2)
+        empty_pair(1, 0, scalar)
+        project(0, 0, 4)
+        aggregate(0, 6, 2)
+        empty_pair(1, 2, vector)
+        sigmoid(0, 0, 4)
+        quantize_x(2, 0)
+        quantize_g(1, 0, 4)
+        multiply(0, 0, 4)
+        aggregate(1, 4, 2)
+        empty_pair(0, 6, scalar)
+        interleave_x(2, 1, vector)
+        project(1, 0, 4)
+        aggregate(1, 6, 2)
+        sigmoid(1, 0, 4)
+        empty_pair(1, 4, scalar)
+        quantize_g(0, 4, 4)
+        multiply(1, 0, 4)
+        quantize_x(2, 1)
+        interleave_x(3, 0, vector)
+        empty_pair(1, 6, scalar)
+        project(0, 4, 4)
+        turn_out(0, 0, 4)
+        turn_out(1, 0, 4)
+        for h in range(4, last):
             b, k0, n = groups[h]
             helper = vector if h + 3 >= len(x_parts) else scalar
             aggregate(b, k0, 2)
-            if h == 0:
-                turn_a(2)
-            if h == 0:
-                scale_a(1, 1)
-                quantize_a(1, 0)
-                interleave_x(1, 1, scalar)
-                quantize_a(1, 1)
-                interleave_x(1, 0, vector)
-                scale_a(2, 0)
-                quantize_x(1, 0)
-                scale_a(2, 1)
-                quantize_x(1, 1)
-                quantize_a(2, 0)
-            if h == 1:
-                quantize_a(2, 1)
-                scale_a(3, 0)
-            if h > 0:
-                quantize_g(*groups[h - 1])
-            if h == 1:
-                scale_a(3, 1)
-            if 1 < h and h + 2 < len(x_parts):
+            quantize_g(*groups[h - 1])
+            if h + 2 < len(x_parts):
                 quantize_x(*x_parts[h + 2])
-            if h >= 2:
-                sigmoid(*groups[h - 2])
-            if h % 2 == 0 and h >= 4:
+            sigmoid(*groups[h - 2])
+            if h % 2 == 0:
                 store(*groups[h - 4], scalar)
                 store(*groups[h - 3], helper)
-            if h >= 2:
-                multiply(*groups[h - 2])
-            empty_g(b, k0, scalar)
-            empty_g(b, k0 + 1, helper)
+            multiply(*groups[h - 2])
+            empty_pair(b, k0, helper)
             aggregate(b, k0 + 2, 2)
-            if h == 1:
-                quantize_a(3, 0)
-                quantize_a(3, 1)
-            if 0 < h and h + 3 < len(x_parts):
+            if h + 3 < len(x_parts):
                 interleave_x(*x_parts[h + 3], vector)
-            empty_g(b, k0 + 2, scalar)
-            empty_g(b, k0 + 3, helper)
-            if h == 0:
-                turn_a(3)
-            if h > 0:
-                project(*groups[h - 1])
-            if h % 2 == 1 and h >= 3:
+            empty_pair(b, k0 + 2, helper)
+            project(*groups[h - 1])
+            if h % 2 == 1:
                 turn_out(*groups[h - 3])
                 turn_out(*groups[h - 2])
         b = BATCH - 1

@@ -20,6 +20,9 @@ PAIR = 2 * P
 PAIRS = NODES // PAIR
 FLOPS = 2 * NODES * NODES * BATCH * CHAN + 2 * NODES * BATCH * CHAN * 2 * HID
 
+POOL_SHARE = 112
+DIRECT = (11, 12)
+
 
 def tile_stsgcm_pa_t_w8_kernel(tc, x, A_bytes, A_scale, W0_words, W0_scales, b0, out):
     nc = tc.nc
@@ -73,8 +76,10 @@ def tile_stsgcm_pa_t_w8_kernel(tc, x, A_bytes, A_scale, W0_words, W0_scales, b0,
         for b in range(2, BATCH):
             for g in range(2):
                 load_x(b, g)
+        bias_row = const.tile([P, 2 * HID], BF16, name="bias_row")
+        nc.sync.dma_start(out=bias_row[:], in_=b0.partition_broadcast(P))
 
-        x_il, x_q, a_wide, a_bank, a_il, a_q, g_bank, g_il, g_q, y_bank, gate, gated, o_bank = ({} for i in range(13))
+        x_il, x_q, a_wide, a_bank, a_il, a_q, g_bank, g_il, g_q, y_bank, gate, gated, o_bank, z = ({} for i in range(14))
 
         def quantize(name, bufs, pool, src, cols):
             codes = pool.tile([P, cols], U32, name=name + "_codes", bufs=bufs, align_bytes=64)
@@ -85,8 +90,8 @@ def tile_stsgcm_pa_t_w8_kernel(tc, x, A_bytes, A_scale, W0_words, W0_scales, b0,
         def interleave_x(b, g, copy):
             x_il[b, g] = work.tile([P, 4 * CHAN], BF16, name="x_il", bufs=4, align_bytes=64)
             copy(
-                out=x_il[b, g][:].rearrange("p (t m i j) -> p m j i t", t=4, i=2, j=4),
-                in_=x_raw[b, g][:].rearrange("p j (m i t) -> p m j i t", i=2, t=4),
+                out=x_il[b, g][:].rearrange("p (t m i j) -> p m j t i", t=4, i=2, j=4),
+                in_=x_raw[b, g][:].rearrange("p j (m i t) -> p m j t i", i=2, t=4),
             )
 
         def quantize_x(b, g):
@@ -175,6 +180,34 @@ def tile_stsgcm_pa_t_w8_kernel(tc, x, A_bytes, A_scale, W0_words, W0_scales, b0,
             copy(out=rows[:], in_=o_bank[b, k0][:])
             nc.sync.dma_start(out=out_view[b][:, k0 : k0 + n, :], in_=rows[:])
 
+        def project_direct(b, k0, n):
+            for k in range(k0, k0 + n):
+                if k % 2 == 0:
+                    y_bank[b, k] = psum.tile([P, 2, 2 * HID], F32, name="bank")
+                cols = slice(P * (k - k0), P * (k - k0 + 1))
+                nc.tensor.matmul_mx(
+                    out=y_bank[b, k - k % 2][:, k % 2, :],
+                    lhsT=g_q[b, k0][0][:, cols].bitcast(FP8X4),
+                    lhsT_scale=g_q[b, k0][1][:, cols],
+                    rhs=w_words[:].bitcast(FP8X4),
+                    rhs_scale=w_scales[:],
+                    start=True,
+                    stop=True,
+                )
+
+        def add_bias(b, k):
+            z[b, k] = work.tile([P, 2, 2 * HID], F32, name="z")
+            nc.vector.tensor_tensor(out=z[b, k][:], in0=y_bank[b, k][:], in1=bias_row[:].unsqueeze(1).to_broadcast([P, 2, 2 * HID]), op=ADD)
+
+        def sigmoid_direct(b, k):
+            gate[b, k] = work.tile([P, 2, HID], F32, name="gate", bufs=6)
+            nc.scalar.activation(out=gate[b, k][:], in_=z[b, k][:, :, HID:], func=ACT.Sigmoid)
+
+        def store_direct(b, k):
+            rows = work.tile([P, 2, HID], F32, name="rows", bufs=6)
+            nc.vector.tensor_tensor(out=rows[:], in0=z[b, k][:, :, :HID], in1=gate[b, k][:], op=MULT)
+            nc.sync.dma_start(out=out_view[b][:, k : k + 2, :], in_=rows[:])
+
         pool = "pool"
 
         def interleave_part(b, g, lo, hi, engine):
@@ -190,7 +223,7 @@ def tile_stsgcm_pa_t_w8_kernel(tc, x, A_bytes, A_scale, W0_words, W0_scales, b0,
                     op1=ADD,
                 )
             else:
-                engine(out=dst.rearrange("p t (m i) j -> p m j i t", i=2), in_=src.rearrange("p j (m i t) -> p m j i t", i=2, t=4))
+                engine(out=dst.rearrange("p t (m i) j -> p m j t i", i=2), in_=src.rearrange("p j (m i t) -> p m j t i", i=2, t=4))
 
         def interleave_shared(b, g, *shares):
             x_il[b, g] = work.tile([P, 4 * CHAN], BF16, name="x_il_shared", bufs=1, align_bytes=64)
@@ -223,16 +256,17 @@ def tile_stsgcm_pa_t_w8_kernel(tc, x, A_bytes, A_scale, W0_words, W0_scales, b0,
         widen_pair(1)
         turn_a(1)
         quantize_x(0, 0)
-        interleave_shared(0, 1, (pool, 0, P))
+        interleave_shared(0, 1, (pool, 0, POOL_SHARE))
         scale_a(0, 0)
         scale_a(0, 1)
         scale_a(1, 0)
+        interleave_part(0, 1, POOL_SHARE, P, scalar)
         widen_pair(2)
         turn_a(2)
         quantize_a(0, 0)
         quantize_a(0, 1)
         quantize_x(0, 1)
-        interleave_shared(1, 1, (pool, 0, P))
+        interleave_shared(1, 1, (pool, 0, POOL_SHARE))
         aggregate(0, 0, 2)
         widen_pair(3)
         interleave_x(1, 0, scalar)
@@ -243,6 +277,7 @@ def tile_stsgcm_pa_t_w8_kernel(tc, x, A_bytes, A_scale, W0_words, W0_scales, b0,
         for q in (1, 2):
             for g in range(2):
                 quantize_a(q, g)
+        interleave_part(1, 1, POOL_SHARE, P, vector)
         quantize_x(1, 0)
         quantize_x(1, 1)
         interleave_shared(2, 0, (pool, 0, P // 2))
@@ -284,60 +319,72 @@ def tile_stsgcm_pa_t_w8_kernel(tc, x, A_bytes, A_scale, W0_words, W0_scales, b0,
         turn_out(1, 0, 4)
         for h in range(4, last):
             b, k0, n = groups[h]
-            helper = vector if h + 3 >= len(x_parts) else scalar
+            old = groups[h - 2]
+            helper = vector if h == last - 1 else scalar
             aggregate(b, k0, 2)
+            if h - 2 in DIRECT:
+                add_bias(old[0], old[1])
+                add_bias(old[0], old[1] + 2)
             quantize_g(*groups[h - 1])
             if h + 2 < len(x_parts):
                 quantize_x(*x_parts[h + 2])
-            sigmoid(*groups[h - 2])
+            if h - 2 not in DIRECT:
+                sigmoid(*old)
             if h % 2 == 0:
-                store(*groups[h - 4], scalar)
-                store(*groups[h - 3], helper)
-            multiply(*groups[h - 2])
+                for i in (h - 4, h - 3):
+                    if i not in DIRECT:
+                        store(*groups[i], scalar)
+            if h - 2 in DIRECT:
+                sigmoid_direct(old[0], old[1])
+                sigmoid_direct(old[0], old[1] + 2)
+            else:
+                multiply(*old)
             empty_pair(b, k0, helper)
             aggregate(b, k0 + 2, 2)
             if h + 3 < len(x_parts):
                 interleave_x(*x_parts[h + 3], vector)
+            if h - 2 in DIRECT:
+                store_direct(old[0], old[1])
+                store_direct(old[0], old[1] + 2)
             empty_pair(b, k0 + 2, helper)
-            project(*groups[h - 1])
+            (project_direct if h - 1 in DIRECT else project)(*groups[h - 1])
             if h % 2 == 1:
-                turn_out(*groups[h - 3])
-                turn_out(*groups[h - 2])
+                for i in (h - 3, h - 2):
+                    if i not in DIRECT:
+                        turn_out(*groups[i])
         b = BATCH - 1
         aggregate(b, 4, 2)
         quantize_g(b, 0, 4)
         sigmoid(b - 1, 4, 4)
         empty_g(b, 4, scalar)
+        project(b, 0, 4)
+        multiply(b - 1, 4, 4)
         empty_g(b, 5, vector)
         aggregate(b, 6, 1)
-        project(b, 0, 4)
         aggregate(b, 7, 1)
-        multiply(b - 1, 4, 4)
+        sigmoid(b, 0, 4)
         quantize_g(b, 4, 2)
         empty_g(b, 6, scalar)
-        sigmoid(b, 0, 4)
         empty_g(b, 7, scalar)
-        quantize_g(b, 6, 1)
-        project(b, 4, 2)
-        project(b, 6, 1)
-        turn_out(b - 1, 0, 4)
-        turn_out(b - 1, 4, 4)
         multiply(b, 0, 4)
+        turn_out(b - 1, 4, 4)
+        project(b, 4, 2)
+        turn_out(b, 0, 4)
+        quantize_g(b, 6, 1)
+        store(b - 1, 4, 4, vector)
         quantize_g(b, 7, 1)
+        project(b, 6, 1)
         project(b, 7, 1)
         sigmoid(b, 4, 2)
+        store(b, 0, 4, scalar)
         sigmoid(b, 6, 1)
-        store(b - 1, 0, 4, scalar)
         sigmoid(b, 7, 1)
-        turn_out(b, 0, 4)
         multiply(b, 4, 2)
         multiply(b, 6, 1)
-        store(b - 1, 4, 4, vector)
         multiply(b, 7, 1)
         turn_out(b, 4, 2)
         turn_out(b, 6, 1)
         turn_out(b, 7, 1)
-        store(b, 0, 4, scalar)
         store(b, 4, 2, vector)
-        store(b, 6, 1, vector)
-        store(b, 7, 1, scalar)
+        store(b, 6, 1, scalar)
+        store(b, 7, 1, vector)

@@ -20,8 +20,10 @@ PAIR = 2 * P
 PAIRS = NODES // PAIR
 FLOPS = 2 * NODES * NODES * BATCH * CHAN + 2 * NODES * BATCH * CHAN * 2 * HID
 
-POOL_SHARE = 112
-DIRECT = (11, 12)
+POOL1 = 112
+POOL3 = 80
+DIRECT = (12,)
+HELP = (6, 8, 10, 12)
 
 
 def tile_stsgcm_pa_t_w8_kernel(tc, x, A_bytes, A_scale, W0_words, W0_scales, b0, out):
@@ -53,6 +55,8 @@ def tile_stsgcm_pa_t_w8_kernel(tc, x, A_bytes, A_scale, W0_words, W0_scales, b0,
         nc.vector.memset(w_scales[:].bitcast(I32), 0)
         ident = const.tile([P, P], F32, name="ident")
         make_identity(nc, ident[:])
+        ident16 = const.tile([P, P], BF16, name="ident16")
+        make_identity(nc, ident16[:])
 
         load_a(0)
         load_x(0, 0)
@@ -79,7 +83,7 @@ def tile_stsgcm_pa_t_w8_kernel(tc, x, A_bytes, A_scale, W0_words, W0_scales, b0,
         bias_row = const.tile([P, 2 * HID], BF16, name="bias_row")
         nc.sync.dma_start(out=bias_row[:], in_=b0.partition_broadcast(P))
 
-        x_il, x_q, a_wide, a_bank, a_il, a_q, g_bank, g_il, g_q, y_bank, gate, gated, o_bank, z = ({} for i in range(14))
+        x_il, x_q, a_wide, a_bank, a_il, a_q, g_bank, g_il, g_q, y_bank, gate, gated, o_bank, z, x_bank = ({} for i in range(15))
 
         def quantize(name, bufs, pool, src, cols):
             codes = pool.tile([P, cols], U32, name=name + "_codes", bufs=bufs, align_bytes=64)
@@ -94,32 +98,51 @@ def tile_stsgcm_pa_t_w8_kernel(tc, x, A_bytes, A_scale, W0_words, W0_scales, b0,
                 in_=x_raw[b, g][:].rearrange("p j (m i t) -> p m j t i", i=2, t=4),
             )
 
+        def interleave_tensor(b, g):
+            x_il[b, g] = work.tile([P, 4 * CHAN], BF16, name="x_il", bufs=4, align_bytes=64)
+            for half in range(2):
+                x_bank[b, g, half] = psum.tile([P, 2, CHAN], BF16, name="bank")
+                for t in range(2):
+                    nc.tensor.matmul(
+                        out=x_bank[b, g, half][:, t, :],
+                        lhsT=ident16[:],
+                        rhs=x_raw[b, g][:].rearrange("p j (m t) -> p t m j", t=4)[:, 2 * half + t],
+                        start=True,
+                        stop=True,
+                    )
+
+        def empty_x(b, g):
+            for half in range(2):
+                nc.scalar.copy(out=x_il[b, g][:, 2 * CHAN * half : 2 * CHAN * (half + 1)], in_=x_bank[b, g, half][:].rearrange("p t c -> p (t c)"))
+
         def quantize_x(b, g):
             x_q[b, g] = quantize("x", 8, work, x_il[b, g][:], CHAN)
 
-        def widen_a(q, k, copy):
-            a_wide[q, k] = work.tile([P, NODES], BF16, name="a_wide", bufs=4)
-            copy(out=a_wide[q, k][:], in_=a_raw[q][:, k, :].bitcast(FP8))
+        def widen_a(q, lo, hi, copy):
+            if q not in a_wide:
+                a_wide[q] = work.tile([P, 2, NODES], BF16, name="a_wide", bufs=2)
+            copy(out=a_wide[q][:, lo:hi, :].rearrange("p k w -> p (k w)"), in_=a_raw[q][:, lo:hi, :].rearrange("p k w -> p (k w)").bitcast(FP8))
 
         def turn_a(q):
             for g in range(2):
                 a_bank[q, g] = psum.tile([P, 2, PAIR], F32, name="bank")
                 for k in range(2):
-                    words = a_wide[q, k][:].bitcast(F32)
+                    words = a_wide[q][:, k, :].bitcast(F32)
                     for u in range(2):
                         nc.tensor.transpose(a_bank[q, g][:, u, P * k : P * (k + 1)], words[:, 256 * g + u : 256 * (g + 1) : 2], ident[:])
 
         def scale_a(q, g):
-            a_il[q, g] = work.tile([P, PAIR, 2, 2], BF16, name="a_il", bufs=4, align_bytes=64)
+            if q not in a_il:
+                a_il[q] = work.tile([P, 2, PAIR, 2, 2], BF16, name="a_il", bufs=2, align_bytes=64)
             nc.vector.tensor_tensor(
-                out=a_il[q, g][:],
+                out=a_il[q][:, g],
                 in0=a_bank[q, g][:].rearrange("p u v -> p (u v)").bitcast(BF16).rearrange("p (u v e) -> p v u e", u=2, e=2),
                 in1=a_scale[:, g, :].rearrange("p (u e) -> p u e", u=2).unsqueeze(1).to_broadcast([P, PAIR, 2, 2]),
                 op=MULT,
             )
 
-        def quantize_a(q, g):
-            a_q[q, g] = quantize("a%d_%d" % (q, g), 1, const, a_il[q, g][:].rearrange("p v u e -> p (v u e)"), PAIR)
+        def quantize_a(q):
+            a_q[q] = quantize("a%d" % q, 1, const, a_il[q][:].rearrange("p g v u e -> p (g v u e)"), 2 * PAIR)
 
         def aggregate(b, k0, n):
             for k in range(k0, k0 + n):
@@ -127,13 +150,13 @@ def tile_stsgcm_pa_t_w8_kernel(tc, x, A_bytes, A_scale, W0_words, W0_scales, b0,
             for t in range(4):
                 for g in range(2):
                     for k in range(k0, k0 + n):
-                        cols = slice(P * (k % 2), P * (k % 2 + 1))
+                        cols = slice(PAIR * g + P * (k % 2), PAIR * g + P * (k % 2 + 1))
                         nc.tensor.matmul_mx(
                             out=g_bank[b, k][:, t, :],
                             lhsT=x_q[b, g][0][:, P * t : P * (t + 1)].bitcast(FP8X4),
                             lhsT_scale=x_q[b, g][1][:, P * t : P * (t + 1)],
-                            rhs=a_q[k // 2, g][0][:, cols].bitcast(FP8X4),
-                            rhs_scale=a_q[k // 2, g][1][:, cols],
+                            rhs=a_q[k // 2][0][:, cols].bitcast(FP8X4),
+                            rhs_scale=a_q[k // 2][1][:, cols],
                             start=(g == 0),
                             stop=(g == 1),
                         )
@@ -235,54 +258,43 @@ def tile_stsgcm_pa_t_w8_kernel(tc, x, A_bytes, A_scale, W0_words, W0_scales, b0,
         vector, scalar = nc.vector.tensor_copy, nc.scalar.copy
         x_parts = [(b, g) for b in range(BATCH) for g in range(2)]
 
-        def widen_pair(q):
-            for k in range(2):
-                widen_a(q, k, scalar)
-
-        def prepare_a(q):
-            for g in range(2):
-                scale_a(q, g)
-            for g in range(2):
-                quantize_a(q, g)
-
         def empty_pair(b, k0, second):
             empty_g(b, k0, scalar)
             empty_g(b, k0 + 1, second)
 
-        widen_a(0, 0, scalar)
-        widen_a(0, 1, vector)
+        widen_a(0, 0, 1, scalar)
+        widen_a(0, 1, 2, vector)
         interleave_shared(0, 0, (vector, 0, P))
         turn_a(0)
-        widen_pair(1)
+        widen_a(1, 0, 2, scalar)
         turn_a(1)
         quantize_x(0, 0)
-        interleave_shared(0, 1, (pool, 0, POOL_SHARE))
+        interleave_shared(0, 1, (pool, 0, POOL1))
         scale_a(0, 0)
         scale_a(0, 1)
         scale_a(1, 0)
-        interleave_part(0, 1, POOL_SHARE, P, scalar)
-        widen_pair(2)
+        interleave_part(0, 1, POOL1, P, scalar)
+        interleave_tensor(1, 0)
+        widen_a(2, 0, 2, scalar)
+        empty_x(1, 0)
         turn_a(2)
-        quantize_a(0, 0)
-        quantize_a(0, 1)
         quantize_x(0, 1)
-        interleave_shared(1, 1, (pool, 0, POOL_SHARE))
+        quantize_a(0)
+        interleave_shared(1, 1, (pool, 0, P))
         aggregate(0, 0, 2)
-        widen_pair(3)
-        interleave_x(1, 0, scalar)
+        widen_a(3, 0, 2, scalar)
         scale_a(1, 1)
         scale_a(2, 0)
         scale_a(2, 1)
         turn_a(3)
-        for q in (1, 2):
-            for g in range(2):
-                quantize_a(q, g)
-        interleave_part(1, 1, POOL_SHARE, P, vector)
-        quantize_x(1, 0)
+        quantize_a(1)
         quantize_x(1, 1)
-        interleave_shared(2, 0, (pool, 0, P // 2))
+        quantize_a(2)
+        quantize_x(1, 0)
+        interleave_shared(2, 0, (pool, 0, POOL3))
         aggregate(0, 2, 2)
         empty_pair(0, 0, scalar)
+        interleave_x(2, 1, scalar)
         aggregate(0, 4, 2)
         scale_a(3, 0)
         scale_a(3, 1)
@@ -290,9 +302,8 @@ def tile_stsgcm_pa_t_w8_kernel(tc, x, A_bytes, A_scale, W0_words, W0_scales, b0,
         empty_pair(0, 2, scalar)
         empty_pair(0, 4, scalar)
         quantize_g(0, 0, 4)
-        quantize_a(3, 0)
-        quantize_a(3, 1)
-        interleave_part(2, 0, P // 2, P, vector)
+        quantize_a(3)
+        interleave_part(2, 0, POOL3, P, vector)
         aggregate(1, 2, 2)
         empty_pair(1, 0, scalar)
         project(0, 0, 4)
@@ -304,14 +315,13 @@ def tile_stsgcm_pa_t_w8_kernel(tc, x, A_bytes, A_scale, W0_words, W0_scales, b0,
         multiply(0, 0, 4)
         aggregate(1, 4, 2)
         empty_pair(0, 6, scalar)
-        interleave_x(2, 1, vector)
         project(1, 0, 4)
         aggregate(1, 6, 2)
         sigmoid(1, 0, 4)
         empty_pair(1, 4, scalar)
+        quantize_x(2, 1)
         quantize_g(0, 4, 4)
         multiply(1, 0, 4)
-        quantize_x(2, 1)
         interleave_x(3, 0, vector)
         empty_pair(1, 6, scalar)
         project(0, 4, 4)
@@ -339,7 +349,7 @@ def tile_stsgcm_pa_t_w8_kernel(tc, x, A_bytes, A_scale, W0_words, W0_scales, b0,
                 sigmoid_direct(old[0], old[1] + 2)
             else:
                 multiply(*old)
-            empty_pair(b, k0, helper)
+            empty_pair(b, k0, vector if h in HELP else helper)
             aggregate(b, k0 + 2, 2)
             if h + 3 < len(x_parts):
                 interleave_x(*x_parts[h + 3], vector)

@@ -23,7 +23,7 @@ FLOPS = 2 * NODES * NODES * BATCH * CHAN + 2 * NODES * BATCH * CHAN * 2 * HID
 POOL1 = 112
 POOL3 = 80
 DIRECT = (12,)
-HELP = (6, 8, 10, 12)
+HELP = (4, 6, 8, 10, 12)
 
 
 def tile_stsgcm_pa_t_w8_kernel(tc, x, A_bytes, A_scale, W0_words, W0_scales, b0, out):
@@ -106,14 +106,17 @@ def tile_stsgcm_pa_t_w8_kernel(tc, x, A_bytes, A_scale, W0_words, W0_scales, b0,
                     nc.tensor.matmul(
                         out=x_bank[b, g, half][:, t, :],
                         lhsT=ident16[:],
-                        rhs=x_raw[b, g][:].rearrange("p j (m t) -> p t m j", t=4)[:, 2 * half + t],
+                        rhs=x_raw[b, g][:, :, P * (2 * half + t) : P * (2 * half + t + 1)].rearrange("p j c -> p c j"),
                         start=True,
                         stop=True,
                     )
 
         def empty_x(b, g):
             for half in range(2):
-                nc.scalar.copy(out=x_il[b, g][:, 2 * CHAN * half : 2 * CHAN * (half + 1)], in_=x_bank[b, g, half][:].rearrange("p t c -> p (t c)"))
+                nc.scalar.copy(
+                    out=x_il[b, g][:].rearrange("p (t m j) -> p t m j", t=4, j=4)[:, :, 64 * half : 64 * (half + 1), :],
+                    in_=x_bank[b, g, half][:].rearrange("p s (m t j) -> p t (s m) j", t=4, j=4),
+                )
 
         def quantize_x(b, g):
             x_q[b, g] = quantize("x", 8, work, x_il[b, g][:], CHAN)
@@ -147,9 +150,9 @@ def tile_stsgcm_pa_t_w8_kernel(tc, x, A_bytes, A_scale, W0_words, W0_scales, b0,
         def aggregate(b, k0, n):
             for k in range(k0, k0 + n):
                 g_bank[b, k] = psum.tile([P, 4, P], F32, name="bank")
-            for t in range(4):
-                for g in range(2):
-                    for k in range(k0, k0 + n):
+            for k in range(k0, k0 + n):
+                for t in range(4):
+                    for g in range(2):
                         cols = slice(PAIR * g + P * (k % 2), PAIR * g + P * (k % 2 + 1))
                         nc.tensor.matmul_mx(
                             out=g_bank[b, k][:, t, :],
@@ -205,11 +208,12 @@ def tile_stsgcm_pa_t_w8_kernel(tc, x, A_bytes, A_scale, W0_words, W0_scales, b0,
 
         def project_direct(b, k0, n):
             for k in range(k0, k0 + n):
-                if k % 2 == 0:
-                    y_bank[b, k] = psum.tile([P, 2, 2 * HID], F32, name="bank")
+                first = k - (k - k0) % 2
+                if k == first:
+                    y_bank[b, k] = psum.tile([P, min(n, 2), 2 * HID], F32, name="bank")
                 cols = slice(P * (k - k0), P * (k - k0 + 1))
                 nc.tensor.matmul_mx(
-                    out=y_bank[b, k - k % 2][:, k % 2, :],
+                    out=y_bank[b, first][:, k - first, :],
                     lhsT=g_q[b, k0][0][:, cols].bitcast(FP8X4),
                     lhsT_scale=g_q[b, k0][1][:, cols],
                     rhs=w_words[:].bitcast(FP8X4),
@@ -218,18 +222,30 @@ def tile_stsgcm_pa_t_w8_kernel(tc, x, A_bytes, A_scale, W0_words, W0_scales, b0,
                     stop=True,
                 )
 
-        def add_bias(b, k):
-            z[b, k] = work.tile([P, 2, 2 * HID], F32, name="z")
-            nc.vector.tensor_tensor(out=z[b, k][:], in0=y_bank[b, k][:], in1=bias_row[:].unsqueeze(1).to_broadcast([P, 2, 2 * HID]), op=ADD)
+        def add_bias(b, k, n=2):
+            z[b, k] = work.tile([P, n, 2 * HID], F32, name="z")
+            nc.vector.tensor_tensor(out=z[b, k][:], in0=y_bank[b, k][:], in1=bias_row[:].unsqueeze(1).to_broadcast([P, n, 2 * HID]), op=ADD)
 
-        def sigmoid_direct(b, k):
-            gate[b, k] = work.tile([P, 2, HID], F32, name="gate", bufs=6)
+        def sigmoid_direct(b, k, n=2):
+            gate[b, k] = work.tile([P, n, HID], F32, name="gate", bufs=6)
             nc.scalar.activation(out=gate[b, k][:], in_=z[b, k][:, :, HID:], func=ACT.Sigmoid)
 
-        def store_direct(b, k):
-            rows = work.tile([P, 2, HID], F32, name="rows", bufs=6)
+        def store_direct(b, k, n=2):
+            rows = work.tile([P, n, HID], F32, name="rows", bufs=6)
             nc.vector.tensor_tensor(out=rows[:], in0=z[b, k][:, :, :HID], in1=gate[b, k][:], op=MULT)
-            nc.sync.dma_start(out=out_view[b][:, k : k + 2, :], in_=rows[:])
+            nc.sync.dma_start(out=out_view[b][:, k : k + n, :], in_=rows[:])
+
+        def quantize_g_half(b, k0, half):
+            if half == 0:
+                codes = work.tile([P, 4 * P], U32, name="g4_codes", bufs=3, align_bytes=64)
+                scales = work.tile([P, 4 * P], U8, name="g4_scales", bufs=3, align_bytes=64)
+                g_q[b, k0] = codes, scales
+            cols = slice(PAIR * half, PAIR * (half + 1))
+            nc.vector.quantize_mx(
+                out=g_q[b, k0][0][:, cols].bitcast(FP8X4),
+                scales=g_q[b, k0][1][:, cols],
+                in_=g_il[b, k0 // 4][:, 2 * half : 2 * half + 2, :, :].rearrange("p k v t -> p (k v t)"),
+            )
 
         pool = "pool"
 
@@ -327,10 +343,9 @@ def tile_stsgcm_pa_t_w8_kernel(tc, x, A_bytes, A_scale, W0_words, W0_scales, b0,
         project(0, 4, 4)
         turn_out(0, 0, 4)
         turn_out(1, 0, 4)
-        for h in range(4, last):
+        for h in range(4, last - 1):
             b, k0, n = groups[h]
             old = groups[h - 2]
-            helper = vector if h == last - 1 else scalar
             aggregate(b, k0, 2)
             if h - 2 in DIRECT:
                 add_bias(old[0], old[1])
@@ -349,29 +364,44 @@ def tile_stsgcm_pa_t_w8_kernel(tc, x, A_bytes, A_scale, W0_words, W0_scales, b0,
                 sigmoid_direct(old[0], old[1] + 2)
             else:
                 multiply(*old)
-            empty_pair(b, k0, vector if h in HELP else helper)
+            empty_pair(b, k0, vector if h in HELP else scalar)
             aggregate(b, k0 + 2, 2)
             if h + 3 < len(x_parts):
                 interleave_x(*x_parts[h + 3], vector)
             if h - 2 in DIRECT:
                 store_direct(old[0], old[1])
                 store_direct(old[0], old[1] + 2)
-            empty_pair(b, k0 + 2, helper)
+            empty_pair(b, k0 + 2, scalar)
             (project_direct if h - 1 in DIRECT else project)(*groups[h - 1])
             if h % 2 == 1:
                 for i in (h - 3, h - 2):
                     if i not in DIRECT:
                         turn_out(*groups[i])
         b = BATCH - 1
+        aggregate(b, 0, 2)
+        add_bias(b - 1, 0)
+        add_bias(b - 1, 2)
+        quantize_g(b - 1, 4, 4)
+        store(b - 2, 0, 4, scalar)
+        store(b - 2, 4, 4, scalar)
+        empty_g(b, 0, vector)
+        sigmoid_direct(b - 1, 0)
+        sigmoid_direct(b - 1, 2)
+        empty_g(b, 1, scalar)
+        aggregate(b, 2, 2)
+        store_direct(b - 1, 0)
+        store_direct(b - 1, 2)
+        quantize_g_half(b, 0, 0)
+        empty_pair(b, 2, vector)
+        project(b - 1, 4, 4)
         aggregate(b, 4, 2)
-        quantize_g(b, 0, 4)
+        quantize_g_half(b, 0, 1)
         sigmoid(b - 1, 4, 4)
         empty_g(b, 4, scalar)
         project(b, 0, 4)
         multiply(b - 1, 4, 4)
         empty_g(b, 5, vector)
-        aggregate(b, 6, 1)
-        aggregate(b, 7, 1)
+        aggregate(b, 6, 2)
         sigmoid(b, 0, 4)
         quantize_g(b, 4, 2)
         empty_g(b, 6, scalar)

@@ -17,13 +17,14 @@ ACT = mybir.ActivationFunctionType
 NODES, BATCH, CHAN, HID = 1024, 8, 512, 128
 P = 128
 PAIR = 2 * P
-PAIRS = NODES // PAIR
+PASS = 4 * P
 FLOPS = 2 * NODES * NODES * BATCH * CHAN + 2 * NODES * BATCH * CHAN * 2 * HID
 
-POOL1 = 112
-POOL3 = 80
-DIRECT = (12,)
-HELP = (4, 6, 8, 10, 12)
+HEAD_POOL = 80
+POOL = 64
+SHARE = 16
+G_BUFS = 5
+HEAD_SHARE = 48
 
 
 def tile_stsgcm_pa_t_w8_kernel(tc, x, A_bytes, A_scale, W0_words, W0_scales, b0, out):
@@ -37,53 +38,21 @@ def tile_stsgcm_pa_t_w8_kernel(tc, x, A_bytes, A_scale, W0_words, W0_scales, b0,
         x_view = x.rearrange("(g p j) b c -> g b p j c", p=P, j=4)
         a_view = A_bytes.rearrange("(k p) w -> p k w", p=P)
         out_view = out.rearrange("(k p) b j -> b p k j", p=P)
+        vector, scalar = nc.vector.tensor_copy, nc.scalar.copy
 
-        x_raw, a_raw = {}, {}
+        x_raw, a_raw, x_il, x_q, a_val, a_bank, a_il, a_q = ({} for i in range(8))
+        g_bank, g_il, g_q, y_bank, gate, gated, o_bank, z = ({} for i in range(8))
 
         def load_x(b, g):
-            x_raw[b, g] = const.tile([P, 4, CHAN], BF16, name="x_raw%d_%d" % (b, g))
+            if (b, g) == (0, 0):
+                x_raw[b, g] = work.tile([P, 4, CHAN], BF16, name="x_il_shared", bufs=1, align_bytes=64)
+            else:
+                x_raw[b, g] = const.tile([P, 4, CHAN], BF16, name="x_raw%d_%d" % (b, g))
             nc.sync.dma_start(out=x_raw[b, g][:], in_=x_view[g][b])
 
         def load_a(q):
             a_raw[q] = const.tile([P, 2, NODES], U8, name="a_raw%d" % q)
             nc.sync.dma_start(out=a_raw[q][:], in_=a_view[:, 2 * q : 2 * q + 2, :])
-
-        warm = const.tile([P, 1], F32, name="warm")
-        nc.vector.memset(warm[:], 0.0)
-        nc.scalar.activation(out=warm[:], in_=warm[:], func=ACT.Sigmoid)
-        w_scales = const.tile([P, 2 * HID], U8, name="w_scales", align_bytes=64)
-        nc.vector.memset(w_scales[:].bitcast(I32), 0)
-        ident = const.tile([P, P], F32, name="ident")
-        make_identity(nc, ident[:])
-        ident16 = const.tile([P, P], BF16, name="ident16")
-        make_identity(nc, ident16[:])
-
-        load_a(0)
-        load_x(0, 0)
-        a_scale = const.tile([P, 2, 4], F32, name="a_scale")
-        with nc.allow_non_contiguous_dma(reason="four scales a partition and pass"):
-            nc.sync.dma_start(out=a_scale[:], in_=A_scale.rearrange("o (g p t) -> (o p) g t", p=P, t=4))
-        load_a(1)
-        load_x(0, 1)
-        load_x(1, 0)
-        load_a(2)
-        load_x(1, 1)
-        load_a(3)
-        w_words = const.tile([P, 2 * HID], U32, name="w_words", align_bytes=64)
-        nc.sync.dma_start(out=w_words[:].bitcast(I32), in_=W0_words.rearrange("o p n t -> (o p) (n t)").bitcast(I32))
-        ws_view = W0_scales.rearrange("o q n -> (o q) n").bitcast(I32)
-        for r in range(4):
-            nc.sync.dma_start(out=w_scales[32 * r : 32 * r + 4, :].bitcast(I32), in_=ws_view[4 * r : 4 * r + 4, :])
-        bias_col = const.tile([P, 2], BF16, name="bias_col")
-        with nc.allow_non_contiguous_dma(reason="one bias value a partition"):
-            nc.sync.dma_start(out=bias_col[:], in_=b0.rearrange("(o p) -> p o", p=P))
-        for b in range(2, BATCH):
-            for g in range(2):
-                load_x(b, g)
-        bias_row = const.tile([P, 2 * HID], BF16, name="bias_row")
-        nc.sync.dma_start(out=bias_row[:], in_=b0.partition_broadcast(P))
-
-        x_il, x_q, a_wide, a_bank, a_il, a_q, g_bank, g_il, g_q, y_bank, gate, gated, o_bank, z, x_bank = ({} for i in range(15))
 
         def quantize(name, bufs, pool, src, cols):
             codes = pool.tile([P, cols], U32, name=name + "_codes", bufs=bufs, align_bytes=64)
@@ -91,69 +60,53 @@ def tile_stsgcm_pa_t_w8_kernel(tc, x, A_bytes, A_scale, W0_words, W0_scales, b0,
             nc.vector.quantize_mx(out=codes[:].bitcast(FP8X4), scales=scales[:], in_=src)
             return codes, scales
 
-        def interleave_x(b, g, copy):
-            x_il[b, g] = work.tile([P, 4 * CHAN], BF16, name="x_il", bufs=4, align_bytes=64)
-            copy(
-                out=x_il[b, g][:].rearrange("p (t m i j) -> p m j t i", t=4, i=2, j=4),
-                in_=x_raw[b, g][:].rearrange("p j (m i t) -> p m j t i", i=2, t=4),
-            )
+        def pool_copy(out, in_):
+            nc.gpsimd.tensor_scalar(out=out, in0=in_, scalar1=1.0, scalar2=0.0, op0=MULT, op1=ADD)
 
-        def interleave_tensor(b, g):
-            x_il[b, g] = work.tile([P, 4 * CHAN], BF16, name="x_il", bufs=4, align_bytes=64)
-            for half in range(2):
-                x_bank[b, g, half] = psum.tile([P, 2, CHAN], BF16, name="bank")
-                for t in range(2):
-                    nc.tensor.matmul(
-                        out=x_bank[b, g, half][:, t, :],
-                        lhsT=ident16[:],
-                        rhs=x_raw[b, g][:, :, P * (2 * half + t) : P * (2 * half + t + 1)].rearrange("p j c -> p c j"),
-                        start=True,
-                        stop=True,
-                    )
+        def new_il(b, g, name="x_il", bufs=3):
+            x_il[b, g] = work.tile([P, 4 * CHAN], BF16, name=name, bufs=bufs, align_bytes=64)
 
-        def empty_x(b, g):
-            for half in range(2):
-                nc.scalar.copy(
-                    out=x_il[b, g][:].rearrange("p (t m j) -> p t m j", t=4, j=4)[:, :, 64 * half : 64 * (half + 1), :],
-                    in_=x_bank[b, g, half][:].rearrange("p s (m t j) -> p t (s m) j", t=4, j=4),
-                )
+        def interleave(b, g, lo, hi, copy):
+            dst = x_il[b, g][:].rearrange("p (t m j) -> p t m j", t=4, j=4)[:, :, lo:hi, :]
+            src = x_raw[b, g][:, :, 4 * lo : 4 * hi]
+            if copy is pool_copy:
+                copy(out=dst.rearrange("p t m j -> p m t j"), in_=src.rearrange("p j (m t) -> p m t j", t=4))
+            else:
+                copy(out=dst.rearrange("p t (m i) j -> p m j t i", i=2), in_=src.rearrange("p j (m i t) -> p m j t i", i=2, t=4))
 
         def quantize_x(b, g):
             x_q[b, g] = quantize("x", 8, work, x_il[b, g][:], CHAN)
 
-        def widen_a(q, lo, hi, copy):
-            if q not in a_wide:
-                a_wide[q] = work.tile([P, 2, NODES], BF16, name="a_wide", bufs=2)
-            copy(out=a_wide[q][:, lo:hi, :].rearrange("p k w -> p (k w)"), in_=a_raw[q][:, lo:hi, :].rearrange("p k w -> p (k w)").bitcast(FP8))
+        def widen_a(k, copy):
+            a_val[k] = work.tile([P, NODES], BF16, name="a_val", bufs=3)
+            copy(out=a_val[k][:], in_=a_raw[k // 2][:, k % 2, :].bitcast(FP8))
 
-        def turn_a(q):
+        def turn_a(k):
+            a_bank[k] = psum.tile([P, 2, 2, P], F32, name="bank")
+            words = a_val[k][:].bitcast(F32)
             for g in range(2):
-                a_bank[q, g] = psum.tile([P, 2, PAIR], F32, name="bank")
-                for k in range(2):
-                    words = a_wide[q][:, k, :].bitcast(F32)
-                    for u in range(2):
-                        nc.tensor.transpose(a_bank[q, g][:, u, P * k : P * (k + 1)], words[:, 256 * g + u : 256 * (g + 1) : 2], ident[:])
+                for u in range(2):
+                    nc.tensor.transpose(a_bank[k][:, u, g, :], words[:, 256 * g + u : 256 * (g + 1) : 2], ident[:])
 
-        def scale_a(q, g):
-            if q not in a_il:
-                a_il[q] = work.tile([P, 2, PAIR, 2, 2], BF16, name="a_il", bufs=2, align_bytes=64)
+        def scale_a(k):
+            if k // 2 not in a_il:
+                a_il[k // 2] = work.tile([P, 2, 2, P, 2, 2], BF16, name="a_il", bufs=2, align_bytes=64)
             nc.vector.tensor_tensor(
-                out=a_il[q][:, g],
-                in0=a_bank[q, g][:].rearrange("p u v -> p (u v)").bitcast(BF16).rearrange("p (u v e) -> p v u e", u=2, e=2),
-                in1=a_scale[:, g, :].rearrange("p (u e) -> p u e", u=2).unsqueeze(1).to_broadcast([P, PAIR, 2, 2]),
+                out=a_il[k // 2][:, k % 2],
+                in0=a_bank[k][:].rearrange("p u g v -> p (u g v)").bitcast(BF16).rearrange("p (u g v e) -> p g v u e", u=2, g=2, e=2),
+                in1=a_scale[:].rearrange("p g (u e) -> p g u e", u=2).unsqueeze(2).to_broadcast([P, 2, P, 2, 2]),
                 op=MULT,
             )
 
         def quantize_a(q):
-            a_q[q] = quantize("a%d" % q, 1, const, a_il[q][:].rearrange("p g v u e -> p (g v u e)"), 2 * PAIR)
+            a_q[q] = quantize("a%d" % q, 1, const, a_il[q][:].rearrange("p k g v u e -> p (k g v u e)"), 2 * PAIR)
 
         def aggregate(b, k0, n):
             for k in range(k0, k0 + n):
                 g_bank[b, k] = psum.tile([P, 4, P], F32, name="bank")
-            for k in range(k0, k0 + n):
                 for t in range(4):
                     for g in range(2):
-                        cols = slice(PAIR * g + P * (k % 2), PAIR * g + P * (k % 2 + 1))
+                        cols = slice(PAIR * (k % 2) + P * g, PAIR * (k % 2) + P * (g + 1))
                         nc.tensor.matmul_mx(
                             out=g_bank[b, k][:, t, :],
                             lhsT=x_q[b, g][0][:, P * t : P * (t + 1)].bitcast(FP8X4),
@@ -166,12 +119,12 @@ def tile_stsgcm_pa_t_w8_kernel(tc, x, A_bytes, A_scale, W0_words, W0_scales, b0,
 
         def empty_g(b, k, copy):
             if (b, k // 4) not in g_il:
-                g_il[b, k // 4] = work.tile([P, 4, P, 4], BF16, name="g_il", bufs=4, align_bytes=64)
+                g_il[b, k // 4] = work.tile([P, 4, P, 4], BF16, name="g_il", bufs=G_BUFS, align_bytes=64)
             copy(out=g_il[b, k // 4][:, k % 4, :, :], in_=g_bank[b, k][:].rearrange("p t v -> p v t"))
 
         def quantize_g(b, k0, n):
             src = g_il[b, k0 // 4][:, k0 % 4 : k0 % 4 + n, :, :]
-            g_q[b, k0] = quantize("g%d" % n, 3, work, src.rearrange("p k v t -> p (k v t)"), n * P)
+            g_q[b, k0] = quantize("g%d" % n, 6 if n == 4 else 3, work, src.rearrange("p k v t -> p (k v t)"), n * P)
 
         def project(b, k0, n):
             for half in (1, 0):
@@ -187,7 +140,7 @@ def tile_stsgcm_pa_t_w8_kernel(tc, x, A_bytes, A_scale, W0_words, W0_scales, b0,
                 )
 
         def sigmoid(b, k0, n):
-            gate[b, k0] = work.tile([P, n * P], F32, name="gate", bufs=6)
+            gate[b, k0] = work.tile([P, n * P], F32, name="gate", bufs=5)
             nc.scalar.activation(out=gate[b, k0][:], in_=y_bank[b, k0, 1][:], func=ACT.Sigmoid, bias=bias_col[:, 1:2])
 
         def multiply(b, k0, n):
@@ -207,224 +160,268 @@ def tile_stsgcm_pa_t_w8_kernel(tc, x, A_bytes, A_scale, W0_words, W0_scales, b0,
             nc.sync.dma_start(out=out_view[b][:, k0 : k0 + n, :], in_=rows[:])
 
         def project_direct(b, k0, n):
-            for k in range(k0, k0 + n):
-                first = k - (k - k0) % 2
-                if k == first:
-                    y_bank[b, k] = psum.tile([P, min(n, 2), 2 * HID], F32, name="bank")
-                cols = slice(P * (k - k0), P * (k - k0 + 1))
-                nc.tensor.matmul_mx(
-                    out=y_bank[b, first][:, k - first, :],
-                    lhsT=g_q[b, k0][0][:, cols].bitcast(FP8X4),
-                    lhsT_scale=g_q[b, k0][1][:, cols],
-                    rhs=w_words[:].bitcast(FP8X4),
-                    rhs_scale=w_scales[:],
-                    start=True,
-                    stop=True,
+            for first in range(k0, k0 + n, 2):
+                y_bank[b, first] = psum.tile([P, min(n, 2), 2 * HID], F32, name="bank")
+                for k in range(first, first + min(n, 2)):
+                    cols = slice(P * (k - k0), P * (k - k0 + 1))
+                    nc.tensor.matmul_mx(
+                        out=y_bank[b, first][:, k - first, :],
+                        lhsT=g_q[b, k0][0][:, cols].bitcast(FP8X4),
+                        lhsT_scale=g_q[b, k0][1][:, cols],
+                        rhs=w_words[:].bitcast(FP8X4),
+                        rhs_scale=w_scales[:],
+                        start=True,
+                        stop=True,
+                    )
+
+        def add_bias(b, k0, n):
+            z[b, k0] = work.tile([P, n, 2 * HID], F32, name="z%d" % n, bufs=2 if n == 4 else 4)
+            for first in range(k0, k0 + n, 2):
+                m = min(n, 2)
+                nc.vector.tensor_tensor(
+                    out=z[b, k0][:, first - k0 : first - k0 + m, :],
+                    in0=y_bank[b, first][:],
+                    in1=bias_row[:].unsqueeze(1).to_broadcast([P, m, 2 * HID]),
+                    op=ADD,
                 )
 
-        def add_bias(b, k, n=2):
-            z[b, k] = work.tile([P, n, 2 * HID], F32, name="z")
-            nc.vector.tensor_tensor(out=z[b, k][:], in0=y_bank[b, k][:], in1=bias_row[:].unsqueeze(1).to_broadcast([P, n, 2 * HID]), op=ADD)
+        def sigmoid_direct(b, k0, n):
+            gate[b, k0] = work.tile([P, n, HID], F32, name="gate", bufs=5)
+            nc.scalar.activation(out=gate[b, k0][:], in_=z[b, k0][:, :, HID:], func=ACT.Sigmoid)
 
-        def sigmoid_direct(b, k, n=2):
-            gate[b, k] = work.tile([P, n, HID], F32, name="gate", bufs=6)
-            nc.scalar.activation(out=gate[b, k][:], in_=z[b, k][:, :, HID:], func=ACT.Sigmoid)
-
-        def store_direct(b, k, n=2):
+        def store_direct(b, k0, n):
             rows = work.tile([P, n, HID], F32, name="rows", bufs=6)
-            nc.vector.tensor_tensor(out=rows[:], in0=z[b, k][:, :, :HID], in1=gate[b, k][:], op=MULT)
-            nc.sync.dma_start(out=out_view[b][:, k : k + n, :], in_=rows[:])
+            nc.vector.tensor_tensor(out=rows[:], in0=z[b, k0][:, :, :HID], in1=gate[b, k0][:], op=MULT)
+            nc.sync.dma_start(out=out_view[b][:, k0 : k0 + n, :], in_=rows[:])
 
-        def quantize_g_half(b, k0, half):
-            if half == 0:
-                codes = work.tile([P, 4 * P], U32, name="g4_codes", bufs=3, align_bytes=64)
-                scales = work.tile([P, 4 * P], U8, name="g4_scales", bufs=3, align_bytes=64)
-                g_q[b, k0] = codes, scales
-            cols = slice(PAIR * half, PAIR * (half + 1))
-            nc.vector.quantize_mx(
-                out=g_q[b, k0][0][:, cols].bitcast(FP8X4),
-                scales=g_q[b, k0][1][:, cols],
-                in_=g_il[b, k0 // 4][:, 2 * half : 2 * half + 2, :, :].rearrange("p k v t -> p (k v t)"),
-            )
+        warm = const.tile([P, 1], F32, name="warm")
+        nc.vector.memset(warm[:], 0.0)
+        nc.scalar.activation(out=warm[:], in_=warm[:], func=ACT.Sigmoid)
+        w_scales = const.tile([P, 2 * HID], U8, name="w_scales", align_bytes=64)
+        nc.vector.memset(w_scales[:].bitcast(I32), 0)
+        ident = const.tile([P, P], F32, name="ident")
+        make_identity(nc, ident[:])
+        a_scale = const.tile([P, 2, 4], F32, name="a_scale")
+        w_words = const.tile([P, 2 * HID], U32, name="w_words", align_bytes=64)
+        bias_col = const.tile([P, 2], BF16, name="bias_col")
+        bias_row = const.tile([P, 2 * HID], BF16, name="bias_row")
 
-        pool = "pool"
+        def load_scale():
+            with nc.allow_non_contiguous_dma(reason="four scales a partition and pass"):
+                nc.sync.dma_start(out=a_scale[:], in_=A_scale.rearrange("o (g p t) -> (o p) g t", p=P, t=4))
 
-        def interleave_part(b, g, lo, hi, engine):
-            dst = x_il[b, g][:].rearrange("p (t m j) -> p t m j", t=4, j=4)[:, :, lo:hi, :]
-            src = x_raw[b, g][:, :, 4 * lo : 4 * hi]
-            if engine is pool:
-                nc.gpsimd.tensor_scalar(
-                    out=dst.rearrange("p t m j -> p m t j"),
-                    in0=src.rearrange("p j (m t) -> p m t j", t=4),
-                    scalar1=1.0,
-                    scalar2=0.0,
-                    op0=MULT,
-                    op1=ADD,
-                )
-            else:
-                engine(out=dst.rearrange("p t (m i) j -> p m j t i", i=2), in_=src.rearrange("p j (m i t) -> p m j t i", i=2, t=4))
+        def load_w():
+            nc.sync.dma_start(out=w_words[:].bitcast(I32), in_=W0_words.rearrange("o p n t -> (o p) (n t)").bitcast(I32))
+            ws_view = W0_scales.rearrange("o q n -> (o q) n").bitcast(I32)
+            for r in range(4):
+                nc.sync.dma_start(out=w_scales[32 * r : 32 * r + 4, :].bitcast(I32), in_=ws_view[4 * r : 4 * r + 4, :])
+            with nc.allow_non_contiguous_dma(reason="one bias value a partition"):
+                nc.sync.dma_start(out=bias_col[:], in_=b0.rearrange("(o p) -> p o", p=P))
 
-        def interleave_shared(b, g, *shares):
-            x_il[b, g] = work.tile([P, 4 * CHAN], BF16, name="x_il_shared", bufs=1, align_bytes=64)
-            for engine, lo, hi in shares:
-                interleave_part(b, g, lo, hi, engine)
+        def load_bias_row():
+            nc.sync.dma_start(out=bias_row[:], in_=b0.partition_broadcast(P))
 
-        groups = [(b, k0, 4) for k0 in (0, 4) for b in range(2)] + [(b, k0, 4) for b in range(2, BATCH) for k0 in (0, 4)]
-        last = len(groups) - 1
-        vector, scalar = nc.vector.tensor_copy, nc.scalar.copy
-        x_parts = [(b, g) for b in range(BATCH) for g in range(2)]
+        load_a(0)
+        load_x(0, 0)
+        load_scale()
+        load_a(1)
+        load_x(0, 1)
+        load_x(1, 0)
+        load_a(2)
+        load_x(1, 1)
+        load_a(3)
+        load_x(2, 0)
+        load_x(2, 1)
+        load_w()
+        for b in range(3, BATCH):
+            for g in range(2):
+                load_x(b, g)
+        load_bias_row()
 
-        def empty_pair(b, k0, second):
-            empty_g(b, k0, scalar)
-            empty_g(b, k0 + 1, second)
+        def shared(b, g, cut):
+            new_il(b, g, "x_il_shared", 1)
+            interleave(b, g, 0, cut, pool_copy)
 
-        widen_a(0, 0, 1, scalar)
-        widen_a(0, 1, 2, vector)
-        interleave_shared(0, 0, (vector, 0, P))
+        widen_a(0, scalar)
+        widen_a(1, vector)
+        new_il(0, 0)
+        interleave(0, 0, 0, P, vector)
+        shared(0, 1, HEAD_POOL)
         turn_a(0)
-        widen_a(1, 0, 2, scalar)
         turn_a(1)
+        widen_a(2, scalar)
         quantize_x(0, 0)
-        interleave_shared(0, 1, (pool, 0, POOL1))
-        scale_a(0, 0)
-        scale_a(0, 1)
-        scale_a(1, 0)
-        interleave_part(0, 1, POOL1, P, scalar)
-        interleave_tensor(1, 0)
-        widen_a(2, 0, 2, scalar)
-        empty_x(1, 0)
+        scale_a(0)
+        scale_a(1)
+        interleave(0, 1, HEAD_POOL, P, scalar)
         turn_a(2)
-        quantize_x(0, 1)
-        quantize_a(0)
-        interleave_shared(1, 1, (pool, 0, P))
-        aggregate(0, 0, 2)
-        widen_a(3, 0, 2, scalar)
-        scale_a(1, 1)
-        scale_a(2, 0)
-        scale_a(2, 1)
+        widen_a(3, scalar)
         turn_a(3)
-        quantize_a(1)
-        quantize_x(1, 1)
-        quantize_a(2)
+        widen_a(4, scalar)
+        turn_a(4)
+        widen_a(5, scalar)
+        quantize_x(0, 1)
+        shared(1, 0, HEAD_POOL)
+        quantize_a(0)
+        scale_a(2)
+        scale_a(3)
+        interleave(1, 0, HEAD_POOL, P, scalar)
+        widen_a(6, scalar)
+        aggregate(0, 0, 2)
+        turn_a(5)
+        turn_a(6)
+        widen_a(7, scalar)
         quantize_x(1, 0)
-        interleave_shared(2, 0, (pool, 0, POOL3))
+        shared(1, 1, HEAD_POOL)
+        quantize_a(1)
+        scale_a(4)
+        scale_a(5)
+        interleave(1, 1, HEAD_POOL, P, scalar)
         aggregate(0, 2, 2)
-        empty_pair(0, 0, scalar)
-        interleave_x(2, 1, scalar)
-        aggregate(0, 4, 2)
-        scale_a(3, 0)
-        scale_a(3, 1)
+        turn_a(7)
+        for k in range(4):
+            empty_g(0, k, scalar)
+        quantize_x(1, 1)
+        shared(2, 0, HEAD_POOL)
+        quantize_a(2)
+        scale_a(6)
+        scale_a(7)
         aggregate(1, 0, 2)
-        empty_pair(0, 2, scalar)
-        empty_pair(0, 4, scalar)
-        quantize_g(0, 0, 4)
-        quantize_a(3)
-        interleave_part(2, 0, POOL3, P, vector)
+        interleave(2, 0, HEAD_POOL, P, scalar)
         aggregate(1, 2, 2)
-        empty_pair(1, 0, scalar)
-        project(0, 0, 4)
-        aggregate(0, 6, 2)
-        empty_pair(1, 2, vector)
-        sigmoid(0, 0, 4)
+        empty_g(1, 0, scalar)
+        empty_g(1, 1, scalar)
         quantize_x(2, 0)
-        quantize_g(1, 0, 4)
-        multiply(0, 0, 4)
+        quantize_a(3)
+        aggregate(0, 4, 2)
+        empty_g(1, 2, scalar)
+        empty_g(1, 3, scalar)
+        quantize_g(0, 0, 4)
+        new_il(2, 1, "x_il_shared", 1)
+        interleave(2, 1, 0, P, vector)
         aggregate(1, 4, 2)
-        empty_pair(0, 6, scalar)
-        project(1, 0, 4)
-        aggregate(1, 6, 2)
-        sigmoid(1, 0, 4)
-        empty_pair(1, 4, scalar)
+        empty_g(0, 4, scalar)
+        empty_g(0, 5, scalar)
+        quantize_g(1, 0, 4)
         quantize_x(2, 1)
-        quantize_g(0, 4, 4)
+        shared(3, 1, POOL)
+        aggregate(0, 6, 2)
+        project(0, 0, 4)
+        empty_g(1, 4, scalar)
+        empty_g(1, 5, scalar)
+        new_il(3, 0)
+        interleave(3, 0, 0, HEAD_SHARE, scalar)
+        interleave(3, 0, HEAD_SHARE, P, vector)
+        sigmoid(0, 0, 4)
+        aggregate(1, 6, 2)
+        project(1, 0, 4)
+        empty_g(0, 6, scalar)
+        empty_g(0, 7, scalar)
+        multiply(0, 0, 4)
+        empty_g(1, 6, vector)
+        sigmoid(1, 0, 4)
         multiply(1, 0, 4)
-        interleave_x(3, 0, vector)
-        empty_pair(1, 6, scalar)
-        project(0, 4, 4)
-        turn_out(0, 0, 4)
-        turn_out(1, 0, 4)
-        for h in range(4, last - 1):
-            b, k0, n = groups[h]
-            old = groups[h - 2]
-            aggregate(b, k0, 2)
-            if h - 2 in DIRECT:
-                add_bias(old[0], old[1])
-                add_bias(old[0], old[1] + 2)
-            quantize_g(*groups[h - 1])
-            if h + 2 < len(x_parts):
-                quantize_x(*x_parts[h + 2])
-            if h - 2 not in DIRECT:
-                sigmoid(*old)
-            if h % 2 == 0:
-                for i in (h - 4, h - 3):
-                    if i not in DIRECT:
-                        store(*groups[i], scalar)
-            if h - 2 in DIRECT:
-                sigmoid_direct(old[0], old[1])
-                sigmoid_direct(old[0], old[1] + 2)
-            else:
-                multiply(*old)
-            empty_pair(b, k0, vector if h in HELP else scalar)
-            aggregate(b, k0 + 2, 2)
-            if h + 3 < len(x_parts):
-                interleave_x(*x_parts[h + 3], vector)
-            if h - 2 in DIRECT:
-                store_direct(old[0], old[1])
-                store_direct(old[0], old[1] + 2)
-            empty_pair(b, k0 + 2, scalar)
-            (project_direct if h - 1 in DIRECT else project)(*groups[h - 1])
-            if h % 2 == 1:
-                for i in (h - 3, h - 2):
-                    if i not in DIRECT:
-                        turn_out(*groups[i])
+        empty_g(1, 7, scalar)
+        turned = [(0, 0, 4), (1, 0, 4)]
+        direct = None
+        for b in range(2, BATCH - 1):
+            first, second = ((0, 4, 4), (1, 4, 4)) if b == 2 else ((b - 1, 0, 4), (b - 1, 4, 4))
+            if b > 2:
+                new_il(b + 1, 0)
+                interleave(b + 1, 0, SHARE, P, vector)
+            interleave(b + 1, 1, POOL, P, vector)
+            aggregate(b, 0, 2)
+            if direct:
+                sigmoid_direct(*direct)
+            if b > 2:
+                interleave(b + 1, 0, 0, SHARE, scalar)
+            empty_g(b, 0, scalar)
+            empty_g(b, 1, scalar)
+            if b == 2:
+                quantize_g(*first)
+            quantize_g(*second)
+            quantize_x(b + 1, 0)
+            if direct:
+                store_direct(*direct)
+            quantize_x(b + 1, 1)
+            if b + 2 < BATCH:
+                shared(b + 2, 1, POOL)
+            aggregate(b, 2, 2)
+            for group in turned:
+                turn_out(*group)
+            empty_g(b, 2, scalar)
+            empty_g(b, 3, scalar)
+            quantize_g(b, 0, 4)
+            aggregate(b, 4, 2)
+            for group in turned:
+                store(*group, scalar)
+            project(*second)
+            project_direct(*first)
+            empty_g(b, 4, scalar)
+            sigmoid(*second)
+            empty_g(b, 5, scalar)
+            add_bias(*first)
+            multiply(*second)
+            aggregate(b, 6, 2)
+            empty_g(b, 6, scalar)
+            empty_g(b, 7, scalar)
+            turned = [second]
+            direct = first
         b = BATCH - 1
+        before = (b - 1, 4, 4)
         aggregate(b, 0, 2)
-        add_bias(b - 1, 0)
-        add_bias(b - 1, 2)
-        quantize_g(b - 1, 4, 4)
-        store(b - 2, 0, 4, scalar)
-        store(b - 2, 4, 4, scalar)
-        empty_g(b, 0, vector)
-        sigmoid_direct(b - 1, 0)
-        sigmoid_direct(b - 1, 2)
+        sigmoid_direct(*direct)
+        project_direct(b - 1, 0, 4)
+        for group in turned:
+            turn_out(*group)
+        quantize_g(*before)
+        store_direct(*direct)
+        add_bias(b - 1, 0, 2)
+        add_bias(b - 1, 2, 2)
+        empty_g(b, 0, scalar)
         empty_g(b, 1, scalar)
+        for group in turned:
+            store(*group, scalar)
         aggregate(b, 2, 2)
-        store_direct(b - 1, 0)
-        store_direct(b - 1, 2)
-        quantize_g_half(b, 0, 0)
-        empty_pair(b, 2, vector)
-        project(b - 1, 4, 4)
+        quantize_g(b, 0, 2)
+        sigmoid_direct(b - 1, 0, 2)
+        sigmoid_direct(b - 1, 2, 2)
+        project(*before)
+        project_direct(b, 0, 2)
+        empty_g(b, 2, scalar)
+        empty_g(b, 3, scalar)
+        store_direct(b - 1, 0, 2)
+        store_direct(b - 1, 2, 2)
+        sigmoid(*before)
         aggregate(b, 4, 2)
-        quantize_g_half(b, 0, 1)
-        sigmoid(b - 1, 4, 4)
+        add_bias(b, 0, 2)
+        quantize_g(b, 2, 2)
+        multiply(*before)
         empty_g(b, 4, scalar)
-        project(b, 0, 4)
-        multiply(b - 1, 4, 4)
-        empty_g(b, 5, vector)
+        empty_g(b, 5, scalar)
+        sigmoid_direct(b, 0, 2)
+        project_direct(b, 2, 2)
         aggregate(b, 6, 2)
-        sigmoid(b, 0, 4)
+        turn_out(*before)
+        add_bias(b, 2, 2)
         quantize_g(b, 4, 2)
+        store_direct(b, 0, 2)
         empty_g(b, 6, scalar)
         empty_g(b, 7, scalar)
-        multiply(b, 0, 4)
-        turn_out(b - 1, 4, 4)
-        project(b, 4, 2)
-        turn_out(b, 0, 4)
+        sigmoid_direct(b, 2, 2)
+        store(*before, scalar)
+        project_direct(b, 4, 2)
         quantize_g(b, 6, 1)
-        store(b - 1, 4, 4, vector)
+        project_direct(b, 6, 1)
         quantize_g(b, 7, 1)
-        project(b, 6, 1)
-        project(b, 7, 1)
-        sigmoid(b, 4, 2)
-        store(b, 0, 4, scalar)
-        sigmoid(b, 6, 1)
-        sigmoid(b, 7, 1)
-        multiply(b, 4, 2)
-        multiply(b, 6, 1)
-        multiply(b, 7, 1)
-        turn_out(b, 4, 2)
-        turn_out(b, 6, 1)
-        turn_out(b, 7, 1)
-        store(b, 4, 2, vector)
-        store(b, 6, 1, scalar)
-        store(b, 7, 1, vector)
+        project_direct(b, 7, 1)
+        add_bias(b, 4, 2)
+        sigmoid_direct(b, 4, 2)
+        add_bias(b, 6, 1)
+        store_direct(b, 2, 2)
+        add_bias(b, 7, 1)
+        sigmoid_direct(b, 6, 1)
+        sigmoid_direct(b, 7, 1)
+        store_direct(b, 4, 2)
+        store_direct(b, 6, 1)
+        store_direct(b, 7, 1)

@@ -20,11 +20,11 @@ PAIR = 2 * P
 PASS = 4 * P
 FLOPS = 2 * NODES * NODES * BATCH * CHAN + 2 * NODES * BATCH * CHAN * 2 * HID
 
-HEAD_POOL = 80
-POOL = 64
-SHARE = 16
+HEAD_POOL = 64
+POOL = 40
+SHARE = 24
 G_BUFS = 5
-HEAD_SHARE = 48
+HEAD_SHARE = 32
 
 
 def tile_stsgcm_pa_t_w8_kernel(tc, x, A_bytes, A_scale, W0_words, W0_scales, b0, out):

@@ -20,11 +20,11 @@ PAIR = 2 * P
 PASS = 4 * P
 FLOPS = 2 * NODES * NODES * BATCH * CHAN + 2 * NODES * BATCH * CHAN * 2 * HID
 
-HEAD_POOL = 64
-POOL = 40
-SHARE = 24
+HEAD_POOL = 72
+POOL = 56
+SHARE = 20
 G_BUFS = 5
-HEAD_SHARE = 32
+HEAD_SHARE = 40
 
 
 def tile_stsgcm_pa_t_w8_kernel(tc, x, A_bytes, A_scale, W0_words, W0_scales, b0, out):
@@ -43,9 +43,26 @@ def tile_stsgcm_pa_t_w8_kernel(tc, x, A_bytes, A_scale, W0_words, W0_scales, b0,
         x_raw, a_raw, x_il, x_q, a_val, a_bank, a_il, a_q = ({} for i in range(8))
         g_bank, g_il, g_q, y_bank, gate, gated, o_bank, z = ({} for i in range(8))
 
+        turns = {}
+
+        def ring(name, size, shape, dtype):
+            turns[name] = turns.get(name, -1) + 1
+            return work.tile(shape, dtype, name="%s%d" % (name, turns[name] % size), bufs=1, align_bytes=64)
+
+        free_banks = list(range(8))
+        bank_of = {}
+
+        def take_bank(key, shape):
+            bank_of[key] = free_banks[0]
+            free_banks.remove(bank_of[key])
+            return psum.tile(shape, F32, name="bank%d" % bank_of[key], bufs=1)
+
+        def give_bank(key):
+            free_banks.append(bank_of[key])
+
         def load_x(b, g):
             if (b, g) == (0, 0):
-                x_raw[b, g] = work.tile([P, 4, CHAN], BF16, name="x_il_shared", bufs=1, align_bytes=64)
+                x_raw[b, g] = ring("x_il_shared", 1, [P, 4, CHAN], BF16)
             else:
                 x_raw[b, g] = const.tile([P, 4, CHAN], BF16, name="x_raw%d_%d" % (b, g))
             nc.sync.dma_start(out=x_raw[b, g][:], in_=x_view[g][b])
@@ -54,9 +71,9 @@ def tile_stsgcm_pa_t_w8_kernel(tc, x, A_bytes, A_scale, W0_words, W0_scales, b0,
             a_raw[q] = const.tile([P, 2, NODES], U8, name="a_raw%d" % q)
             nc.sync.dma_start(out=a_raw[q][:], in_=a_view[:, 2 * q : 2 * q + 2, :])
 
-        def quantize(name, bufs, pool, src, cols):
-            codes = pool.tile([P, cols], U32, name=name + "_codes", bufs=bufs, align_bytes=64)
-            scales = pool.tile([P, cols], U8, name=name + "_scales", bufs=bufs, align_bytes=64)
+        def quantize(name, bufs, src, cols):
+            codes = ring(name + "_codes", bufs, [P, cols], U32)
+            scales = ring(name + "_scales", bufs, [P, cols], U8)
             nc.vector.quantize_mx(out=codes[:].bitcast(FP8X4), scales=scales[:], in_=src)
             return codes, scales
 
@@ -64,7 +81,7 @@ def tile_stsgcm_pa_t_w8_kernel(tc, x, A_bytes, A_scale, W0_words, W0_scales, b0,
             nc.gpsimd.tensor_scalar(out=out, in0=in_, scalar1=1.0, scalar2=0.0, op0=MULT, op1=ADD)
 
         def new_il(b, g, name="x_il", bufs=3):
-            x_il[b, g] = work.tile([P, 4 * CHAN], BF16, name=name, bufs=bufs, align_bytes=64)
+            x_il[b, g] = ring(name, bufs, [P, 4 * CHAN], BF16)
 
         def interleave(b, g, lo, hi, copy):
             dst = x_il[b, g][:].rearrange("p (t m j) -> p t m j", t=4, j=4)[:, :, lo:hi, :]
@@ -75,14 +92,14 @@ def tile_stsgcm_pa_t_w8_kernel(tc, x, A_bytes, A_scale, W0_words, W0_scales, b0,
                 copy(out=dst.rearrange("p t (m i) j -> p m j t i", i=2), in_=src.rearrange("p j (m i t) -> p m j t i", i=2, t=4))
 
         def quantize_x(b, g):
-            x_q[b, g] = quantize("x", 8, work, x_il[b, g][:], CHAN)
+            x_q[b, g] = quantize("x", 8, x_il[b, g][:], CHAN)
 
         def widen_a(k, copy):
-            a_val[k] = work.tile([P, NODES], BF16, name="a_val", bufs=3)
+            a_val[k] = ring("a_val", 3, [P, NODES], BF16)
             copy(out=a_val[k][:], in_=a_raw[k // 2][:, k % 2, :].bitcast(FP8))
 
         def turn_a(k):
-            a_bank[k] = psum.tile([P, 2, 2, P], F32, name="bank")
+            a_bank[k] = take_bank(("a", k), [P, 2, 2, P])
             words = a_val[k][:].bitcast(F32)
             for g in range(2):
                 for u in range(2):
@@ -90,20 +107,21 @@ def tile_stsgcm_pa_t_w8_kernel(tc, x, A_bytes, A_scale, W0_words, W0_scales, b0,
 
         def scale_a(k):
             if k // 2 not in a_il:
-                a_il[k // 2] = work.tile([P, 2, 2, P, 2, 2], BF16, name="a_il", bufs=2, align_bytes=64)
+                a_il[k // 2] = ring("a_il", 2, [P, 2, 2, P, 2, 2], BF16)
             nc.vector.tensor_tensor(
                 out=a_il[k // 2][:, k % 2],
                 in0=a_bank[k][:].rearrange("p u g v -> p (u g v)").bitcast(BF16).rearrange("p (u g v e) -> p g v u e", u=2, g=2, e=2),
                 in1=a_scale[:].rearrange("p g (u e) -> p g u e", u=2).unsqueeze(2).to_broadcast([P, 2, P, 2, 2]),
                 op=MULT,
             )
+            give_bank(("a", k))
 
         def quantize_a(q):
-            a_q[q] = quantize("a%d" % q, 1, const, a_il[q][:].rearrange("p k g v u e -> p (k g v u e)"), 2 * PAIR)
+            a_q[q] = quantize("a", 4, a_il[q][:].rearrange("p k g v u e -> p (k g v u e)"), 2 * PAIR)
 
         def aggregate(b, k0, n):
             for k in range(k0, k0 + n):
-                g_bank[b, k] = psum.tile([P, 4, P], F32, name="bank")
+                g_bank[b, k] = take_bank(("g", b, k), [P, 4, P])
                 for t in range(4):
                     for g in range(2):
                         cols = slice(PAIR * (k % 2) + P * g, PAIR * (k % 2) + P * (g + 1))
@@ -119,16 +137,17 @@ def tile_stsgcm_pa_t_w8_kernel(tc, x, A_bytes, A_scale, W0_words, W0_scales, b0,
 
         def empty_g(b, k, copy):
             if (b, k // 4) not in g_il:
-                g_il[b, k // 4] = work.tile([P, 4, P, 4], BF16, name="g_il", bufs=G_BUFS, align_bytes=64)
+                g_il[b, k // 4] = ring("g_il", G_BUFS, [P, 4, P, 4], BF16)
             copy(out=g_il[b, k // 4][:, k % 4, :, :], in_=g_bank[b, k][:].rearrange("p t v -> p v t"))
+            give_bank(("g", b, k))
 
         def quantize_g(b, k0, n):
             src = g_il[b, k0 // 4][:, k0 % 4 : k0 % 4 + n, :, :]
-            g_q[b, k0] = quantize("g%d" % n, 6 if n == 4 else 3, work, src.rearrange("p k v t -> p (k v t)"), n * P)
+            g_q[b, k0] = quantize("g%d" % n, 6 if n == 4 else 3, src.rearrange("p k v t -> p (k v t)"), n * P)
 
         def project(b, k0, n):
             for half in (1, 0):
-                y_bank[b, k0, half] = psum.tile([P, n * P], F32, name="bank")
+                y_bank[b, k0, half] = take_bank(("y", b, k0, half), [P, n * P])
                 nc.tensor.matmul_mx(
                     out=y_bank[b, k0, half][:],
                     lhsT=w_words[:, HID * half : HID * (half + 1)].bitcast(FP8X4),
@@ -140,28 +159,31 @@ def tile_stsgcm_pa_t_w8_kernel(tc, x, A_bytes, A_scale, W0_words, W0_scales, b0,
                 )
 
         def sigmoid(b, k0, n):
-            gate[b, k0] = work.tile([P, n * P], F32, name="gate", bufs=5)
+            gate[b, k0] = ring("gate", 5, [P, n * P], F32)
             nc.scalar.activation(out=gate[b, k0][:], in_=y_bank[b, k0, 1][:], func=ACT.Sigmoid, bias=bias_col[:, 1:2])
+            give_bank(("y", b, k0, 1))
 
         def multiply(b, k0, n):
-            gated[b, k0] = work.tile([P, n * P], F32, name="gated", bufs=4)
+            gated[b, k0] = ring("gated", 4, [P, n * P], F32)
             nc.vector.scalar_tensor_tensor(
                 out=gated[b, k0][:], in0=y_bank[b, k0, 0][:], scalar=bias_col[:, 0:1], in1=gate[b, k0][:], op0=ADD, op1=MULT
             )
+            give_bank(("y", b, k0, 0))
 
         def turn_out(b, k0, n):
-            o_bank[b, k0] = psum.tile([P, n, P], F32, name="bank")
+            o_bank[b, k0] = take_bank(("o", b, k0), [P, n, P])
             for k in range(n):
                 nc.tensor.transpose(o_bank[b, k0][:, k, :], gated[b, k0][:, P * k : P * (k + 1)], ident[:])
 
         def store(b, k0, n, copy):
-            rows = work.tile([P, n, HID], F32, name="rows", bufs=6)
+            rows = ring("rows", 6, [P, n, HID], F32)
             copy(out=rows[:], in_=o_bank[b, k0][:])
+            give_bank(("o", b, k0))
             nc.sync.dma_start(out=out_view[b][:, k0 : k0 + n, :], in_=rows[:])
 
         def project_direct(b, k0, n):
             for first in range(k0, k0 + n, 2):
-                y_bank[b, first] = psum.tile([P, min(n, 2), 2 * HID], F32, name="bank")
+                y_bank[b, first] = take_bank(("y", b, first), [P, min(n, 2), 2 * HID])
                 for k in range(first, first + min(n, 2)):
                     cols = slice(P * (k - k0), P * (k - k0 + 1))
                     nc.tensor.matmul_mx(
@@ -175,7 +197,7 @@ def tile_stsgcm_pa_t_w8_kernel(tc, x, A_bytes, A_scale, W0_words, W0_scales, b0,
                     )
 
         def add_bias(b, k0, n):
-            z[b, k0] = work.tile([P, n, 2 * HID], F32, name="z%d" % n, bufs=2 if n == 4 else 4)
+            z[b, k0] = ring("z%d_" % n, 2 if n == 4 else 4, [P, n, 2 * HID], F32)
             for first in range(k0, k0 + n, 2):
                 m = min(n, 2)
                 nc.vector.tensor_tensor(
@@ -184,13 +206,14 @@ def tile_stsgcm_pa_t_w8_kernel(tc, x, A_bytes, A_scale, W0_words, W0_scales, b0,
                     in1=bias_row[:].unsqueeze(1).to_broadcast([P, m, 2 * HID]),
                     op=ADD,
                 )
+                give_bank(("y", b, first))
 
         def sigmoid_direct(b, k0, n):
-            gate[b, k0] = work.tile([P, n, HID], F32, name="gate", bufs=5)
+            gate[b, k0] = ring("gate", 5, [P, n, HID], F32)
             nc.scalar.activation(out=gate[b, k0][:], in_=z[b, k0][:, :, HID:], func=ACT.Sigmoid)
 
         def store_direct(b, k0, n):
-            rows = work.tile([P, n, HID], F32, name="rows", bufs=6)
+            rows = ring("rows", 6, [P, n, HID], F32)
             nc.vector.tensor_tensor(out=rows[:], in0=z[b, k0][:, :, :HID], in1=gate[b, k0][:], op=MULT)
             nc.sync.dma_start(out=out_view[b][:, k0 : k0 + n, :], in_=rows[:])
 
@@ -347,13 +370,14 @@ def tile_stsgcm_pa_t_w8_kernel(tc, x, A_bytes, A_scale, W0_words, W0_scales, b0,
             if b + 2 < BATCH:
                 shared(b + 2, 1, POOL)
             aggregate(b, 2, 2)
-            for group in turned:
+            run = turned if len(turned) == 2 else []
+            for group in run:
                 turn_out(*group)
             empty_g(b, 2, scalar)
             empty_g(b, 3, scalar)
             quantize_g(b, 0, 4)
             aggregate(b, 4, 2)
-            for group in turned:
+            for group in run:
                 store(*group, scalar)
             project(*second)
             project_direct(*first)
@@ -364,8 +388,8 @@ def tile_stsgcm_pa_t_w8_kernel(tc, x, A_bytes, A_scale, W0_words, W0_scales, b0,
             multiply(*second)
             aggregate(b, 6, 2)
             empty_g(b, 6, scalar)
-            empty_g(b, 7, scalar)
-            turned = [second]
+            empty_g(b, 7, vector if b == BATCH - 2 else scalar)
+            turned = turned[len(run) :] + [second]
             direct = first
         b = BATCH - 1
         before = (b - 1, 4, 4)

@@ -22,9 +22,9 @@ FLOPS = 2 * NODES * NODES * BATCH * CHAN + 2 * NODES * BATCH * CHAN * 2 * HID
 
 HEAD_POOL = 72
 POOL = 56
-SHARE = 20
+SHARE = 12
 G_BUFS = 5
-HEAD_SHARE = 40
+HEAD_SHARE = 32
 
 
 def tile_stsgcm_pa_t_w8_kernel(tc, x, A_bytes, A_scale, W0_words, W0_scales, b0, out):
@@ -138,7 +138,10 @@ def tile_stsgcm_pa_t_w8_kernel(tc, x, A_bytes, A_scale, W0_words, W0_scales, b0,
         def empty_g(b, k, copy):
             if (b, k // 4) not in g_il:
                 g_il[b, k // 4] = ring("g_il", G_BUFS, [P, 4, P, 4], BF16)
-            copy(out=g_il[b, k // 4][:, k % 4, :, :], in_=g_bank[b, k][:].rearrange("p t v -> p v t"))
+            copy(
+                out=g_il[b, k // 4][:, k % 4, :, :].rearrange("p (w i) t -> p w t i", i=2),
+                in_=g_bank[b, k][:].rearrange("p t (w i) -> p w t i", i=2),
+            )
             give_bank(("g", b, k))
 
         def quantize_g(b, k0, n):
@@ -400,33 +403,33 @@ def tile_stsgcm_pa_t_w8_kernel(tc, x, A_bytes, A_scale, W0_words, W0_scales, b0,
             turn_out(*group)
         quantize_g(*before)
         store_direct(*direct)
-        add_bias(b - 1, 0, 2)
-        add_bias(b - 1, 2, 2)
         empty_g(b, 0, scalar)
         empty_g(b, 1, scalar)
+        add_bias(b - 1, 0, 2)
+        quantize_g(b, 0, 2)
+        add_bias(b - 1, 2, 2)
         for group in turned:
             store(*group, scalar)
         aggregate(b, 2, 2)
-        quantize_g(b, 0, 2)
-        sigmoid_direct(b - 1, 0, 2)
-        sigmoid_direct(b - 1, 2, 2)
         project(*before)
         project_direct(b, 0, 2)
         empty_g(b, 2, scalar)
         empty_g(b, 3, scalar)
-        store_direct(b - 1, 0, 2)
-        store_direct(b - 1, 2, 2)
+        sigmoid_direct(b - 1, 0, 2)
         sigmoid(*before)
         aggregate(b, 4, 2)
         add_bias(b, 0, 2)
         quantize_g(b, 2, 2)
+        store_direct(b - 1, 0, 2)
         multiply(*before)
+        sigmoid_direct(b - 1, 2, 2)
         empty_g(b, 4, scalar)
         empty_g(b, 5, scalar)
         sigmoid_direct(b, 0, 2)
         project_direct(b, 2, 2)
         aggregate(b, 6, 2)
         turn_out(*before)
+        store_direct(b - 1, 2, 2)
         add_bias(b, 2, 2)
         quantize_g(b, 4, 2)
         store_direct(b, 0, 2)
@@ -442,8 +445,8 @@ def tile_stsgcm_pa_t_w8_kernel(tc, x, A_bytes, A_scale, W0_words, W0_scales, b0,
         add_bias(b, 4, 2)
         sigmoid_direct(b, 4, 2)
         add_bias(b, 6, 1)
-        store_direct(b, 2, 2)
         add_bias(b, 7, 1)
+        store_direct(b, 2, 2)
         sigmoid_direct(b, 6, 1)
         sigmoid_direct(b, 7, 1)
         store_direct(b, 4, 2)

@@ -131,8 +131,8 @@ def tile_stsgcm_pa_t_w8_kernel(tc, x, A_bytes, A_scale, W0_words, W0_scales, b0,
                             lhsT_scale=x_q[b, g][1][:, P * t : P * (t + 1)],
                             rhs=a_q[k // 2][0][:, cols].bitcast(FP8X4),
                             rhs_scale=a_q[k // 2][1][:, cols],
-                            start=(g == 0),
-                            stop=(g == 1),
+                            start=(t == 0 and g == 0),
+                            stop=(t == 3 and g == 1),
                         )
 
         def empty_g(b, k, copy):
@@ -195,8 +195,8 @@ def tile_stsgcm_pa_t_w8_kernel(tc, x, A_bytes, A_scale, W0_words, W0_scales, b0,
                         lhsT_scale=g_q[b, k0][1][:, cols],
                         rhs=w_words[:].bitcast(FP8X4),
                         rhs_scale=w_scales[:],
-                        start=True,
-                        stop=True,
+                        start=(k == first),
+                        stop=(k == first + min(n, 2) - 1),
                     )
 
         def add_bias(b, k0, n):

@@ -20,11 +20,11 @@ PAIR = 2 * P
 PASS = 4 * P
 FLOPS = 2 * NODES * NODES * BATCH * CHAN + 2 * NODES * BATCH * CHAN * 2 * HID
 
-HEAD_POOL = 72
+HEAD_POOL = 76
 POOL = 56
-SHARE = 12
+SHARE = 20
 G_BUFS = 5
-HEAD_SHARE = 32
+HEAD_SHARE = 40
 
 
 def tile_stsgcm_pa_t_w8_kernel(tc, x, A_bytes, A_scale, W0_words, W0_scales, b0, out):
@@ -119,11 +119,12 @@ def tile_stsgcm_pa_t_w8_kernel(tc, x, A_bytes, A_scale, W0_words, W0_scales, b0,
         def quantize_a(q):
             a_q[q] = quantize("a", 4, a_il[q][:].rearrange("p k g v u e -> p (k g v u e)"), 2 * PAIR)
 
-        def aggregate(b, k0, n):
+        def aggregate(b, k0, n, passes=(0, 1)):
             for k in range(k0, k0 + n):
-                g_bank[b, k] = take_bank(("g", b, k), [P, 4, P])
+                if 0 in passes:
+                    g_bank[b, k] = take_bank(("g", b, k), [P, 4, P])
                 for t in range(4):
-                    for g in range(2):
+                    for g in passes:
                         cols = slice(PAIR * (k % 2) + P * g, PAIR * (k % 2) + P * (g + 1))
                         nc.tensor.matmul_mx(
                             out=g_bank[b, k][:, t, :],
@@ -305,16 +306,20 @@ def tile_stsgcm_pa_t_w8_kernel(tc, x, A_bytes, A_scale, W0_words, W0_scales, b0,
         interleave(1, 1, HEAD_POOL, P, scalar)
         aggregate(0, 2, 2)
         turn_a(7)
-        for k in range(4):
-            empty_g(0, k, scalar)
+        aggregate(1, 0, 2, (0,))
+        empty_g(0, 0, scalar)
+        empty_g(0, 1, scalar)
+        aggregate(1, 2, 2, (0,))
+        empty_g(0, 2, scalar)
+        empty_g(0, 3, scalar)
         quantize_x(1, 1)
         shared(2, 0, HEAD_POOL)
         quantize_a(2)
         scale_a(6)
         scale_a(7)
-        aggregate(1, 0, 2)
+        aggregate(1, 0, 2, (1,))
         interleave(2, 0, HEAD_POOL, P, scalar)
-        aggregate(1, 2, 2)
+        aggregate(1, 2, 2, (1,))
         empty_g(1, 0, scalar)
         empty_g(1, 1, scalar)
         quantize_x(2, 0)
@@ -391,7 +396,7 @@ def tile_stsgcm_pa_t_w8_kernel(tc, x, A_bytes, A_scale, W0_words, W0_scales, b0,
             multiply(*second)
             aggregate(b, 6, 2)
             empty_g(b, 6, scalar)
-            empty_g(b, 7, vector if b == BATCH - 2 else scalar)
+            empty_g(b, 7, scalar)
             turned = turned[len(run) :] + [second]
             direct = first
         b = BATCH - 1

@@ -25,6 +25,7 @@ POOL = 56
 SHARE = 20
 G_BUFS = 5
 HEAD_SHARE = 40
+SHIFT = 64
 
 
 def tile_stsgcm_pa_t_w8_kernel(tc, x, A_bytes, A_scale, W0_words, W0_scales, b0, out):
@@ -49,6 +50,10 @@ def tile_stsgcm_pa_t_w8_kernel(tc, x, A_bytes, A_scale, W0_words, W0_scales, b0,
             turns[name] = turns.get(name, -1) + 1
             return work.tile(shape, dtype, name="%s%d" % (name, turns[name] % size), bufs=1, align_bytes=64)
 
+        def slot(name, size):
+            turns[name] = turns.get(name, -1) + 1
+            return "%s%d" % (name, turns[name] % size)
+
         free_banks = list(range(8))
         bank_of = {}
 
@@ -71,10 +76,10 @@ def tile_stsgcm_pa_t_w8_kernel(tc, x, A_bytes, A_scale, W0_words, W0_scales, b0,
             a_raw[q] = const.tile([P, 2, NODES], U8, name="a_raw%d" % q)
             nc.sync.dma_start(out=a_raw[q][:], in_=a_view[:, 2 * q : 2 * q + 2, :])
 
-        def quantize(name, bufs, src, cols):
-            codes = ring(name + "_codes", bufs, [P, cols], U32)
-            scales = ring(name + "_scales", bufs, [P, cols], U8)
-            nc.vector.quantize_mx(out=codes[:].bitcast(FP8X4), scales=scales[:], in_=src)
+        def quantize(name, bufs, src, cols, shift=0):
+            codes = work.tile([P, cols + 64], U32, name=slot(name + "_codes", bufs), bufs=1, align_bytes=256)[:, shift // 4 : shift // 4 + cols]
+            scales = work.tile([P, cols + 256], U8, name=slot(name + "_scales", bufs), bufs=1, align_bytes=256)[:, shift : shift + cols]
+            nc.vector.quantize_mx(out=codes.bitcast(FP8X4), scales=scales, in_=src)
             return codes, scales
 
         def pool_copy(out, in_):
@@ -92,7 +97,7 @@ def tile_stsgcm_pa_t_w8_kernel(tc, x, A_bytes, A_scale, W0_words, W0_scales, b0,
                 copy(out=dst.rearrange("p t (m i) j -> p m j t i", i=2), in_=src.rearrange("p j (m i t) -> p m j t i", i=2, t=4))
 
         def quantize_x(b, g):
-            x_q[b, g] = quantize("x", 8, x_il[b, g][:], CHAN)
+            x_q[b, g] = quantize("x", 6, x_il[b, g][:], CHAN)
 
         def widen_a(k, copy):
             a_val[k] = ring("a_val", 3, [P, NODES], BF16)
@@ -117,7 +122,7 @@ def tile_stsgcm_pa_t_w8_kernel(tc, x, A_bytes, A_scale, W0_words, W0_scales, b0,
             give_bank(("a", k))
 
         def quantize_a(q):
-            a_q[q] = quantize("a", 4, a_il[q][:].rearrange("p k g v u e -> p (k g v u e)"), 2 * PAIR)
+            a_q[q] = quantize("a", 4, a_il[q][:].rearrange("p k g v u e -> p (k g v u e)"), 2 * PAIR, SHIFT)
 
         def aggregate(b, k0, n, passes=(0, 1)):
             for k in range(k0, k0 + n):
@@ -147,7 +152,7 @@ def tile_stsgcm_pa_t_w8_kernel(tc, x, A_bytes, A_scale, W0_words, W0_scales, b0,
 
         def quantize_g(b, k0, n):
             src = g_il[b, k0 // 4][:, k0 % 4 : k0 % 4 + n, :, :]
-            g_q[b, k0] = quantize("g%d" % n, 6 if n == 4 else 3, src.rearrange("p k v t -> p (k v t)"), n * P)
+            g_q[b, k0] = quantize("g%d" % n, 6 if n == 4 else 3, src.rearrange("p k v t -> p (k v t)"), n * P, SHIFT)
 
         def project(b, k0, n):
             for half in (1, 0):
@@ -156,8 +161,8 @@ def tile_stsgcm_pa_t_w8_kernel(tc, x, A_bytes, A_scale, W0_words, W0_scales, b0,
                     out=y_bank[b, k0, half][:],
                     lhsT=w_words[:, HID * half : HID * (half + 1)].bitcast(FP8X4),
                     lhsT_scale=w_scales[:, HID * half : HID * (half + 1)],
-                    rhs=g_q[b, k0][0][:].bitcast(FP8X4),
-                    rhs_scale=g_q[b, k0][1][:],
+                    rhs=g_q[b, k0][0].bitcast(FP8X4),
+                    rhs_scale=g_q[b, k0][1],
                     start=True,
                     stop=True,
                 )
@@ -224,12 +229,12 @@ def tile_stsgcm_pa_t_w8_kernel(tc, x, A_bytes, A_scale, W0_words, W0_scales, b0,
         warm = const.tile([P, 1], F32, name="warm")
         nc.vector.memset(warm[:], 0.0)
         nc.scalar.activation(out=warm[:], in_=warm[:], func=ACT.Sigmoid)
-        w_scales = const.tile([P, 2 * HID], U8, name="w_scales", align_bytes=64)
+        w_scales = const.tile([P, 2 * HID], U8, name="w_scales", align_bytes=256)
         nc.vector.memset(w_scales[:].bitcast(I32), 0)
         ident = const.tile([P, P], F32, name="ident")
         make_identity(nc, ident[:])
         a_scale = const.tile([P, 2, 4], F32, name="a_scale")
-        w_words = const.tile([P, 2 * HID], U32, name="w_words", align_bytes=64)
+        w_words = const.tile([P, 2 * HID], U32, name="w_words", align_bytes=256)
         bias_col = const.tile([P, 2], BF16, name="bias_col")
         bias_row = const.tile([P, 2 * HID], BF16, name="bias_row")
 

@@ -26,6 +26,7 @@ SHARE = 20
 G_BUFS = 5
 HEAD_SHARE = 40
 SHIFT = 64
+X_ROW, A_ROW, G_ROW = 8, 4, 4
 
 
 def tile_stsgcm_pa_t_w8_kernel(tc, x, A_bytes, A_scale, W0_words, W0_scales, b0, out):
@@ -76,9 +77,9 @@ def tile_stsgcm_pa_t_w8_kernel(tc, x, A_bytes, A_scale, W0_words, W0_scales, b0,
             a_raw[q] = const.tile([P, 2, NODES], U8, name="a_raw%d" % q)
             nc.sync.dma_start(out=a_raw[q][:], in_=a_view[:, 2 * q : 2 * q + 2, :])
 
-        def quantize(name, bufs, src, cols, shift=0):
+        def quantize(name, bufs, src, cols, row, shift=0):
             codes = work.tile([P, cols + 64], U32, name=slot(name + "_codes", bufs), bufs=1, align_bytes=256)[:, shift // 4 : shift // 4 + cols]
-            scales = work.tile([P, cols + 256], U8, name=slot(name + "_scales", bufs), bufs=1, align_bytes=256)[:, shift : shift + cols]
+            scales = work.tile([P, cols + 256], U8, name=slot(name + "_scales", bufs), bufs=1, align_bytes=256)[row:, shift : shift + cols]
             nc.vector.quantize_mx(out=codes.bitcast(FP8X4), scales=scales, in_=src)
             return codes, scales
 
@@ -97,7 +98,7 @@ def tile_stsgcm_pa_t_w8_kernel(tc, x, A_bytes, A_scale, W0_words, W0_scales, b0,
                 copy(out=dst.rearrange("p t (m i) j -> p m j t i", i=2), in_=src.rearrange("p j (m i t) -> p m j t i", i=2, t=4))
 
         def quantize_x(b, g):
-            x_q[b, g] = quantize("x", 6, x_il[b, g][:], CHAN)
+            x_q[b, g] = quantize("x", 6, x_il[b, g][:], CHAN, X_ROW)
 
         def widen_a(k, copy):
             a_val[k] = ring("a_val", 3, [P, NODES], BF16)
@@ -122,7 +123,7 @@ def tile_stsgcm_pa_t_w8_kernel(tc, x, A_bytes, A_scale, W0_words, W0_scales, b0,
             give_bank(("a", k))
 
         def quantize_a(q):
-            a_q[q] = quantize("a", 4, a_il[q][:].rearrange("p k g v u e -> p (k g v u e)"), 2 * PAIR, SHIFT)
+            a_q[q] = quantize("a", 4, a_il[q][:].rearrange("p k g v u e -> p (k g v u e)"), 2 * PAIR, A_ROW, SHIFT)
 
         def aggregate(b, k0, n, passes=(0, 1)):
             for k in range(k0, k0 + n):
@@ -152,7 +153,7 @@ def tile_stsgcm_pa_t_w8_kernel(tc, x, A_bytes, A_scale, W0_words, W0_scales, b0,
 
         def quantize_g(b, k0, n):
             src = g_il[b, k0 // 4][:, k0 % 4 : k0 % 4 + n, :, :]
-            g_q[b, k0] = quantize("g%d" % n, 6 if n == 4 else 3, src.rearrange("p k v t -> p (k v t)"), n * P, SHIFT)
+            g_q[b, k0] = quantize("g%d" % n, 6 if n == 4 else 3, src.rearrange("p k v t -> p (k v t)"), n * P, G_ROW, SHIFT)
 
         def project(b, k0, n):
             for half in (1, 0):

@@ -17,24 +17,28 @@ ACT = mybir.ActivationFunctionType
 NODES, BATCH, CHAN, HID = 1024, 8, 512, 128
 P = 128
 PAIR = 2 * P
-PASS = 4 * P
 FLOPS = 2 * NODES * NODES * BATCH * CHAN + 2 * NODES * BATCH * CHAN * 2 * HID
 
 HEAD_POOL = 76
 POOL = 56
 SHARE = 20
-G_BUFS = 5
 HEAD_SHARE = 40
+G_BUFS = 5
+Z_BUFS = 3
+X_CODES = 6
+A_VALS = 3
 SHIFT = 64
-X_ROW, A_ROW, G_ROW = 8, 4, 4
+X_ROW = 8
+A_ROW = 4
+G_ROW = 4
 
 
 def tile_stsgcm_pa_t_w8_kernel(tc, x, A_bytes, A_scale, W0_words, W0_scales, b0, out):
     nc = tc.nc
     with ExitStack() as ctx:
         const = ctx.enter_context(tc.tile_pool(name="const", bufs=1))
-        work = ctx.enter_context(tc.tile_pool(name="work", bufs=3))
-        psum = ctx.enter_context(tc.psum_pool(name="psum", bufs=8))
+        work = ctx.enter_context(tc.tile_pool(name="work", bufs=1))
+        psum = ctx.enter_context(tc.psum_pool(name="psum", bufs=1))
         ctx.enter_context(tc.manual_schedule())
 
         x_view = x.rearrange("(g p j) b c -> g b p j c", p=P, j=4)
@@ -43,17 +47,13 @@ def tile_stsgcm_pa_t_w8_kernel(tc, x, A_bytes, A_scale, W0_words, W0_scales, b0,
         vector, scalar = nc.vector.tensor_copy, nc.scalar.copy
 
         x_raw, a_raw, x_il, x_q, a_val, a_bank, a_il, a_q = ({} for i in range(8))
-        g_bank, g_il, g_q, y_bank, gate, gated, o_bank, z = ({} for i in range(8))
+        g_bank, g_il, g_q, y_bank, gate, z, gated, o_bank, rows = ({} for i in range(9))
 
         turns = {}
 
-        def ring(name, size, shape, dtype):
+        def ring(name, size, shape, dtype, align=64):
             turns[name] = turns.get(name, -1) + 1
-            return work.tile(shape, dtype, name="%s%d" % (name, turns[name] % size), bufs=1, align_bytes=64)
-
-        def slot(name, size):
-            turns[name] = turns.get(name, -1) + 1
-            return "%s%d" % (name, turns[name] % size)
+            return work.tile(shape, dtype, name="%s%d" % (name, turns[name] % size), bufs=1, align_bytes=align)
 
         free_banks = list(range(8))
         bank_of = {}
@@ -68,41 +68,54 @@ def tile_stsgcm_pa_t_w8_kernel(tc, x, A_bytes, A_scale, W0_words, W0_scales, b0,
 
         def load_x(b, g):
             if (b, g) == (0, 0):
-                x_raw[b, g] = ring("x_il_shared", 1, [P, 4, CHAN], BF16)
+                x_raw[b, g] = ring("shared", 1, [P, 4, CHAN], BF16)
             else:
-                x_raw[b, g] = const.tile([P, 4, CHAN], BF16, name="x_raw%d_%d" % (b, g))
+                x_raw[b, g] = const.tile([P, 4, CHAN], BF16, name="x_raw%d_%d" % (b, g), align_bytes=64)
             nc.sync.dma_start(out=x_raw[b, g][:], in_=x_view[g][b])
 
-        def load_a(q):
-            a_raw[q] = const.tile([P, 2, NODES], U8, name="a_raw%d" % q)
-            nc.sync.dma_start(out=a_raw[q][:], in_=a_view[:, 2 * q : 2 * q + 2, :])
+        def load_a(k0, n):
+            tiles = const.tile([P, n, NODES], U8, name="a_raw%d" % k0)
+            nc.sync.dma_start(out=tiles[:], in_=a_view[:, k0 : k0 + n, :])
+            for k in range(n):
+                a_raw[k0 + k] = tiles[:, k, :]
 
         def quantize(name, bufs, src, cols, row, shift=0):
-            codes = work.tile([P, cols + 64], U32, name=slot(name + "_codes", bufs), bufs=1, align_bytes=256)[:, shift // 4 : shift // 4 + cols]
-            scales = work.tile([P, cols + 256], U8, name=slot(name + "_scales", bufs), bufs=1, align_bytes=256)[row:, shift : shift + cols]
+            codes = ring(name + "_codes", bufs, [P, cols + 64], U32, 256)[:, shift // 4 : shift // 4 + cols]
+            scales = ring(name + "_scales", bufs, [P, cols + 256], U8, 256)[row:, shift : shift + cols]
             nc.vector.quantize_mx(out=codes.bitcast(FP8X4), scales=scales, in_=src)
             return codes, scales
 
-        def pool_copy(out, in_):
+        def pool(out, in_):
             nc.gpsimd.tensor_scalar(out=out, in0=in_, scalar1=1.0, scalar2=0.0, op0=MULT, op1=ADD)
 
-        def new_il(b, g, name="x_il", bufs=3):
-            x_il[b, g] = ring(name, bufs, [P, 4 * CHAN], BF16)
+        def operand(name, size, passes=1):
+            return ring(name, size, [P, passes * 4 * CHAN], BF16)[:]
 
         def interleave(b, g, lo, hi, copy):
-            dst = x_il[b, g][:].rearrange("p (t m j) -> p t m j", t=4, j=4)[:, :, lo:hi, :]
+            dst = x_il[b, g].rearrange("p (t m j) -> p t m j", t=4, j=4)[:, :, lo:hi, :]
             src = x_raw[b, g][:, :, 4 * lo : 4 * hi]
-            if copy is pool_copy:
+            if copy is pool:
                 copy(out=dst.rearrange("p t m j -> p m t j"), in_=src.rearrange("p j (m t) -> p m t j", t=4))
             else:
                 copy(out=dst.rearrange("p t (m i) j -> p m j t i", i=2), in_=src.rearrange("p j (m i t) -> p m j t i", i=2, t=4))
 
         def quantize_x(b, g):
-            x_q[b, g] = quantize("x", 6, x_il[b, g][:], CHAN, X_ROW)
+            codes, scales = quantize("x", X_CODES, x_il[b, g], CHAN, X_ROW)
+            x_q[b, g] = codes, scales
+
+        def both_passes(b):
+            x_il[b] = operand("shared", 1, 2)
+            for g in range(2):
+                x_il[b, g] = x_il[b][:, 4 * CHAN * g : 4 * CHAN * (g + 1)]
+
+        def quantize_entry(b):
+            codes, scales = quantize("xx", 2, x_il[b], 2 * CHAN, 0)
+            for g in range(2):
+                x_q[b, g] = codes[:, CHAN * g : CHAN * (g + 1)], scales[:, CHAN * g : CHAN * (g + 1)]
 
         def widen_a(k, copy):
-            a_val[k] = ring("a_val", 3, [P, NODES], BF16)
-            copy(out=a_val[k][:], in_=a_raw[k // 2][:, k % 2, :].bitcast(FP8))
+            a_val[k] = ring("a_val", A_VALS, [P, NODES], BF16)
+            copy(out=a_val[k][:], in_=a_raw[k].bitcast(FP8))
 
         def turn_a(k):
             a_bank[k] = take_bank(("a", k), [P, 2, 2, P])
@@ -112,18 +125,19 @@ def tile_stsgcm_pa_t_w8_kernel(tc, x, A_bytes, A_scale, W0_words, W0_scales, b0,
                     nc.tensor.transpose(a_bank[k][:, u, g, :], words[:, 256 * g + u : 256 * (g + 1) : 2], ident[:])
 
         def scale_a(k):
-            if k // 2 not in a_il:
-                a_il[k // 2] = ring("a_il", 2, [P, 2, 2, P, 2, 2], BF16)
             nc.vector.tensor_tensor(
-                out=a_il[k // 2][:, k % 2],
+                out=a_il[k // 2].rearrange("p (k g v u e) -> p k g v u e", k=2, g=2, u=2, e=2)[:, k % 2],
                 in0=a_bank[k][:].rearrange("p u g v -> p (u g v)").bitcast(BF16).rearrange("p (u g v e) -> p g v u e", u=2, g=2, e=2),
                 in1=a_scale[:].rearrange("p g (u e) -> p g u e", u=2).unsqueeze(2).to_broadcast([P, 2, P, 2, 2]),
                 op=MULT,
             )
             give_bank(("a", k))
 
-        def quantize_a(q):
-            a_q[q] = quantize("a", 4, a_il[q][:].rearrange("p k g v u e -> p (k g v u e)"), 2 * PAIR, A_ROW, SHIFT)
+        def quantize_a(k0, n):
+            src = a_il[k0 // 2][:, 2 * CHAN * (k0 % 2) : 2 * CHAN * (k0 % 2 + n)]
+            codes, scales = quantize("a%d_" % k0, 1, src, n * PAIR, A_ROW, SHIFT)
+            for k in range(n):
+                a_q[k0 + k] = codes[:, PAIR * k : PAIR * (k + 1)], scales[:, PAIR * k : PAIR * (k + 1)]
 
         def aggregate(b, k0, n, passes=(0, 1)):
             for k in range(k0, k0 + n):
@@ -131,31 +145,74 @@ def tile_stsgcm_pa_t_w8_kernel(tc, x, A_bytes, A_scale, W0_words, W0_scales, b0,
                     g_bank[b, k] = take_bank(("g", b, k), [P, 4, P])
                 for t in range(4):
                     for g in passes:
-                        cols = slice(PAIR * (k % 2) + P * g, PAIR * (k % 2) + P * (g + 1))
+                        cols = slice(P * g, P * (g + 1))
                         nc.tensor.matmul_mx(
                             out=g_bank[b, k][:, t, :],
                             lhsT=x_q[b, g][0][:, P * t : P * (t + 1)].bitcast(FP8X4),
                             lhsT_scale=x_q[b, g][1][:, P * t : P * (t + 1)],
-                            rhs=a_q[k // 2][0][:, cols].bitcast(FP8X4),
-                            rhs_scale=a_q[k // 2][1][:, cols],
+                            rhs=a_q[k][0][:, cols].bitcast(FP8X4),
+                            rhs_scale=a_q[k][1][:, cols],
                             start=(t == 0 and g == 0),
                             stop=(t == 3 and g == 1),
                         )
 
-        def empty_g(b, k, copy):
-            if (b, k // 4) not in g_il:
-                g_il[b, k // 4] = ring("g_il", G_BUFS, [P, 4, P, 4], BF16)
-            copy(
-                out=g_il[b, k // 4][:, k % 4, :, :].rearrange("p (w i) t -> p w t i", i=2),
-                in_=g_bank[b, k][:].rearrange("p t (w i) -> p w t i", i=2),
-            )
-            give_bank(("g", b, k))
+        def empty_g(b, k0, n, copy=scalar):
+            for k in range(k0, k0 + n):
+                if (b, k // 4) not in g_il:
+                    g_il[b, k // 4] = ring("g_il", G_BUFS, [P, 4, P, 4], BF16)[:]
+                copy(
+                    out=g_il[b, k // 4][:, k % 4, :, :].rearrange("p (w i) t -> p w t i", i=2),
+                    in_=g_bank[b, k][:].rearrange("p t (w i) -> p w t i", i=2),
+                )
+                give_bank(("g", b, k))
 
         def quantize_g(b, k0, n):
             src = g_il[b, k0 // 4][:, k0 % 4 : k0 % 4 + n, :, :]
-            g_q[b, k0] = quantize("g%d" % n, 6 if n == 4 else 3, src.rearrange("p k v t -> p (k v t)"), n * P, G_ROW, SHIFT)
+            codes, scales = quantize("g%d" % n, 4 if n == 4 else 3, src.rearrange("p k v t -> p (k v t)"), n * P, G_ROW, SHIFT)
+            g_q[b, k0] = codes, scales
 
         def project(b, k0, n):
+            for first in range(k0, k0 + n, 2):
+                y_bank[b, first] = take_bank(("y", b, first), [P, min(n, 2), 2 * HID])
+                for k in range(first, first + min(n, 2)):
+                    cols = slice(P * (k - k0), P * (k - k0 + 1))
+                    nc.tensor.matmul_mx(
+                        out=y_bank[b, first][:, k - first, :],
+                        lhsT=g_q[b, k0][0][:, cols].bitcast(FP8X4),
+                        lhsT_scale=g_q[b, k0][1][:, cols],
+                        rhs=w_words[:].bitcast(FP8X4),
+                        rhs_scale=w_scales[:],
+                        start=(k == first),
+                        stop=(k == first + min(n, 2) - 1),
+                    )
+
+        def add_bias(b, k0, n):
+            z[b, k0] = ring("z%d_" % n, Z_BUFS if n == 4 else 4, [P, n, 2 * HID], F32)
+            for first in range(k0, k0 + n, 2):
+                m = min(n, 2)
+                nc.vector.tensor_tensor(
+                    out=z[b, k0][:, first - k0 : first - k0 + m, :],
+                    in0=y_bank[b, first][:],
+                    in1=bias_row[:].unsqueeze(1).to_broadcast([P, m, 2 * HID]),
+                    op=ADD,
+                )
+                give_bank(("y", b, first))
+
+        def sigmoid(b, k0, n):
+            gate[b, k0] = ring("gate", 5, [P, n, HID], F32)
+            nc.scalar.activation(out=gate[b, k0][:], in_=z[b, k0][:, :, HID:], func=ACT.Sigmoid)
+
+        def result(b, k0, n):
+            if (b, k0 // 4) not in rows:
+                rows[b, k0 // 4] = const.tile([P, 4, HID], F32, name="x_raw%d_%d" % (b, k0 // 4), align_bytes=64)
+            return rows[b, k0 // 4][:, k0 % 4 : k0 % 4 + n, :]
+
+        def store(b, k0, n, lo=0):
+            done = result(b, k0 + lo, n)
+            nc.vector.tensor_tensor(out=done, in0=z[b, k0][:, lo : lo + n, :HID], in1=gate[b, k0][:, lo : lo + n, :], op=MULT)
+            nc.sync.dma_start(out=out_view[b][:, k0 + lo : k0 + lo + n, :], in_=done)
+
+        def project_t(b, k0, n):
             for half in (1, 0):
                 y_bank[b, k0, half] = take_bank(("y", b, k0, half), [P, n * P])
                 nc.tensor.matmul_mx(
@@ -168,7 +225,7 @@ def tile_stsgcm_pa_t_w8_kernel(tc, x, A_bytes, A_scale, W0_words, W0_scales, b0,
                     stop=True,
                 )
 
-        def sigmoid(b, k0, n):
+        def sigmoid_t(b, k0, n):
             gate[b, k0] = ring("gate", 5, [P, n * P], F32)
             nc.scalar.activation(out=gate[b, k0][:], in_=y_bank[b, k0, 1][:], func=ACT.Sigmoid, bias=bias_col[:, 1:2])
             give_bank(("y", b, k0, 1))
@@ -185,47 +242,16 @@ def tile_stsgcm_pa_t_w8_kernel(tc, x, A_bytes, A_scale, W0_words, W0_scales, b0,
             for k in range(n):
                 nc.tensor.transpose(o_bank[b, k0][:, k, :], gated[b, k0][:, P * k : P * (k + 1)], ident[:])
 
-        def store(b, k0, n, copy):
-            rows = ring("rows", 6, [P, n, HID], F32)
-            copy(out=rows[:], in_=o_bank[b, k0][:])
+        def store_t(b, k0, n, copy=scalar):
+            done = result(b, k0, n)
+            copy(out=done, in_=o_bank[b, k0][:])
             give_bank(("o", b, k0))
-            nc.sync.dma_start(out=out_view[b][:, k0 : k0 + n, :], in_=rows[:])
+            nc.sync.dma_start(out=out_view[b][:, k0 : k0 + n, :], in_=done)
 
-        def project_direct(b, k0, n):
-            for first in range(k0, k0 + n, 2):
-                y_bank[b, first] = take_bank(("y", b, first), [P, min(n, 2), 2 * HID])
-                for k in range(first, first + min(n, 2)):
-                    cols = slice(P * (k - k0), P * (k - k0 + 1))
-                    nc.tensor.matmul_mx(
-                        out=y_bank[b, first][:, k - first, :],
-                        lhsT=g_q[b, k0][0][:, cols].bitcast(FP8X4),
-                        lhsT_scale=g_q[b, k0][1][:, cols],
-                        rhs=w_words[:].bitcast(FP8X4),
-                        rhs_scale=w_scales[:],
-                        start=(k == first),
-                        stop=(k == first + min(n, 2) - 1),
-                    )
-
-        def add_bias(b, k0, n):
-            z[b, k0] = ring("z%d_" % n, 2 if n == 4 else 4, [P, n, 2 * HID], F32)
-            for first in range(k0, k0 + n, 2):
-                m = min(n, 2)
-                nc.vector.tensor_tensor(
-                    out=z[b, k0][:, first - k0 : first - k0 + m, :],
-                    in0=y_bank[b, first][:],
-                    in1=bias_row[:].unsqueeze(1).to_broadcast([P, m, 2 * HID]),
-                    op=ADD,
-                )
-                give_bank(("y", b, first))
-
-        def sigmoid_direct(b, k0, n):
-            gate[b, k0] = ring("gate", 5, [P, n, HID], F32)
-            nc.scalar.activation(out=gate[b, k0][:], in_=z[b, k0][:, :, HID:], func=ACT.Sigmoid)
-
-        def store_direct(b, k0, n):
-            rows = ring("rows", 6, [P, n, HID], F32)
-            nc.vector.tensor_tensor(out=rows[:], in0=z[b, k0][:, :, :HID], in1=gate[b, k0][:], op=MULT)
-            nc.sync.dma_start(out=out_view[b][:, k0 : k0 + n, :], in_=rows[:])
+        def pool_store(b, k0, n, name, lo=0):
+            done = work.tile([P, n, HID], F32, name=name, bufs=1, align_bytes=64)
+            nc.gpsimd.tensor_tensor(out=done[:], in0=z[b, k0][:, lo : lo + n, :HID], in1=gate[b, k0][:, lo : lo + n, :], op=MULT)
+            nc.sync.dma_start(out=out_view[b][:, k0 + lo : k0 + lo + n, :], in_=done[:])
 
         warm = const.tile([P, 1], F32, name="warm")
         nc.vector.memset(warm[:], 0.0)
@@ -254,15 +280,15 @@ def tile_stsgcm_pa_t_w8_kernel(tc, x, A_bytes, A_scale, W0_words, W0_scales, b0,
         def load_bias_row():
             nc.sync.dma_start(out=bias_row[:], in_=b0.partition_broadcast(P))
 
-        load_a(0)
+        load_a(0, 2)
         load_x(0, 0)
         load_scale()
-        load_a(1)
+        load_a(2, 2)
         load_x(0, 1)
         load_x(1, 0)
-        load_a(2)
+        load_a(4, 2)
         load_x(1, 1)
-        load_a(3)
+        load_a(6, 2)
         load_x(2, 0)
         load_x(2, 1)
         load_w()
@@ -271,19 +297,20 @@ def tile_stsgcm_pa_t_w8_kernel(tc, x, A_bytes, A_scale, W0_words, W0_scales, b0,
                 load_x(b, g)
         load_bias_row()
 
-        def shared(b, g, cut):
-            new_il(b, g, "x_il_shared", 1)
-            interleave(b, g, 0, cut, pool_copy)
+        def pool_start(b, g, cut):
+            x_il[b, g] = operand("shared", 1)
+            interleave(b, g, 0, cut, pool)
 
         widen_a(0, scalar)
         widen_a(1, vector)
-        new_il(0, 0)
+        x_il[0, 0] = operand("x_il", 3)
         interleave(0, 0, 0, P, vector)
-        shared(0, 1, HEAD_POOL)
+        pool_start(0, 1, HEAD_POOL)
         turn_a(0)
         turn_a(1)
         widen_a(2, scalar)
         quantize_x(0, 0)
+        a_il[0] = operand("a_il", 2)
         scale_a(0)
         scale_a(1)
         interleave(0, 1, HEAD_POOL, P, scalar)
@@ -294,8 +321,9 @@ def tile_stsgcm_pa_t_w8_kernel(tc, x, A_bytes, A_scale, W0_words, W0_scales, b0,
         turn_a(4)
         widen_a(5, scalar)
         quantize_x(0, 1)
-        shared(1, 0, HEAD_POOL)
-        quantize_a(0)
+        pool_start(1, 0, HEAD_POOL)
+        quantize_a(0, 2)
+        a_il[1] = operand("a_il", 2)
         scale_a(2)
         scale_a(3)
         interleave(1, 0, HEAD_POOL, P, scalar)
@@ -305,161 +333,158 @@ def tile_stsgcm_pa_t_w8_kernel(tc, x, A_bytes, A_scale, W0_words, W0_scales, b0,
         turn_a(6)
         widen_a(7, scalar)
         quantize_x(1, 0)
-        shared(1, 1, HEAD_POOL)
-        quantize_a(1)
+        pool_start(1, 1, HEAD_POOL)
+        quantize_a(2, 2)
+        a_il[2] = operand("a_il", 2)
         scale_a(4)
         scale_a(5)
         interleave(1, 1, HEAD_POOL, P, scalar)
         aggregate(0, 2, 2)
         turn_a(7)
         aggregate(1, 0, 2, (0,))
-        empty_g(0, 0, scalar)
-        empty_g(0, 1, scalar)
+        empty_g(0, 0, 2)
         aggregate(1, 2, 2, (0,))
-        empty_g(0, 2, scalar)
-        empty_g(0, 3, scalar)
+        empty_g(0, 2, 2)
         quantize_x(1, 1)
-        shared(2, 0, HEAD_POOL)
-        quantize_a(2)
+        pool_start(2, 0, HEAD_POOL)
+        quantize_a(4, 2)
+        a_il[3] = operand("a_il", 2)
         scale_a(6)
         scale_a(7)
         aggregate(1, 0, 2, (1,))
         interleave(2, 0, HEAD_POOL, P, scalar)
         aggregate(1, 2, 2, (1,))
-        empty_g(1, 0, scalar)
-        empty_g(1, 1, scalar)
+        empty_g(1, 0, 2)
         quantize_x(2, 0)
-        quantize_a(3)
+        quantize_a(6, 2)
         aggregate(0, 4, 2)
-        empty_g(1, 2, scalar)
-        empty_g(1, 3, scalar)
+        empty_g(1, 2, 2)
         quantize_g(0, 0, 4)
-        new_il(2, 1, "x_il_shared", 1)
+        x_il[2, 1] = operand("shared", 1)
         interleave(2, 1, 0, P, vector)
         aggregate(1, 4, 2)
-        empty_g(0, 4, scalar)
-        empty_g(0, 5, scalar)
+        empty_g(0, 4, 2)
         quantize_g(1, 0, 4)
         quantize_x(2, 1)
-        shared(3, 1, POOL)
+        pool_start(3, 1, POOL)
         aggregate(0, 6, 2)
-        project(0, 0, 4)
-        empty_g(1, 4, scalar)
-        empty_g(1, 5, scalar)
-        new_il(3, 0)
+        project_t(0, 0, 4)
+        empty_g(1, 4, 2)
+        x_il[3, 0] = operand("x_il", 3)
         interleave(3, 0, 0, HEAD_SHARE, scalar)
         interleave(3, 0, HEAD_SHARE, P, vector)
-        sigmoid(0, 0, 4)
+        sigmoid_t(0, 0, 4)
         aggregate(1, 6, 2)
-        project(1, 0, 4)
-        empty_g(0, 6, scalar)
-        empty_g(0, 7, scalar)
+        project_t(1, 0, 4)
+        empty_g(0, 6, 2)
         multiply(0, 0, 4)
-        empty_g(1, 6, vector)
-        sigmoid(1, 0, 4)
+        empty_g(1, 6, 1, vector)
+        sigmoid_t(1, 0, 4)
         multiply(1, 0, 4)
-        empty_g(1, 7, scalar)
+        empty_g(1, 7, 1)
         turned = [(0, 0, 4), (1, 0, 4)]
         direct = None
         for b in range(2, BATCH - 1):
             first, second = ((0, 4, 4), (1, 4, 4)) if b == 2 else ((b - 1, 0, 4), (b - 1, 4, 4))
-            if b > 2:
-                new_il(b + 1, 0)
-                interleave(b + 1, 0, SHARE, P, vector)
+            last = b + 2 == BATCH
             interleave(b + 1, 1, POOL, P, vector)
+            if b > 2:
+                interleave(b + 1, 0, SHARE, P, vector)
             aggregate(b, 0, 2)
             if direct:
-                sigmoid_direct(*direct)
-            if b > 2:
-                interleave(b + 1, 0, 0, SHARE, scalar)
-            empty_g(b, 0, scalar)
-            empty_g(b, 1, scalar)
+                sigmoid(*direct)
+            empty_g(b, 0, 2)
             if b == 2:
                 quantize_g(*first)
             quantize_g(*second)
-            quantize_x(b + 1, 0)
-            if direct:
-                store_direct(*direct)
-            quantize_x(b + 1, 1)
-            if b + 2 < BATCH:
-                shared(b + 2, 1, POOL)
+            if b == 2:
+                quantize_x(3, 0)
+                quantize_x(3, 1)
+            else:
+                quantize_entry(b + 1)
+            if last:
+                pool_store(*direct, "shared0")
+            else:
+                both_passes(b + 2)
+                interleave(b + 2, 1, 0, POOL, pool)
+                if direct:
+                    store(*direct)
             aggregate(b, 2, 2)
             run = turned if len(turned) == 2 else []
             for group in run:
                 turn_out(*group)
-            empty_g(b, 2, scalar)
-            empty_g(b, 3, scalar)
+            empty_g(b, 2, 2)
             quantize_g(b, 0, 4)
             aggregate(b, 4, 2)
             for group in run:
-                store(*group, scalar)
-            project(*second)
-            project_direct(*first)
-            empty_g(b, 4, scalar)
-            sigmoid(*second)
-            empty_g(b, 5, scalar)
-            add_bias(*first)
-            multiply(*second)
+                store_t(*group)
+            if last:
+                project(*first)
+                project(*second)
+                empty_g(b, 4, 2)
+                add_bias(*first)
+                add_bias(*second)
+            else:
+                project_t(*second)
+                project(*first)
+                empty_g(b, 4, 1)
+                sigmoid_t(*second)
+                empty_g(b, 5, 1)
+                interleave(b + 2, 0, 0, SHARE, scalar)
+                add_bias(*first)
+                multiply(*second)
             aggregate(b, 6, 2)
-            empty_g(b, 6, scalar)
-            empty_g(b, 7, scalar)
+            empty_g(b, 6, 1)
+            if last:
+                sigmoid(*first)
+            empty_g(b, 7, 1)
             turned = turned[len(run) :] + [second]
             direct = first
         b = BATCH - 1
         before = (b - 1, 4, 4)
         aggregate(b, 0, 2)
-        sigmoid_direct(*direct)
-        project_direct(b - 1, 0, 4)
-        for group in turned:
-            turn_out(*group)
+        project(b - 1, 0, 4)
+        sigmoid(b - 2, 4, 4)
+        store(b - 2, 0, 4)
         quantize_g(*before)
-        store_direct(*direct)
-        empty_g(b, 0, scalar)
-        empty_g(b, 1, scalar)
-        add_bias(b - 1, 0, 2)
+        empty_g(b, 0, 2)
+        add_bias(b - 1, 0, 4)
         quantize_g(b, 0, 2)
-        add_bias(b - 1, 2, 2)
-        for group in turned:
-            store(*group, scalar)
         aggregate(b, 2, 2)
-        project(*before)
-        project_direct(b, 0, 2)
-        empty_g(b, 2, scalar)
-        empty_g(b, 3, scalar)
-        sigmoid_direct(b - 1, 0, 2)
-        sigmoid(*before)
-        aggregate(b, 4, 2)
-        add_bias(b, 0, 2)
+        project_t(*before)
+        project(b, 0, 2)
+        store(b - 2, 4, 4)
+        empty_g(b, 2, 2)
+        sigmoid_t(*before)
+        sigmoid(b - 1, 0, 4)
         quantize_g(b, 2, 2)
-        store_direct(b - 1, 0, 2)
+        add_bias(b, 0, 2)
+        aggregate(b, 4, 2)
+        project(b, 2, 2)
         multiply(*before)
-        sigmoid_direct(b - 1, 2, 2)
-        empty_g(b, 4, scalar)
-        empty_g(b, 5, scalar)
-        sigmoid_direct(b, 0, 2)
-        project_direct(b, 2, 2)
-        aggregate(b, 6, 2)
-        turn_out(*before)
-        store_direct(b - 1, 2, 2)
+        store(b - 1, 0, 4)
+        empty_g(b, 4, 2)
+        sigmoid(b, 0, 2)
         add_bias(b, 2, 2)
+        aggregate(b, 6, 2)
         quantize_g(b, 4, 2)
-        store_direct(b, 0, 2)
-        empty_g(b, 6, scalar)
-        empty_g(b, 7, scalar)
-        sigmoid_direct(b, 2, 2)
-        store(*before, scalar)
-        project_direct(b, 4, 2)
+        store(b, 0, 2)
+        turn_out(*before)
+        project(b, 4, 2)
+        empty_g(b, 6, 2)
+        sigmoid(b, 2, 2)
         quantize_g(b, 6, 1)
-        project_direct(b, 6, 1)
+        project(b, 6, 1)
         quantize_g(b, 7, 1)
-        project_direct(b, 7, 1)
+        project(b, 7, 1)
         add_bias(b, 4, 2)
-        sigmoid_direct(b, 4, 2)
+        store_t(*before)
+        sigmoid(b, 4, 2)
+        store(b, 2, 2)
         add_bias(b, 6, 1)
         add_bias(b, 7, 1)
-        store_direct(b, 2, 2)
-        sigmoid_direct(b, 6, 1)
-        sigmoid_direct(b, 7, 1)
-        store_direct(b, 4, 2)
-        store_direct(b, 6, 1)
-        store_direct(b, 7, 1)
+        sigmoid(b, 6, 1)
+        sigmoid(b, 7, 1)
+        store(b, 4, 2)
+        store(b, 6, 1)
+        store(b, 7, 1)

@@ -31,6 +31,7 @@ SHIFT = 64
 X_ROW = 8
 A_ROW = 4
 G_ROW = 4
+FIRST_SHARE = 32
 
 
 def tile_stsgcm_pa_t_w8_kernel(tc, x, A_bytes, A_scale, W0_words, W0_scales, b0, out):
@@ -114,7 +115,7 @@ def tile_stsgcm_pa_t_w8_kernel(tc, x, A_bytes, A_scale, W0_words, W0_scales, b0,
                 x_q[b, g] = codes[:, CHAN * g : CHAN * (g + 1)], scales[:, CHAN * g : CHAN * (g + 1)]
 
         def widen_a(k, copy):
-            a_val[k] = ring("a_val", A_VALS, [P, NODES], BF16)
+            a_val[k] = ring("a_val", A_VALS, [P, NODES], BF16, 256)
             copy(out=a_val[k][:], in_=a_raw[k].bitcast(FP8))
 
         def turn_a(k):
@@ -122,7 +123,7 @@ def tile_stsgcm_pa_t_w8_kernel(tc, x, A_bytes, A_scale, W0_words, W0_scales, b0,
             words = a_val[k][:].bitcast(F32)
             for g in range(2):
                 for u in range(2):
-                    nc.tensor.transpose(a_bank[k][:, u, g, :], words[:, 256 * g + u : 256 * (g + 1) : 2], ident[:])
+                    nc.tensor.transpose(a_bank[k][:, u, g, :], words[:, 256 * g + u : 256 * (g + 1) : 2], ident)
 
         def scale_a(k):
             nc.vector.tensor_tensor(
@@ -231,7 +232,7 @@ def tile_stsgcm_pa_t_w8_kernel(tc, x, A_bytes, A_scale, W0_words, W0_scales, b0,
             give_bank(("y", b, k0, 1))
 
         def multiply(b, k0, n):
-            gated[b, k0] = ring("gated", 4, [P, n * P], F32)
+            gated[b, k0] = ring("gated", 4, [P, n * P], F32, 256)
             nc.vector.scalar_tensor_tensor(
                 out=gated[b, k0][:], in0=y_bank[b, k0, 0][:], scalar=bias_col[:, 0:1], in1=gate[b, k0][:], op0=ADD, op1=MULT
             )
@@ -240,7 +241,7 @@ def tile_stsgcm_pa_t_w8_kernel(tc, x, A_bytes, A_scale, W0_words, W0_scales, b0,
         def turn_out(b, k0, n):
             o_bank[b, k0] = take_bank(("o", b, k0), [P, n, P])
             for k in range(n):
-                nc.tensor.transpose(o_bank[b, k0][:, k, :], gated[b, k0][:, P * k : P * (k + 1)], ident[:])
+                nc.tensor.transpose(o_bank[b, k0][:, k, :], gated[b, k0][:, P * k : P * (k + 1)], ident)
 
         def store_t(b, k0, n, copy=scalar):
             done = result(b, k0, n)
@@ -258,8 +259,8 @@ def tile_stsgcm_pa_t_w8_kernel(tc, x, A_bytes, A_scale, W0_words, W0_scales, b0,
         nc.scalar.activation(out=warm[:], in_=warm[:], func=ACT.Sigmoid)
         w_scales = const.tile([P, 2 * HID], U8, name="w_scales", align_bytes=256)
         nc.vector.memset(w_scales[:].bitcast(I32), 0)
-        ident = const.tile([P, P], F32, name="ident")
-        make_identity(nc, ident[:])
+        ident = const.tile([P, P + 64], F32, name="ident", align_bytes=256)[:, SHIFT // 4 : SHIFT // 4 + P]
+        make_identity(nc, ident)
         a_scale = const.tile([P, 2, 4], F32, name="a_scale")
         w_words = const.tile([P, 2 * HID], U32, name="w_words", align_bytes=256)
         bias_col = const.tile([P, 2], BF16, name="bias_col")
@@ -304,7 +305,8 @@ def tile_stsgcm_pa_t_w8_kernel(tc, x, A_bytes, A_scale, W0_words, W0_scales, b0,
         widen_a(0, scalar)
         widen_a(1, vector)
         x_il[0, 0] = operand("x_il", 3)
-        interleave(0, 0, 0, P, vector)
+        interleave(0, 0, FIRST_SHARE, P, vector)
+        interleave(0, 0, 0, FIRST_SHARE, scalar)
         pool_start(0, 1, HEAD_POOL)
         turn_a(0)
         turn_a(1)

@@ -32,6 +32,7 @@ X_ROW = 8
 A_ROW = 4
 G_ROW = 4
 FIRST_SHARE = 32
+RUNS = (4, 6)
 
 
 def tile_stsgcm_pa_t_w8_kernel(tc, x, A_bytes, A_scale, W0_words, W0_scales, b0, out):
@@ -296,7 +297,8 @@ def tile_stsgcm_pa_t_w8_kernel(tc, x, A_bytes, A_scale, W0_words, W0_scales, b0,
         for b in range(3, BATCH):
             for g in range(2):
                 load_x(b, g)
-        load_bias_row()
+            if b == 3:
+                load_bias_row()
 
         def pool_start(b, g, cut):
             x_il[b, g] = operand("shared", 1)
@@ -377,15 +379,13 @@ def tile_stsgcm_pa_t_w8_kernel(tc, x, A_bytes, A_scale, W0_words, W0_scales, b0,
         interleave(3, 0, HEAD_SHARE, P, vector)
         sigmoid_t(0, 0, 4)
         aggregate(1, 6, 2)
-        project_t(1, 0, 4)
+        project(1, 0, 4)
         empty_g(0, 6, 2)
         multiply(0, 0, 4)
-        empty_g(1, 6, 1, vector)
-        sigmoid_t(1, 0, 4)
-        multiply(1, 0, 4)
-        empty_g(1, 7, 1)
-        turned = [(0, 0, 4), (1, 0, 4)]
-        direct = None
+        add_bias(1, 0, 4)
+        empty_g(1, 6, 2)
+        turned = [(0, 0, 4)]
+        direct = (1, 0, 4)
         for b in range(2, BATCH - 1):
             first, second = ((0, 4, 4), (1, 4, 4)) if b == 2 else ((b - 1, 0, 4), (b - 1, 4, 4))
             last = b + 2 == BATCH
@@ -409,10 +409,9 @@ def tile_stsgcm_pa_t_w8_kernel(tc, x, A_bytes, A_scale, W0_words, W0_scales, b0,
             else:
                 both_passes(b + 2)
                 interleave(b + 2, 1, 0, POOL, pool)
-                if direct:
-                    store(*direct)
+                store(*direct)
             aggregate(b, 2, 2)
-            run = turned if len(turned) == 2 else []
+            run = turned if b in RUNS else []
             for group in run:
                 turn_out(*group)
             empty_g(b, 2, 2)

@@ -20,13 +20,14 @@ PAIR = 2 * P
 FLOPS = 2 * NODES * NODES * BATCH * CHAN + 2 * NODES * BATCH * CHAN * 2 * HID
 
 HEAD_POOL = 76
-POOL = 56
+POOL = 60
 SHARE = 20
 HEAD_SHARE = 40
-G_BUFS = 5
+G_BUFS = 3
 Z_BUFS = 3
 X_CODES = 6
 A_VALS = 3
+WHOLE = (3, 4, 5)
 SHIFT = 64
 X_ROW = 8
 A_ROW = 4
@@ -82,8 +83,8 @@ def tile_stsgcm_pa_t_w8_kernel(tc, x, A_bytes, A_scale, W0_words, W0_scales, b0,
                 a_raw[k0 + k] = tiles[:, k, :]
 
         def quantize(name, bufs, src, cols, row, shift=0):
-            codes = ring(name + "_codes", bufs, [P, cols + 64], U32, 256)[:, shift // 4 : shift // 4 + cols]
-            scales = ring(name + "_scales", bufs, [P, cols + 256], U8, 256)[row:, shift : shift + cols]
+            codes = ring(name + "_codes", bufs, [P, cols + shift // 4], U32, 256)[:, shift // 4 : shift // 4 + cols]
+            scales = ring(name + "_scales", bufs, [P, cols + shift], U8, 256)[row:, shift : shift + cols]
             nc.vector.quantize_mx(out=codes.bitcast(FP8X4), scales=scales, in_=src)
             return codes, scales
 
@@ -160,18 +161,23 @@ def tile_stsgcm_pa_t_w8_kernel(tc, x, A_bytes, A_scale, W0_words, W0_scales, b0,
 
         def empty_g(b, k0, n, copy=scalar):
             for k in range(k0, k0 + n):
-                if (b, k // 4) not in g_il:
-                    g_il[b, k // 4] = ring("g_il", G_BUFS, [P, 4, P, 4], BF16)[:]
+                if b not in g_il:
+                    g_il[b] = ring("g_il", G_BUFS, [P, 8, P, 4], BF16)
                 copy(
-                    out=g_il[b, k // 4][:, k % 4, :, :].rearrange("p (w i) t -> p w t i", i=2),
+                    out=g_il[b][:, k, :, :].rearrange("p (w i) t -> p w t i", i=2),
                     in_=g_bank[b, k][:].rearrange("p t (w i) -> p w t i", i=2),
                 )
                 give_bank(("g", b, k))
 
         def quantize_g(b, k0, n):
-            src = g_il[b, k0 // 4][:, k0 % 4 : k0 % 4 + n, :, :]
-            codes, scales = quantize("g%d" % n, 4 if n == 4 else 3, src.rearrange("p k v t -> p (k v t)"), n * P, G_ROW, SHIFT)
+            src = g_il[b][:, k0 : k0 + n, :, :]
+            codes, scales = quantize("g%d" % n, 3 if n == 4 else 2, src.rearrange("p k v t -> p (k v t)"), n * P, G_ROW, SHIFT)
             g_q[b, k0] = codes, scales
+
+        def quantize_whole(b):
+            codes, scales = quantize("gg", 2, g_il[b][:].rearrange("p k v t -> p (k v t)"), 8 * P, 0, SHIFT)
+            for k0 in (0, 4):
+                g_q[b, k0] = codes[:, P * k0 : P * (k0 + 4)], scales[:, P * k0 : P * (k0 + 4)]
 
         def project(b, k0, n):
             for first in range(k0, k0 + n, 2):
@@ -189,7 +195,7 @@ def tile_stsgcm_pa_t_w8_kernel(tc, x, A_bytes, A_scale, W0_words, W0_scales, b0,
                     )
 
         def add_bias(b, k0, n):
-            z[b, k0] = ring("z%d_" % n, Z_BUFS if n == 4 else 4, [P, n, 2 * HID], F32)
+            z[b, k0] = ring("z%d_" % n, Z_BUFS if n > 1 else 2, [P, n, 2 * HID], F32)
             for first in range(k0, k0 + n, 2):
                 m = min(n, 2)
                 nc.vector.tensor_tensor(
@@ -201,7 +207,7 @@ def tile_stsgcm_pa_t_w8_kernel(tc, x, A_bytes, A_scale, W0_words, W0_scales, b0,
                 give_bank(("y", b, first))
 
         def sigmoid(b, k0, n):
-            gate[b, k0] = ring("gate", 5, [P, n, HID], F32)
+            gate[b, k0] = ring("gate", 4, [P, n, HID], F32)
             nc.scalar.activation(out=gate[b, k0][:], in_=z[b, k0][:, :, HID:], func=ACT.Sigmoid)
 
         def result(b, k0, n):
@@ -228,12 +234,12 @@ def tile_stsgcm_pa_t_w8_kernel(tc, x, A_bytes, A_scale, W0_words, W0_scales, b0,
                 )
 
         def sigmoid_t(b, k0, n):
-            gate[b, k0] = ring("gate", 5, [P, n * P], F32)
+            gate[b, k0] = ring("gate", 4, [P, n * P], F32)
             nc.scalar.activation(out=gate[b, k0][:], in_=y_bank[b, k0, 1][:], func=ACT.Sigmoid, bias=bias_col[:, 1:2])
             give_bank(("y", b, k0, 1))
 
         def multiply(b, k0, n):
-            gated[b, k0] = ring("gated", 4, [P, n * P], F32, 256)
+            gated[b, k0] = ring("gated", 3, [P, n * P], F32, 256)
             nc.vector.scalar_tensor_tensor(
                 out=gated[b, k0][:], in0=y_bank[b, k0, 0][:], scalar=bias_col[:, 0:1], in1=gate[b, k0][:], op0=ADD, op1=MULT
             )
@@ -393,12 +399,17 @@ def tile_stsgcm_pa_t_w8_kernel(tc, x, A_bytes, A_scale, W0_words, W0_scales, b0,
             if b > 2:
                 interleave(b + 1, 0, SHARE, P, vector)
             aggregate(b, 0, 2)
-            if direct:
+            if b > 2:
                 sigmoid(*direct)
             empty_g(b, 0, 2)
             if b == 2:
+                sigmoid(*direct)
+            if b == 2:
                 quantize_g(*first)
-            quantize_g(*second)
+            if b - 1 in WHOLE:
+                quantize_whole(b - 1)
+            else:
+                quantize_g(*second)
             if b == 2:
                 quantize_x(3, 0)
                 quantize_x(3, 1)
@@ -415,13 +426,16 @@ def tile_stsgcm_pa_t_w8_kernel(tc, x, A_bytes, A_scale, W0_words, W0_scales, b0,
             for group in run:
                 turn_out(*group)
             empty_g(b, 2, 2)
-            quantize_g(b, 0, 4)
+            if b not in WHOLE:
+                quantize_g(b, 0, 4)
             aggregate(b, 4, 2)
             for group in run:
                 store_t(*group)
             if last:
                 project(*first)
+                aggregate(b, 6, 1)
                 project(*second)
+                aggregate(b, 7, 1)
                 empty_g(b, 4, 2)
                 add_bias(*first)
                 add_bias(*second)
@@ -434,7 +448,7 @@ def tile_stsgcm_pa_t_w8_kernel(tc, x, A_bytes, A_scale, W0_words, W0_scales, b0,
                 interleave(b + 2, 0, 0, SHARE, scalar)
                 add_bias(*first)
                 multiply(*second)
-            aggregate(b, 6, 2)
+                aggregate(b, 6, 2)
             empty_g(b, 6, 1)
             if last:
                 sigmoid(*first)

@@ -34,6 +34,8 @@ A_ROW = 4
 G_ROW = 4
 FIRST_SHARE = 32
 RUNS = (4, 6)
+PAIR_HOME = {(0, 0): "x_raw0_0", (0, 1): "x_raw0_1", (1, 0): "x_pair1_0", (1, 1): "x_pair1_1", (2, 0): "shared0"}
+SINGLE_HOME = {(4, 1): "x_pair2_1", (5, 1): "x_pair3_1", (6, 0): "x_raw1_0", (6, 1): "x_raw1_1", (7, 0): "x_pair2_0", (7, 1): "x_pair3_0"}
 
 
 def tile_stsgcm_pa_t_w8_kernel(tc, x, A_bytes, A_scale, W0_words, W0_scales, b0, out):
@@ -45,6 +47,8 @@ def tile_stsgcm_pa_t_w8_kernel(tc, x, A_bytes, A_scale, W0_words, W0_scales, b0,
         ctx.enter_context(tc.manual_schedule())
 
         x_view = x.rearrange("(g p j) b c -> g b p j c", p=P, j=4)
+        pair_view = x.rearrange("(g p j) (h b) c -> g h p j (b c)", p=P, j=4, b=2)
+        out_pairs = out.rearrange("(k p) (h b) j -> h p k (b j)", p=P, b=2)
         a_view = A_bytes.rearrange("(k p) w -> p k w", p=P)
         out_view = out.rearrange("(k p) b j -> b p k j", p=P)
         vector, scalar = nc.vector.tensor_copy, nc.scalar.copy
@@ -53,6 +57,7 @@ def tile_stsgcm_pa_t_w8_kernel(tc, x, A_bytes, A_scale, W0_words, W0_scales, b0,
         g_bank, g_il, g_q, y_bank, gate, z, gated, o_bank, rows = ({} for i in range(9))
 
         turns = {}
+        filled = {}
 
         def ring(name, size, shape, dtype, align=64):
             turns[name] = turns.get(name, -1) + 1
@@ -75,6 +80,12 @@ def tile_stsgcm_pa_t_w8_kernel(tc, x, A_bytes, A_scale, W0_words, W0_scales, b0,
             else:
                 x_raw[b, g] = const.tile([P, 4, CHAN], BF16, name="x_raw%d_%d" % (b, g), align_bytes=64)
             nc.sync.dma_start(out=x_raw[b, g][:], in_=x_view[g][b])
+
+        def load_pair(h, g):
+            both = const.tile([P, 4, 2 * CHAN], BF16, name="x_pair%d_%d" % (h, g), align_bytes=64)
+            nc.sync.dma_start(out=both[:], in_=pair_view[g][h])
+            for i in range(2):
+                x_raw[2 * h + i, g] = both[:, :, CHAN * i : CHAN * (i + 1)]
 
         def load_a(k0, n):
             tiles = const.tile([P, n, NODES], U8, name="a_raw%d" % k0)
@@ -211,14 +222,29 @@ def tile_stsgcm_pa_t_w8_kernel(tc, x, A_bytes, A_scale, W0_words, W0_scales, b0,
             nc.scalar.activation(out=gate[b, k0][:], in_=z[b, k0][:, :, HID:], func=ACT.Sigmoid)
 
         def result(b, k0, n):
-            if (b, k0 // 4) not in rows:
-                rows[b, k0 // 4] = const.tile([P, 4, HID], F32, name="x_raw%d_%d" % (b, k0 // 4), align_bytes=64)
-            return rows[b, k0 // 4][:, k0 % 4 : k0 % 4 + n, :]
+            half = k0 // 4
+            if (b, half) in SINGLE_HOME:
+                if (b, half) not in rows:
+                    rows[b, half] = const.tile([P, 4, HID], F32, name=SINGLE_HOME[b, half], align_bytes=64)
+                return rows[b, half][:, k0 % 4 : k0 % 4 + n, :]
+            key = ("pair", b // 2, half)
+            if key not in rows:
+                home = work if PAIR_HOME[b // 2, half] == "shared0" else const
+                rows[key] = home.tile([P, 4, 2 * HID], F32, name=PAIR_HOME[b // 2, half], bufs=1, align_bytes=64)
+                filled[key] = 0
+            filled[key] = filled[key] + 1
+            return rows[key][:, :, HID * (b % 2) : HID * (b % 2 + 1)]
+
+        def send(b, k0, n, done):
+            if (b, k0 // 4) in SINGLE_HOME:
+                nc.sync.dma_start(out=out_view[b][:, k0 : k0 + n, :], in_=done)
+            elif filled["pair", b // 2, k0 // 4] == 2:
+                nc.sync.dma_start(out=out_pairs[b // 2][:, k0 : k0 + n, :], in_=rows["pair", b // 2, k0 // 4][:])
 
         def store(b, k0, n, lo=0):
             done = result(b, k0 + lo, n)
             nc.vector.tensor_tensor(out=done, in0=z[b, k0][:, lo : lo + n, :HID], in1=gate[b, k0][:, lo : lo + n, :], op=MULT)
-            nc.sync.dma_start(out=out_view[b][:, k0 + lo : k0 + lo + n, :], in_=done)
+            send(b, k0 + lo, n, done)
 
         def project_t(b, k0, n):
             for half in (1, 0):
@@ -254,12 +280,12 @@ def tile_stsgcm_pa_t_w8_kernel(tc, x, A_bytes, A_scale, W0_words, W0_scales, b0,
             done = result(b, k0, n)
             copy(out=done, in_=o_bank[b, k0][:])
             give_bank(("o", b, k0))
-            nc.sync.dma_start(out=out_view[b][:, k0 : k0 + n, :], in_=done)
+            send(b, k0, n, done)
 
-        def pool_store(b, k0, n, name, lo=0):
-            done = work.tile([P, n, HID], F32, name=name, bufs=1, align_bytes=64)
-            nc.gpsimd.tensor_tensor(out=done[:], in0=z[b, k0][:, lo : lo + n, :HID], in1=gate[b, k0][:, lo : lo + n, :], op=MULT)
-            nc.sync.dma_start(out=out_view[b][:, k0 + lo : k0 + lo + n, :], in_=done[:])
+        def pool_store(b, k0, n):
+            done = result(b, k0, n)
+            nc.gpsimd.tensor_tensor(out=done, in0=z[b, k0][:, :, :HID], in1=gate[b, k0][:], op=MULT)
+            send(b, k0, n, done)
 
         warm = const.tile([P, 1], F32, name="warm")
         nc.vector.memset(warm[:], 0.0)
@@ -297,14 +323,13 @@ def tile_stsgcm_pa_t_w8_kernel(tc, x, A_bytes, A_scale, W0_words, W0_scales, b0,
         load_a(4, 2)
         load_x(1, 1)
         load_a(6, 2)
-        load_x(2, 0)
-        load_x(2, 1)
+        load_pair(1, 0)
+        load_pair(1, 1)
         load_w()
-        for b in range(3, BATCH):
+        load_bias_row()
+        for h in range(2, BATCH // 2):
             for g in range(2):
-                load_x(b, g)
-            if b == 3:
-                load_bias_row()
+                load_pair(h, g)
 
         def pool_start(b, g, cut):
             x_il[b, g] = operand("shared", 1)
@@ -416,7 +441,7 @@ def tile_stsgcm_pa_t_w8_kernel(tc, x, A_bytes, A_scale, W0_words, W0_scales, b0,
             else:
                 quantize_entry(b + 1)
             if last:
-                pool_store(*direct, "shared0")
+                pool_store(*direct)
             else:
                 both_passes(b + 2)
                 interleave(b + 2, 1, 0, POOL, pool)

from contextlib import ExitStack

import concourse.mybir as mybir
from concourse.masks import make_identity

F32 = mybir.dt.float32
BF16 = mybir.dt.bfloat16
I32 = mybir.dt.int32
U32 = mybir.dt.uint32
U8 = mybir.dt.uint8
FP8 = mybir.dt.float8_e4m3fn
FP8X4 = mybir.dt.float8_e4m3fn_x4
MULT = mybir.AluOpType.mult
ADD = mybir.AluOpType.add
ACT = mybir.ActivationFunctionType

NODES, BATCH, CHAN, HID = 1024, 8, 512, 128
P = 128
PAIR = 2 * P
FLOPS = 2 * NODES * NODES * BATCH * CHAN + 2 * NODES * BATCH * CHAN * 2 * HID

HEAD_POOL = 76
POOL = 60
SHARE = 20
HEAD_SHARE = 40
G_BUFS = 3
Z_BUFS = 3
X_CODES = 6
A_VALS = 3
WHOLE = (3, 4, 5)
SHIFT = 64
X_ROW = 8
A_ROW = 4
G_ROW = 4
FIRST_SHARE = 32
RUNS = (4, 6)
PAIR_HOME = {(0, 0): "x_raw0_0", (0, 1): "x_raw0_1", (1, 0): "x_pair1_0", (1, 1): "x_pair1_1", (2, 0): "shared0"}
SINGLE_HOME = {(4, 1): "x_pair2_1", (5, 1): "x_pair3_1", (6, 0): "x_raw1_0", (6, 1): "x_raw1_1", (7, 0): "x_pair2_0", (7, 1): "x_pair3_0"}


def tile_stsgcm_pa_t_w8_kernel(tc, x, A_bytes, A_scale, W0_words, W0_scales, b0, out):
    nc = tc.nc
    with ExitStack() as ctx:
        const = ctx.enter_context(tc.tile_pool(name="const", bufs=1))
        work = ctx.enter_context(tc.tile_pool(name="work", bufs=1))
        psum = ctx.enter_context(tc.psum_pool(name="psum", bufs=1))
        ctx.enter_context(tc.manual_schedule())

        x_view = x.rearrange("(g p j) b c -> g b p j c", p=P, j=4)
        pair_view = x.rearrange("(g p j) (h b) c -> g h p j (b c)", p=P, j=4, b=2)
        out_pairs = out.rearrange("(k p) (h b) j -> h p k (b j)", p=P, b=2)
        a_view = A_bytes.rearrange("(k p) w -> p k w", p=P)
        out_view = out.rearrange("(k p) b j -> b p k j", p=P)
        vector, scalar = nc.vector.tensor_copy, nc.scalar.copy

        x_raw, a_raw, x_il, x_q, a_val, a_bank, a_il, a_q = ({} for i in range(8))
        g_bank, g_il, g_q, y_bank, gate, z, gated, o_bank, rows = ({} for i in range(9))

        turns = {}
        filled = {}

        def ring(name, size, shape, dtype, align=64):
            turns[name] = turns.get(name, -1) + 1
            return work.tile(shape, dtype, name="%s%d" % (name, turns[name] % size), bufs=1, align_bytes=align)

        free_banks = list(range(8))
        bank_of = {}

        def take_bank(key, shape):
            bank_of[key] = free_banks[0]
            free_banks.remove(bank_of[key])
            return psum.tile(shape, F32, name="bank%d" % bank_of[key], bufs=1)

        def give_bank(key):
            free_banks.append(bank_of[key])

        def load_x(b, g):
            if (b, g) == (0, 0):
                x_raw[b, g] = ring("shared", 1, [P, 4, CHAN], BF16)
            else:
                x_raw[b, g] = const.tile([P, 4, CHAN], BF16, name="x_raw%d_%d" % (b, g), align_bytes=64)
            nc.sync.dma_start(out=x_raw[b, g][:], in_=x_view[g][b])

        def load_pair(h, g):
            both = const.tile([P, 4, 2 * CHAN], BF16, name="x_pair%d_%d" % (h, g), align_bytes=64)
            nc.sync.dma_start(out=both[:], in_=pair_view[g][h])
            for i in range(2):
                x_raw[2 * h + i, g] = both[:, :, CHAN * i : CHAN * (i + 1)]

        def load_a(k0, n):
            tiles = const.tile([P, n, NODES], U8, name="a_raw%d" % k0)
            nc.sync.dma_start(out=tiles[:], in_=a_view[:, k0 : k0 + n, :])
            for k in range(n):
                a_raw[k0 + k] = tiles[:, k, :]

        def quantize(name, bufs, src, cols, row, shift=0):
            codes = ring(name + "_codes", bufs, [P, cols + shift // 4], U32, 256)[:, shift // 4 : shift // 4 + cols]
            scales = ring(name + "_scales", bufs, [P, cols + shift], U8, 256)[row:, shift : shift + cols]
            nc.vector.quantize_mx(out=codes.bitcast(FP8X4), scales=scales, in_=src)
            return codes, scales

        def pool(out, in_):
            nc.gpsimd.tensor_scalar(out=out, in0=in_, scalar1=1.0, scalar2=0.0, op0=MULT, op1=ADD)

        def operand(name, size, passes=1):
            return ring(name, size, [P, passes * 4 * CHAN], BF16)[:]

        def interleave(b, g, lo, hi, copy):
            dst = x_il[b, g].rearrange("p (t m j) -> p t m j", t=4, j=4)[:, :, lo:hi, :]
            src = x_raw[b, g][:, :, 4 * lo : 4 * hi]
            if copy is pool:
                copy(out=dst.rearrange("p t m j -> p m t j"), in_=src.rearrange("p j (m t) -> p m t j", t=4))
            else:
                copy(out=dst.rearrange("p t (m i) j -> p m j t i", i=2), in_=src.rearrange("p j (m i t) -> p m j t i", i=2, t=4))

        def quantize_x(b, g):
            codes, scales = quantize("x", X_CODES, x_il[b, g], CHAN, X_ROW)
            x_q[b, g] = codes, scales

        def both_passes(b):
            x_il[b] = operand("shared", 1, 2)
            for g in range(2):
                x_il[b, g] = x_il[b][:, 4 * CHAN * g : 4 * CHAN * (g + 1)]

        def quantize_entry(b):
            codes, scales = quantize("xx", 2, x_il[b], 2 * CHAN, 0)
            for g in range(2):
                x_q[b, g] = codes[:, CHAN * g : CHAN * (g + 1)], scales[:, CHAN * g : CHAN * (g + 1)]

        def widen_a(k, copy):
            a_val[k] = ring("a_val", A_VALS, [P, NODES], BF16, 256)
            copy(out=a_val[k][:], in_=a_raw[k].bitcast(FP8))

        def turn_a(k):
            a_bank[k] = take_bank(("a", k), [P, 2, 2, P])
            words = a_val[k][:].bitcast(F32)
            for g in range(2):
                for u in range(2):
                    nc.tensor.transpose(a_bank[k][:, u, g, :], words[:, 256 * g + u : 256 * (g + 1) : 2], ident)

        def scale_a(k):
            nc.vector.tensor_tensor(
                out=a_il[k // 2].rearrange("p (k g v u e) -> p k g v u e", k=2, g=2, u=2, e=2)[:, k % 2],
                in0=a_bank[k][:].rearrange("p u g v -> p (u g v)").bitcast(BF16).rearrange("p (u g v e) -> p g v u e", u=2, g=2, e=2),
                in1=a_scale[:].rearrange("p g (u e) -> p g u e", u=2).unsqueeze(2).to_broadcast([P, 2, P, 2, 2]),
                op=MULT,
            )
            give_bank(("a", k))

        def quantize_a(k0, n):
            src = a_il[k0 // 2][:, 2 * CHAN * (k0 % 2) : 2 * CHAN * (k0 % 2 + n)]
            codes, scales = quantize("a%d_" % k0, 1, src, n * PAIR, A_ROW, SHIFT)
            for k in range(n):
                a_q[k0 + k] = codes[:, PAIR * k : PAIR * (k + 1)], scales[:, PAIR * k : PAIR * (k + 1)]

        def aggregate(b, k0, n, passes=(0, 1)):
            for k in range(k0, k0 + n):
                if 0 in passes:
                    g_bank[b, k] = take_bank(("g", b, k), [P, 4, P])
                for t in range(4):
                    for g in passes:
                        cols = slice(P * g, P * (g + 1))
                        nc.tensor.matmul_mx(
                            out=g_bank[b, k][:, t, :],
                            lhsT=x_q[b, g][0][:, P * t : P * (t + 1)].bitcast(FP8X4),
                            lhsT_scale=x_q[b, g][1][:, P * t : P * (t + 1)],
                            rhs=a_q[k][0][:, cols].bitcast(FP8X4),
                            rhs_scale=a_q[k][1][:, cols],
                            start=(t == 0 and g == 0),
                            stop=(t == 3 and g == 1),
                        )

        def empty_g(b, k0, n, copy=scalar):
            for k in range(k0, k0 + n):
                if b not in g_il:
                    g_il[b] = ring("g_il", G_BUFS, [P, 8, P, 4], BF16)
                copy(
                    out=g_il[b][:, k, :, :].rearrange("p (w i) t -> p w t i", i=2),
                    in_=g_bank[b, k][:].rearrange("p t (w i) -> p w t i", i=2),
                )
                give_bank(("g", b, k))

        def quantize_g(b, k0, n):
            src = g_il[b][:, k0 : k0 + n, :, :]
            codes, scales = quantize("g%d" % n, 3 if n == 4 else 2, src.rearrange("p k v t -> p (k v t)"), n * P, G_ROW, SHIFT)
            g_q[b, k0] = codes, scales

        def quantize_whole(b):
            codes, scales = quantize("gg", 2, g_il[b][:].rearrange("p k v t -> p (k v t)"), 8 * P, 0, SHIFT)
            for k0 in (0, 4):
                g_q[b, k0] = codes[:, P * k0 : P * (k0 + 4)], scales[:, P * k0 : P * (k0 + 4)]

        def project(b, k0, n):
            for first in range(k0, k0 + n, 2):
                y_bank[b, first] = take_bank(("y", b, first), [P, min(n, 2), 2 * HID])
                for k in range(first, first + min(n, 2)):
                    cols = slice(P * (k - k0), P * (k - k0 + 1))
                    nc.tensor.matmul_mx(
                        out=y_bank[b, first][:, k - first, :],
                        lhsT=g_q[b, k0][0][:, cols].bitcast(FP8X4),
                        lhsT_scale=g_q[b, k0][1][:, cols],
                        rhs=w_words[:].bitcast(FP8X4),
                        rhs_scale=w_scales[:],
                        start=(k == first),
                        stop=(k == first + min(n, 2) - 1),
                    )

        def add_bias(b, k0, n):
            z[b, k0] = ring("z%d_" % n, Z_BUFS if n > 1 else 2, [P, n, 2 * HID], F32)
            for first in range(k0, k0 + n, 2):
                m = min(n, 2)
                nc.vector.tensor_tensor(
                    out=z[b, k0][:, first - k0 : first - k0 + m, :],
                    in0=y_bank[b, first][:],
                    in1=bias_row[:].unsqueeze(1).to_broadcast([P, m, 2 * HID]),
                    op=ADD,
                )
                give_bank(("y", b, first))

        def sigmoid(b, k0, n):
            gate[b, k0] = ring("gate", 4, [P, n, HID], F32)
            nc.scalar.activation(out=gate[b, k0][:], in_=z[b, k0][:, :, HID:], func=ACT.Sigmoid)

        def result(b, k0, n):
            half = k0 // 4
            if (b, half) in SINGLE_HOME:
                if (b, half) not in rows:
                    rows[b, half] = const.tile([P, 4, HID], F32, name=SINGLE_HOME[b, half], align_bytes=64)
                return rows[b, half][:, k0 % 4 : k0 % 4 + n, :]
            key = ("pair", b // 2, half)
            if key not in rows:
                home = work if PAIR_HOME[b // 2, half] == "shared0" else const
                rows[key] = home.tile([P, 4, 2 * HID], F32, name=PAIR_HOME[b // 2, half], bufs=1, align_bytes=64)
                filled[key] = 0
            filled[key] = filled[key] + 1
            return rows[key][:, :, HID * (b % 2) : HID * (b % 2 + 1)]

        def send(b, k0, n, done):
            if (b, k0 // 4) in SINGLE_HOME:
                nc.sync.dma_start(out=out_view[b][:, k0 : k0 + n, :], in_=done)
            elif filled["pair", b // 2, k0 // 4] == 2:
                nc.sync.dma_start(out=out_pairs[b // 2][:, k0 : k0 + n, :], in_=rows["pair", b // 2, k0 // 4][:])

        def store(b, k0, n, lo=0):
            done = result(b, k0 + lo, n)
            nc.vector.tensor_tensor(out=done, in0=z[b, k0][:, lo : lo + n, :HID], in1=gate[b, k0][:, lo : lo + n, :], op=MULT)
            send(b, k0 + lo, n, done)

        def project_t(b, k0, n):
            for half in (1, 0):
                y_bank[b, k0, half] = take_bank(("y", b, k0, half), [P, n * P])
                nc.tensor.matmul_mx(
                    out=y_bank[b, k0, half][:],
                    lhsT=w_words[:, HID * half : HID * (half + 1)].bitcast(FP8X4),
                    lhsT_scale=w_scales[:, HID * half : HID * (half + 1)],
                    rhs=g_q[b, k0][0].bitcast(FP8X4),
                    rhs_scale=g_q[b, k0][1],
                    start=True,
                    stop=True,
                )

        def sigmoid_t(b, k0, n):
            gate[b, k0] = ring("gate", 4, [P, n * P], F32)
            nc.scalar.activation(out=gate[b, k0][:], in_=y_bank[b, k0, 1][:], func=ACT.Sigmoid, bias=bias_col[:, 1:2])
            give_bank(("y", b, k0, 1))

        def multiply(b, k0, n):
            gated[b, k0] = ring("gated", 3, [P, n * P], F32, 256)
            nc.vector.scalar_tensor_tensor(
                out=gated[b, k0][:], in0=y_bank[b, k0, 0][:], scalar=bias_col[:, 0:1], in1=gate[b, k0][:], op0=ADD, op1=MULT
            )
            give_bank(("y", b, k0, 0))

        def turn_out(b, k0, n):
            o_bank[b, k0] = take_bank(("o", b, k0), [P, n, P])
            for k in range(n):
                nc.tensor.transpose(o_bank[b, k0][:, k, :], gated[b, k0][:, P * k : P * (k + 1)], ident)

        def store_t(b, k0, n, copy=scalar):
            done = result(b, k0, n)
            copy(out=done, in_=o_bank[b, k0][:])
            give_bank(("o", b, k0))
            send(b, k0, n, done)

        def pool_store(b, k0, n):
            done = result(b, k0, n)
            nc.gpsimd.tensor_tensor(out=done, in0=z[b, k0][:, :, :HID], in1=gate[b, k0][:], op=MULT)
            send(b, k0, n, done)

        warm = const.tile([P, 1], F32, name="warm")
        nc.vector.memset(warm[:], 0.0)
        nc.scalar.activation(out=warm[:], in_=warm[:], func=ACT.Sigmoid)
        w_scales = const.tile([P, 2 * HID], U8, name="w_scales", align_bytes=256)
        nc.vector.memset(w_scales[:].bitcast(I32), 0)
        ident = const.tile([P, P + 64], F32, name="ident", align_bytes=256)[:, SHIFT // 4 : SHIFT // 4 + P]
        make_identity(nc, ident)
        a_scale = const.tile([P, 2, 4], F32, name="a_scale")
        w_words = const.tile([P, 2 * HID], U32, name="w_words", align_bytes=256)
        bias_col = const.tile([P, 2], BF16, name="bias_col")
        bias_row = const.tile([P, 2 * HID], BF16, name="bias_row")

        def load_scale():
            with nc.allow_non_contiguous_dma(reason="four scales a partition and pass"):
                nc.sync.dma_start(out=a_scale[:], in_=A_scale.rearrange("o (g p t) -> (o p) g t", p=P, t=4))

        def load_w():
            nc.sync.dma_start(out=w_words[:].bitcast(I32), in_=W0_words.rearrange("o p n t -> (o p) (n t)").bitcast(I32))
            ws_view = W0_scales.rearrange("o q n -> (o q) n").bitcast(I32)
            for r in range(4):
                nc.sync.dma_start(out=w_scales[32 * r : 32 * r + 4, :].bitcast(I32), in_=ws_view[4 * r : 4 * r + 4, :])
            with nc.allow_non_contiguous_dma(reason="one bias value a partition"):
                nc.sync.dma_start(out=bias_col[:], in_=b0.rearrange("(o p) -> p o", p=P))

        def load_bias_row():
            nc.sync.dma_start(out=bias_row[:], in_=b0.partition_broadcast(P))

        load_a(0, 2)
        load_x(0, 0)
        load_scale()
        load_a(2, 2)
        load_x(0, 1)
        load_x(1, 0)
        load_a(4, 2)
        load_x(1, 1)
        load_a(6, 2)
        load_pair(1, 0)
        load_pair(1, 1)
        load_w()
        load_bias_row()
        for h in range(2, BATCH // 2):
            for g in range(2):
                load_pair(h, g)

        def pool_start(b, g, cut):
            x_il[b, g] = operand("shared", 1)
            interleave(b, g, 0, cut, pool)

        widen_a(0, scalar)
        widen_a(1, vector)
        x_il[0, 0] = operand("x_il", 3)
        interleave(0, 0, FIRST_SHARE, P, vector)
        interleave(0, 0, 0, FIRST_SHARE, scalar)
        pool_start(0, 1, HEAD_POOL)
        turn_a(0)
        turn_a(1)
        widen_a(2, scalar)
        quantize_x(0, 0)
        a_il[0] = operand("a_il", 2)
        scale_a(0)
        scale_a(1)
        interleave(0, 1, HEAD_POOL, P, scalar)
        turn_a(2)
        widen_a(3, scalar)
        turn_a(3)
        widen_a(4, scalar)
        turn_a(4)
        widen_a(5, scalar)
        quantize_x(0, 1)
        pool_start(1, 0, HEAD_POOL)
        quantize_a(0, 2)
        a_il[1] = operand("a_il", 2)
        scale_a(2)
        scale_a(3)
        interleave(1, 0, HEAD_POOL, P, scalar)
        widen_a(6, scalar)
        aggregate(0, 0, 2)
        turn_a(5)
        turn_a(6)
        widen_a(7, scalar)
        quantize_x(1, 0)
        pool_start(1, 1, HEAD_POOL)
        quantize_a(2, 2)
        a_il[2] = operand("a_il", 2)
        scale_a(4)
        scale_a(5)
        interleave(1, 1, HEAD_POOL, P, scalar)
        aggregate(0, 2, 2)
        turn_a(7)
        aggregate(1, 0, 2, (0,))
        empty_g(0, 0, 2)
        aggregate(1, 2, 2, (0,))
        empty_g(0, 2, 2)
        quantize_x(1, 1)
        pool_start(2, 0, HEAD_POOL)
        quantize_a(4, 2)
        a_il[3] = operand("a_il", 2)
        scale_a(6)
        scale_a(7)
        aggregate(1, 0, 2, (1,))
        interleave(2, 0, HEAD_POOL, P, scalar)
        aggregate(1, 2, 2, (1,))
        empty_g(1, 0, 2)
        quantize_x(2, 0)
        quantize_a(6, 2)
        aggregate(0, 4, 2)
        empty_g(1, 2, 2)
        quantize_g(0, 0, 4)
        x_il[2, 1] = operand("shared", 1)
        interleave(2, 1, 0, P, vector)
        aggregate(1, 4, 2)
        empty_g(0, 4, 2)
        quantize_g(1, 0, 4)
        quantize_x(2, 1)
        pool_start(3, 1, POOL)
        aggregate(0, 6, 2)
        project_t(0, 0, 4)
        empty_g(1, 4, 2)
        x_il[3, 0] = operand("x_il", 3)
        interleave(3, 0, 0, HEAD_SHARE, scalar)
        interleave(3, 0, HEAD_SHARE, P, vector)
        sigmoid_t(0, 0, 4)
        aggregate(1, 6, 2)
        project(1, 0, 4)
        empty_g(0, 6, 2)
        multiply(0, 0, 4)
        add_bias(1, 0, 4)
        empty_g(1, 6, 2)
        turned = [(0, 0, 4)]
        direct = (1, 0, 4)
        for b in range(2, BATCH - 1):
            first, second = ((0, 4, 4), (1, 4, 4)) if b == 2 else ((b - 1, 0, 4), (b - 1, 4, 4))
            last = b + 2 == BATCH
            interleave(b + 1, 1, POOL, P, vector)
            if b > 2:
                interleave(b + 1, 0, SHARE, P, vector)
            aggregate(b, 0, 2)
            if b > 2:
                sigmoid(*direct)
            empty_g(b, 0, 2)
            if b == 2:
                sigmoid(*direct)
            if b == 2:
                quantize_g(*first)
            if b - 1 in WHOLE:
                quantize_whole(b - 1)
            else:
                quantize_g(*second)
            if b == 2:
                quantize_x(3, 0)
                quantize_x(3, 1)
            else:
                quantize_entry(b + 1)
            if last:
                pool_store(*direct)
            else:
                both_passes(b + 2)
                interleave(b + 2, 1, 0, POOL, pool)
                store(*direct)
            aggregate(b, 2, 2)
            run = turned if b in RUNS else []
            for group in run:
                turn_out(*group)
            empty_g(b, 2, 2)
            if b not in WHOLE:
                quantize_g(b, 0, 4)
            aggregate(b, 4, 2)
            for group in run:
                store_t(*group)
            if last:
                project(*first)
                aggregate(b, 6, 1)
                project(*second)
                aggregate(b, 7, 1)
                empty_g(b, 4, 2)
                add_bias(*first)
                add_bias(*second)
            else:
                project_t(*second)
                project(*first)
                empty_g(b, 4, 1)
                sigmoid_t(*second)
                empty_g(b, 5, 1)
                interleave(b + 2, 0, 0, SHARE, scalar)
                add_bias(*first)
                multiply(*second)
                aggregate(b, 6, 2)
            empty_g(b, 6, 1)
            if last:
                sigmoid(*first)
            empty_g(b, 7, 1)
            turned = turned[len(run) :] + [second]
            direct = first
        b = BATCH - 1
        before = (b - 1, 4, 4)
        aggregate(b, 0, 2)
        project(b - 1, 0, 4)
        sigmoid(b - 2, 4, 4)
        store(b - 2, 0, 4)
        quantize_g(*before)
        empty_g(b, 0, 2)
        add_bias(b - 1, 0, 4)
        quantize_g(b, 0, 2)
        aggregate(b, 2, 2)
        project_t(*before)
        project(b, 0, 2)
        store(b - 2, 4, 4)
        empty_g(b, 2, 2)
        sigmoid_t(*before)
        sigmoid(b - 1, 0, 4)
        quantize_g(b, 2, 2)
        add_bias(b, 0, 2)
        aggregate(b, 4, 2)
        project(b, 2, 2)
        multiply(*before)
        store(b - 1, 0, 4)
        empty_g(b, 4, 2)
        sigmoid(b, 0, 2)
        add_bias(b, 2, 2)
        aggregate(b, 6, 2)
        quantize_g(b, 4, 2)
        store(b, 0, 2)
        turn_out(*before)
        project(b, 4, 2)
        empty_g(b, 6, 2)
        sigmoid(b, 2, 2)
        quantize_g(b, 6, 1)
        project(b, 6, 1)
        quantize_g(b, 7, 1)
        project(b, 7, 1)
        add_bias(b, 4, 2)
        store_t(*before)
        sigmoid(b, 4, 2)
        store(b, 2, 2)
        add_bias(b, 6, 1)
        add_bias(b, 7, 1)
        sigmoid(b, 6, 1)
        sigmoid(b, 7, 1)
        store(b, 4, 2)
        store(b, 6, 1)
        store(b, 7, 1)
